import numpy as np
import ml_dtypes


def mxq(x, axis, fmt="e4m3"):
    dtype, down = {"e4m3": (ml_dtypes.float8_e4m3fn, 7), "e5m2": (ml_dtypes.float8_e5m2, 14)}[fmt]
    v = np.moveaxis(np.asarray(x, np.float32).astype(ml_dtypes.bfloat16).astype(np.float64), axis, -1)
    blocks = v.reshape(v.shape[:-1] + (-1, 32))
    amax = np.abs(blocks).max(-1, keepdims=True)
    byte = np.maximum(np.where(amax > 0, np.frexp(amax)[1] - 1 + 127, 0) - down, 1)
    scale = np.exp2(byte - 127.0)
    codes = (blocks / scale).astype(np.float32).astype(dtype).astype(np.float64)
    return np.moveaxis((codes * scale).reshape(v.shape), -1, axis)


WIDE = False


def mx_kscale(k):
    if not WIDE:
        return np.ones(k)
    levels = np.array([10, -10, 5, -5, 0])
    a = np.random.permutation(np.resize(levels, k // 512 * 4)).reshape(k // 512, 4)
    idx = np.arange(k)
    return np.exp2(a[idx // 512, idx % 128 // 32])


BF16 = ml_dtypes.bfloat16


def bf(x):
    return np.asarray(x, np.float32).astype(BF16)


def f64(x):
    return np.asarray(x).astype(np.float64)


E2M1 = np.array([0.0, 0.5, 1.0, 1.5, 2.0, 3.0, 4.0, 6.0, -0.0, -0.5, -1.0, -1.5, -2.0, -3.0, -4.0, -6.0])


def pack_weight(w, fmt):
    k, n = w.shape
    w = f64(bf(w)).reshape(k // 32, 32, n)
    amax = np.abs(w).max(1)
    if fmt == "e4m3":
        byte = np.frexp(amax)[1] - 1 + 127 - 7
    else:
        mant, ex = np.frexp(amax / 6.0)
        byte = np.where(mant > 0.5, ex, ex - 1) + 127
    byte = np.clip(np.where(amax > 0, byte, 1), 1, 254)
    scaled = (w * np.exp2(127.0 - byte)[:, None, :]).reshape(k, n).astype(np.float32)
    by_word = np.ascontiguousarray(scaled.reshape(k // 512, 128, 4, n).transpose(0, 1, 3, 2))
    if fmt == "e4m3":
        words = by_word.astype(ml_dtypes.float8_e4m3fn).view(np.uint8)
    else:
        c = by_word.astype(ml_dtypes.float4_e2m1fn).view(np.uint8) & 0xF
        words = c[..., 0::2] | (c[..., 1::2] << 4)
    return np.ascontiguousarray(words), np.ascontiguousarray(byte.astype(np.uint8).reshape(k // 512, 16, n))


def unpack_weight(words, scales, fmt):
    g, p, n, _ = words.shape
    if fmt == "e4m3":
        vals = np.ascontiguousarray(words).view(ml_dtypes.float8_e4m3fn).astype(np.float64)
    else:
        nib = np.empty((g, p, n, 4), np.uint8)
        nib[..., 0::2] = words & 0xF
        nib[..., 1::2] = words >> 4
        vals = E2M1[nib]
    vals = vals * np.repeat(np.exp2(scales.astype(np.float64) - 127.0), 8, axis=1)[..., None]
    return vals.transpose(0, 1, 3, 2).reshape(g * 512, n)


B, IN, H, OUT, L, STEPS = 1024, 512, 1024, 128, 3, 3
LN_EPS = 1e-5
TAU_EPS = 1e-6
FMT = "e4m3"


def layer_norm(v, g, b):
    m = v.mean(-1, keepdims=True)
    var = ((v - m) ** 2).mean(-1, keepdims=True)
    return (v - m) / np.sqrt(var + LN_EPS) * g + b


def setup_inputs():
    r = mx_kscale(IN)
    s = mx_kscale(H)
    s = s / s.max()
    t = mx_kscale(H)
    liq_rms = np.sqrt(L * (L + 1) / 2.0)
    liq = bf(np.random.standard_normal((B, H)) * liq_rms * s)
    h = bf(np.random.standard_normal((B, H)))
    x = bf(np.random.standard_normal((B, IN)) * r)
    W_in_words, W_in_scales = pack_weight(np.ascontiguousarray((np.random.standard_normal((H, IN)) * 0.7 / np.sqrt(IN) / r).T), FMT)
    b_in = bf(np.random.standard_normal(H) * 0.3)
    W_v_words, W_v_scales = pack_weight(np.ascontiguousarray((np.random.standard_normal((H, H)) / np.sqrt(H) * t[:, None] / s).T), FMT)
    b_v = bf(np.random.standard_normal(H) * 0.5 * t)
    W_o_words, W_o_scales = pack_weight(np.ascontiguousarray((np.random.standard_normal((H, H)) / np.sqrt(H) / t).T), FMT)
    b_o = bf(np.random.standard_normal(H) * 0.5)
    g_att = bf(1.0 + 0.1 * np.random.standard_normal(H))
    beta_att = bf(np.random.standard_normal(H) * 0.3)
    tau = bf(0.5 + 0.5 * np.random.random(H))
    return {"liq": liq,
            "h": h,
            "x": x,
            "W_in_words": W_in_words,
            "W_in_scales": W_in_scales,
            "b_in": b_in,
            "W_v_words": W_v_words,
            "W_v_scales": W_v_scales,
            "b_v": b_v,
            "W_o_words": W_o_words,
            "W_o_scales": W_o_scales,
            "b_o": b_o,
            "g_att": g_att,
            "beta_att": beta_att,
            "tau": tau}


def reference(liq, h, x, W_in_words, W_in_scales, b_in, W_v_words, W_v_scales, b_v, W_o_words, W_o_scales, b_o, g_att, beta_att, tau):
    liq, h = f64(liq), f64(h)
    xin = (mxq(f64(x), 1, "e4m3") @ unpack_weight(W_in_words, W_in_scales, FMT)) + f64(b_in)
    v = (mxq(liq, 1, "e4m3") @ unpack_weight(W_v_words, W_v_scales, FMT)) + f64(b_v)
    att = (mxq(v, 1, "e4m3") @ unpack_weight(W_o_words, W_o_scales, FMT)) + f64(b_o)
    z = layer_norm(att + liq, f64(g_att), f64(beta_att))
    dh = (-h + np.tanh(z + xin)) / (f64(tau) + TAU_EPS)
    return h + dh

@@ -1,0 +1,384 @@
+from contextlib import ExitStack
+
+import concourse.mybir as mybir
+from concourse.masks import make_identity
+
+F32 = mybir.dt.float32
+BF16 = mybir.dt.bfloat16
+I32 = mybir.dt.int32
+U32 = mybir.dt.uint32
+U8 = mybir.dt.uint8
+FP8X4 = mybir.dt.float8_e4m3fn_x4
+ALU = mybir.AluOpType
+ACT = mybir.ActivationFunctionType
+
+P = 128
+PACK = 4
+K_PASS = P * PACK
+BANK = 512
+B, IN, H = 1024, 512, 1024
+TILES = B // P
+H_GROUPS = H // K_PASS
+H_BANKS = H // BANK
+H_BLOCKS = H // P
+LN_EPS = 1e-5
+TAU_EPS = 1e-6
+
+FLOPS = 2 * B * (IN * H + H * H + H * H)
+
+PLANE_IN, PLANE_V, PLANE_O = 0, 1, 3
+PLANES = 5
+WORK_BUFS = 4
+XIN_BLOCKS_A_STEP = 4
+ROW_TAU, ROW_BETA, ROW_B_IN, ROW_B_V, ROW_B_O, ROW_G = 0, 1, 2, 3, 4, 5
+
+
+def tile_advancedliquidneuralnetwork_pb_kernel(
+    tc,
+    liq,
+    h,
+    x,
+    W_in_words,
+    W_in_scales,
+    b_in,
+    W_v_words,
+    W_v_scales,
+    b_v,
+    W_o_words,
+    W_o_scales,
+    b_o,
+    g_att,
+    beta_att,
+    tau,
+    out,
+):
+    nc = tc.nc
+    with ExitStack() as ctx:
+        keep = ctx.enter_context(tc.tile_pool(name="keep", bufs=1))
+        ring = ctx.enter_context(tc.tile_pool(name="ring", bufs=3))
+        stat = ctx.enter_context(tc.tile_pool(name="stat", bufs=4))
+        psum = ctx.enter_context(tc.psum_pool(name="psum", bufs=2))
+        ctx.enter_context(tc.manual_schedule())
+
+        def bank(tag):
+            return psum.tile([P, BANK], F32, name=tag, tag=tag)
+
+        liq_sb = keep.tile([P, TILES, H], BF16)
+        x_sb = keep.tile([P, TILES, IN], BF16)
+        h_sb = keep.tile([P, TILES, H], BF16)
+        w_in_codes = keep.tile([P, 1, H], U32, align_bytes=64)
+        w_v_codes = keep.tile([P, H_GROUPS, H], U32, align_bytes=64)
+        w_o_codes = keep.tile([P, H_GROUPS, H], U32, align_bytes=64)
+        w_scales = keep.tile([P, PLANES, H], U8, align_bytes=64)
+        liq_codes = keep.tile([P, TILES, H_GROUPS * P], U32, align_bytes=64)
+        liq_scales = keep.tile([P, TILES, H_GROUPS * P], U8, align_bytes=64)
+        v_codes = keep.tile([P, TILES, H_GROUPS * P], U32, align_bytes=64)
+        v_scales = keep.tile([P, TILES, H_GROUPS * P], U8, align_bytes=64)
+        x_codes = keep.tile([P, B], U32, align_bytes=64)
+        x_scales = keep.tile([P, B], U8, align_bytes=64)
+        xin_turned = keep.tile([P, H_BLOCKS, B], F32)
+        vec_rows = keep.tile([P, P], BF16)
+        ident_bf = keep.tile([P, P], BF16)
+        ident_f32 = keep.tile([P, P], F32)
+        minus_half = keep.tile([P, 1], F32)
+
+        liq_rows = liq.rearrange("(p i) f -> p i f", i=TILES)
+        x_rows = x.rearrange("(p i) f -> p i f", i=TILES)
+        h_rows = h.rearrange("(p i) f -> p i f", i=TILES)
+        out_rows = out.rearrange("(p i) f -> p i f", i=TILES)
+
+        nc.vector.memset(w_scales[:].bitcast(I32), 0)
+        nc.vector.memset(vec_rows[:], 0.0)
+        nc.vector.memset(minus_half[:], -0.5)
+        make_identity(nc, ident_bf[:])
+        make_identity(nc, ident_f32[:])
+
+        for row, vec in (
+            (ROW_TAU, tau),
+            (ROW_BETA, beta_att),
+            (ROW_B_IN, b_in),
+            (ROW_B_V, b_v),
+            (ROW_B_O, b_o),
+            (ROW_G, g_att),
+        ):
+            nc.scalar.dma_start(
+                out=vec_rows[H_BLOCKS * row : H_BLOCKS * (row + 1), :],
+                in_=vec.rearrange("(m c) -> m c", c=P),
+            )
+
+        def load_tokens(dst, src, first, count):
+            nc.sync.dma_start(out=dst[:, first : first + count, :], in_=src[:, first : first + count, :])
+
+        def load_weight(words, scales, codes, plane):
+            groups = words.shape[0]
+            for quad in range(4):
+                nc.sync.dma_start(
+                    out=w_scales[32 * quad : 32 * quad + 4, plane : plane + groups, :].bitcast(I32),
+                    in_=scales[:, 4 * quad : 4 * quad + 4, :].bitcast(I32).rearrange("g r n -> r g n"),
+                )
+            for g in range(groups):
+                nc.sync.dma_start(
+                    out=codes[:, g, :].bitcast(I32),
+                    in_=words[g].rearrange("p n t -> p (n t)").bitcast(I32),
+                )
+
+        load_tokens(liq_sb, liq_rows, 0, 2)
+        load_weight(W_v_words, W_v_scales, w_v_codes, PLANE_V)
+        load_tokens(x_sb, x_rows, 0, 4)
+        load_weight(W_in_words, W_in_scales, w_in_codes, PLANE_IN)
+        load_weight(W_o_words, W_o_scales, w_o_codes, PLANE_O)
+        load_tokens(liq_sb, liq_rows, 2, 2)
+        load_tokens(x_sb, x_rows, 4, 4)
+        load_tokens(h_sb, h_rows, 0, 2)
+        load_tokens(liq_sb, liq_rows, 4, 4)
+        load_tokens(h_sb, h_rows, 2, 2)
+        load_tokens(h_sb, h_rows, 4, 4)
+
+        vec_ps = psum.tile([P, P], BF16, name="vec_ps", tag="tp")
+        nc.tensor.transpose(vec_ps[:], vec_rows[:], ident_bf[:])
+        vec_cols_bf = keep.tile([P, 6 * H_BLOCKS], BF16)
+        vec_cols = keep.tile([P, 3 * H_BLOCKS], F32)
+        nc.vector.tensor_copy(out=vec_cols_bf[:], in_=vec_ps[:, : 6 * H_BLOCKS])
+        nc.vector.tensor_copy(out=vec_cols[:], in_=vec_ps[:, : 3 * H_BLOCKS])
+
+        def block_cols(cols, row):
+            return cols[:, H_BLOCKS * row : H_BLOCKS * (row + 1)]
+
+        shift_cols = keep.tile([P, H_BLOCKS], F32)
+        rate_cols = keep.tile([P, H_BLOCKS], F32)
+        nc.vector.tensor_tensor(
+            out=shift_cols[:], in0=block_cols(vec_cols, ROW_BETA), in1=block_cols(vec_cols, ROW_B_IN), op=ALU.add
+        )
+        nc.vector.tensor_scalar_add(out=rate_cols[:], in0=block_cols(vec_cols, ROW_TAU), scalar1=TAU_EPS)
+        nc.vector.reciprocal(out=rate_cols[:], in_=rate_cols[:])
+
+        def columns(half):
+            return slice(half * BANK, (half + 1) * BANK)
+
+        def spread(cols, ident, half):
+            rows = bank("tp")
+            for q in range(BANK // P):
+                m = half * (BANK // P) + q
+                nc.tensor.matmul(
+                    out=rows[:, q * P : (q + 1) * P],
+                    lhsT=cols[:, m : m + 1].to_broadcast([P, P]),
+                    rhs=ident[:],
+                    start=True,
+                    stop=True,
+                )
+            return rows
+
+        def spread_input_vector(row, name):
+            everywhere = keep.tile([P, H], BF16, name=name)
+            for half in range(H_BANKS):
+                rows = spread(block_cols(vec_cols_bf, row), ident_bf, half)
+                nc.vector.tensor_copy(out=everywhere[:, columns(half)], in_=rows[:])
+            return everywhere
+
+        def turn(first, second, tag):
+            turned = psum.tile([P, 2, 2, P], F32, name="turned", tag="tp")
+            for a, rows in enumerate((first, second)):
+                words = rows.bitcast(F32)
+                for u in range(2):
+                    nc.tensor.transpose(turned[:, a, u, :], words[:, u : K_PASS // 2 : 2], ident_f32[:])
+            grouped = ring.tile([P, 2, P, PACK], BF16, name=tag, tag=tag, align_bytes=64)
+            nc.scalar.copy(out=grouped[:].bitcast(F32), in_=turned[:].rearrange("p a u r -> p a r u"))
+            return grouped
+
+        def quantise(grouped, codes, scales):
+            nc.vector.quantize_mx(
+                out=codes.bitcast(FP8X4), scales=scales, in_=grouped[:].rearrange("p a r t -> p (a r t)")
+            )
+
+        def turn_liq(i):
+            return turn(liq_sb[:, i, :K_PASS], liq_sb[:, i, K_PASS:], "grouped_liq")
+
+        def prepare_x(pair):
+            grouped = turn(x_sb[:, 2 * pair, :], x_sb[:, 2 * pair + 1, :], "grouped_x")
+            tokens = slice(2 * pair * P, (2 * pair + 2) * P)
+            quantise(grouped, x_codes[:, tokens], x_scales[:, tokens])
+
+        def xin_block(token_half, m):
+            tokens = columns(token_half)
+            features = slice(m * P, (m + 1) * P)
+            acc = bank("tp")
+            nc.tensor.matmul_mx(
+                out=acc[:],
+                lhsT=w_in_codes[:, 0, features].bitcast(FP8X4),
+                lhsT_scale=w_scales[:, PLANE_IN, features],
+                rhs=x_codes[:, tokens].bitcast(FP8X4),
+                rhs_scale=x_scales[:, tokens],
+                start=True,
+                stop=True,
+            )
+            nc.scalar.activation(
+                out=xin_turned[:, m, tokens], in_=acc[:], func=ACT.Identity, bias=shift_cols[:, m : m + 1], scale=1.0
+            )
+
+        def tokens_times_weight(tag, codes, scales, i, w_codes, plane):
+            banks = []
+            for half in range(H_BANKS):
+                acc = bank(tag)
+                for g in range(H_GROUPS):
+                    group = slice(g * P, (g + 1) * P)
+                    nc.tensor.matmul_mx(
+                        out=acc[:],
+                        lhsT=codes[:, i, group].bitcast(FP8X4),
+                        lhsT_scale=scales[:, i, group],
+                        rhs=w_codes[:, g, columns(half)].bitcast(FP8X4),
+                        rhs_scale=w_scales[:, plane + g, columns(half)],
+                        start=(g == 0),
+                        stop=(g == H_GROUPS - 1),
+                    )
+                banks.append(acc)
+            return banks
+
+        v_acc, att_acc, xin_acc = {}, {}, {}
+        grouped_liq, grouped_v = {}, {}
+        resid, work, h_share, sums, neg_mean, rstd = {}, {}, {}, {}, {}, {}
+
+        def start_residual(i):
+            resid[i] = ring.tile([P, H], F32, name="resid", tag="resid")
+            nc.gpsimd.tensor_tensor(out=resid[i][:], in0=liq_sb[:, i, :], in1=b_o_rows[:], op=ALU.add)
+
+        def share_of_h(i):
+            h_share[i] = ring.tile([P, H], F32, name="h_share", tag="h_share")
+            nc.gpsimd.tensor_tensor(out=h_share[i][:], in0=h_sb[:, i, :], in1=stay_rows[:], op=ALU.mult)
+
+        def round_v(i):
+            v_bf = ring.tile([P, H], BF16, name="v_bf", tag="v_bf")
+            for half in range(H_BANKS):
+                nc.vector.tensor_tensor(
+                    out=v_bf[:, columns(half)], in0=v_acc[i][half][:], in1=b_v_rows[:, columns(half)], op=ALU.add
+                )
+            grouped_v[i] = turn(v_bf[:, :K_PASS], v_bf[:, K_PASS:], "grouped_v")
+
+        def turn_xin_back(i):
+            xin_acc[i] = [bank("xin"), bank("xin")]
+            for m in range(H_BLOCKS):
+                q = m % (BANK // P)
+                nc.tensor.transpose(
+                    xin_acc[i][m // (BANK // P)][:, q * P : (q + 1) * P],
+                    xin_turned[:, m, i * P : (i + 1) * P],
+                    ident_f32[:],
+                )
+
+        def add_residual(i):
+            sums[i] = stat.tile([P, H_BANKS], F32, name="sums", tag="sums")
+            for half in range(H_BANKS):
+                nc.vector.scalar_tensor_tensor(
+                    out=resid[i][:, columns(half)],
+                    in0=att_acc[i][half][:],
+                    scalar=1.0,
+                    in1=resid[i][:, columns(half)],
+                    op0=ALU.mult,
+                    op1=ALU.add,
+                    accum_out=sums[i][:, half : half + 1],
+                )
+
+        def variance(i):
+            neg_mean[i] = stat.tile([P, 1], F32, name="neg_mean", tag="neg_mean")
+            nc.vector.tensor_scalar(
+                out=neg_mean[i][:],
+                in0=sums[i][:, 0:1],
+                scalar1=sums[i][:, 1:2],
+                scalar2=-1.0 / H,
+                op0=ALU.add,
+                op1=ALU.mult,
+            )
+            squares = ring.tile([P, H], BF16, name="squares", tag="squares")
+            sum_sq = stat.tile([P, 1], F32, name="sum_sq", tag="sum_sq")
+            nc.scalar.activation(
+                out=squares[:], in_=resid[i][:], func=ACT.Square, bias=neg_mean[i][:], scale=1.0, accum_out=sum_sq[:]
+            )
+            var_eps = stat.tile([P, 1], F32, name="var_eps", tag="var_eps")
+            nc.gpsimd.tensor_scalar(
+                out=var_eps[:], in0=sum_sq[:], scalar1=1.0 / H, scalar2=LN_EPS, op0=ALU.mult, op1=ALU.add
+            )
+            rstd[i] = stat.tile([P, 1], F32, name="rstd", tag="rstd")
+            nc.gpsimd.tensor_tensor(out=rstd[i][:], in0=var_eps[:], in1=minus_half[:], op=ALU.pow)
+
+        def centre_and_gain(i):
+            work[i] = ring.tile([P, H], F32, name="work", tag="work", bufs=WORK_BUFS)
+            nc.vector.scalar_tensor_tensor(
+                out=work[i][:], in0=resid[i][:], scalar=neg_mean[i][:], in1=g_rows[:], op0=ALU.add, op1=ALU.mult
+            )
+
+        def squash(i):
+            for half in range(H_BANKS):
+                nc.vector.scalar_tensor_tensor(
+                    out=work[i][:, columns(half)],
+                    in0=work[i][:, columns(half)],
+                    scalar=rstd[i][:],
+                    in1=xin_acc[i][half][:],
+                    op0=ALU.mult,
+                    op1=ALU.add,
+                )
+            nc.scalar.activation(out=work[i][:], in_=work[i][:], func=ACT.Tanh)
+
+        def times_rate(i):
+            nc.vector.tensor_tensor(out=work[i][:], in0=work[i][:], in1=rate_rows[:], op=ALU.mult)
+
+        def add_share_of_h(i):
+            nc.vector.tensor_tensor(out=work[i][:], in0=work[i][:], in1=h_share[i][:], op=ALU.add)
+            nc.sync.dma_start(out=out_rows[:, i, :], in_=work[i][:])
+
+        b_v_rows = spread_input_vector(ROW_B_V, "b_v_rows")
+        for i in range(2):
+            quantise(turn_liq(i), liq_codes[:, i, :], liq_scales[:, i, :])
+        v_acc[0] = tokens_times_weight("v", liq_codes, liq_scales, 0, w_v_codes, PLANE_V)
+        b_o_rows = spread_input_vector(ROW_B_O, "b_o_rows")
+        rate_rows = keep.tile([P, H], F32)
+        stay_rows = keep.tile([P, H], F32)
+
+        def live(tile_index):
+            return 0 <= tile_index < TILES
+
+        for step in range(TILES + 4):
+            i = step
+            if live(i - 1):
+                start_residual(i - 1)
+            if live(i - 2):
+                add_residual(i - 2)
+            if live(i):
+                round_v(i)
+            if live(i + 2):
+                grouped_liq[i + 2] = turn_liq(i + 2)
+            if live(i + 1):
+                v_acc[i + 1] = tokens_times_weight("v", liq_codes, liq_scales, i + 1, w_v_codes, PLANE_V)
+            if live(i - 2):
+                variance(i - 2)
+            if live(i - 3):
+                share_of_h(i - 3)
+            if live(i - 1):
+                quantise(grouped_v[i - 1], v_codes[:, i - 1, :], v_scales[:, i - 1, :])
+                att_acc[i - 1] = tokens_times_weight("att", v_codes, v_scales, i - 1, w_o_codes, PLANE_O)
+            if live(i - 2):
+                centre_and_gain(i - 2)
+            if live(i - 4):
+                times_rate(i - 4)
+            if live(i - 3):
+                squash(i - 3)
+            if live(i - 2):
+                turn_xin_back(i - 2)
+            if live(i - 4):
+                add_share_of_h(i - 4)
+            if live(i + 2):
+                quantise(grouped_liq[i + 2], liq_codes[:, i + 2, :], liq_scales[:, i + 2, :])
+
+            if step == 0:
+                g_rows = spread_input_vector(ROW_G, "g_rows")
+            if step == 1:
+                for half in range(H_BANKS):
+                    rows = spread(rate_cols, ident_f32, half)
+                    nc.vector.tensor_copy(out=rate_rows[:, columns(half)], in_=rows[:])
+                    nc.vector.tensor_scalar(
+                        out=stay_rows[:, columns(half)], in0=rows[:], scalar1=-1.0, scalar2=1.0, op0=ALU.mult, op1=ALU.add
+                    )
+            for token_half, first_step in ((0, 0), (1, 3)):
+                if step == first_step:
+                    prepare_x(2 * token_half)
+                    prepare_x(2 * token_half + 1)
+                if step in (first_step, first_step + 1):
+                    for q in range(XIN_BLOCKS_A_STEP):
+                        xin_block(token_half, (step - first_step) * XIN_BLOCKS_A_STEP + q)

@@ -239,11 +239,11 @@ def tile_advancedliquidneuralnetwork_pb_kernel(
 
         def start_residual(i):
             resid[i] = ring.tile([P, H], F32, name="resid", tag="resid")
-            nc.gpsimd.tensor_tensor(out=resid[i][:], in0=liq_sb[:, i, :], in1=b_o_rows[:], op=ALU.add)
+            nc.vector.tensor_tensor(out=resid[i][:], in0=liq_sb[:, i, :], in1=b_o_rows[:], op=ALU.add)
 
         def share_of_h(i):
             h_share[i] = ring.tile([P, H], F32, name="h_share", tag="h_share")
-            nc.gpsimd.tensor_tensor(out=h_share[i][:], in0=h_sb[:, i, :], in1=stay_rows[:], op=ALU.mult)
+            nc.vector.tensor_tensor(out=h_share[i][:], in0=h_sb[:, i, :], in1=stay_rows[:], op=ALU.mult)
 
         def round_v(i):
             v_bf = ring.tile([P, H], BF16, name="v_bf", tag="v_bf")

@@ -29,7 +29,8 @@ FLOPS = 2 * B * (IN * H + H * H + H * H)
 PLANE_IN, PLANE_V, PLANE_O = 0, 1, 3
 PLANES = 5
 WORK_BUFS = 4
-XIN_BLOCKS_A_STEP = 4
+LIQ_AHEAD = 3
+H_SHARE_BUFS = TILES
 ROW_TAU, ROW_BETA, ROW_B_IN, ROW_B_V, ROW_B_O, ROW_G = 0, 1, 2, 3, 4, 5
 
 
@@ -55,7 +56,7 @@ def tile_advancedliquidneuralnetwork_pb_kernel(
     nc = tc.nc
     with ExitStack() as ctx:
         keep = ctx.enter_context(tc.tile_pool(name="keep", bufs=1))
-        ring = ctx.enter_context(tc.tile_pool(name="ring", bufs=3))
+        ring = ctx.enter_context(tc.tile_pool(name="ring", bufs=2))
         stat = ctx.enter_context(tc.tile_pool(name="stat", bufs=4))
         psum = ctx.enter_context(tc.psum_pool(name="psum", bufs=2))
         ctx.enter_context(tc.manual_schedule())
@@ -72,11 +73,12 @@ def tile_advancedliquidneuralnetwork_pb_kernel(
         w_scales = keep.tile([P, PLANES, H], U8, align_bytes=64)
         liq_codes = keep.tile([P, TILES, H_GROUPS * P], U32, align_bytes=64)
         liq_scales = keep.tile([P, TILES, H_GROUPS * P], U8, align_bytes=64)
-        v_codes = keep.tile([P, TILES, H_GROUPS * P], U32, align_bytes=64)
-        v_scales = keep.tile([P, TILES, H_GROUPS * P], U8, align_bytes=64)
-        x_codes = keep.tile([P, B], U32, align_bytes=64)
-        x_scales = keep.tile([P, B], U8, align_bytes=64)
+        v_codes = keep.tile([P, H_GROUPS, B], U32, align_bytes=64)
+        v_scales = keep.tile([P, H_GROUPS, B], U8, align_bytes=64)
+        x_codes = keep.tile([P, 1, B], U32, align_bytes=64)
+        x_scales = keep.tile([P, 1, B], U8, align_bytes=64)
         xin_turned = keep.tile([P, H_BLOCKS, B], F32)
+        att_turned = keep.tile([P, H_BLOCKS, BANK], F32)
         vec_rows = keep.tile([P, P], BF16)
         ident_bf = keep.tile([P, P], BF16)
         ident_f32 = keep.tile([P, P], F32)
@@ -124,22 +126,23 @@ def tile_advancedliquidneuralnetwork_pb_kernel(
 
         load_tokens(liq_sb, liq_rows, 0, 2)
         load_weight(W_v_words, W_v_scales, w_v_codes, PLANE_V)
+        load_tokens(liq_sb, liq_rows, 2, 2)
+        load_tokens(h_sb, h_rows, 0, 2)
+        load_tokens(liq_sb, liq_rows, 4, 2)
+        load_tokens(h_sb, h_rows, 2, 2)
+        load_weight(W_o_words, W_o_scales, w_o_codes, PLANE_O)
         load_tokens(x_sb, x_rows, 0, 4)
         load_weight(W_in_words, W_in_scales, w_in_codes, PLANE_IN)
-        load_weight(W_o_words, W_o_scales, w_o_codes, PLANE_O)
-        load_tokens(liq_sb, liq_rows, 2, 2)
-        load_tokens(x_sb, x_rows, 4, 4)
-        load_tokens(h_sb, h_rows, 0, 2)
-        load_tokens(liq_sb, liq_rows, 4, 4)
-        load_tokens(h_sb, h_rows, 2, 2)
+        load_tokens(liq_sb, liq_rows, 6, 2)
         load_tokens(h_sb, h_rows, 4, 4)
+        load_tokens(x_sb, x_rows, 4, 4)
 
         vec_ps = psum.tile([P, P], BF16, name="vec_ps", tag="tp")
         nc.tensor.transpose(vec_ps[:], vec_rows[:], ident_bf[:])
         vec_cols_bf = keep.tile([P, 6 * H_BLOCKS], BF16)
-        vec_cols = keep.tile([P, 3 * H_BLOCKS], F32)
+        vec_cols = keep.tile([P, 6 * H_BLOCKS], F32)
         nc.vector.tensor_copy(out=vec_cols_bf[:], in_=vec_ps[:, : 6 * H_BLOCKS])
-        nc.vector.tensor_copy(out=vec_cols[:], in_=vec_ps[:, : 3 * H_BLOCKS])
+        nc.vector.tensor_copy(out=vec_cols[:], in_=vec_ps[:, : 6 * H_BLOCKS])
 
         def block_cols(cols, row):
             return cols[:, H_BLOCKS * row : H_BLOCKS * (row + 1)]
@@ -181,7 +184,7 @@ def tile_advancedliquidneuralnetwork_pb_kernel(
                 words = rows.bitcast(F32)
                 for u in range(2):
                     nc.tensor.transpose(turned[:, a, u, :], words[:, u : K_PASS // 2 : 2], ident_f32[:])
-            grouped = ring.tile([P, 2, P, PACK], BF16, name=tag, tag=tag, align_bytes=64)
+            grouped = ring.tile([P, 2, P, PACK], BF16, name=tag, tag=tag, bufs=3, align_bytes=64)
             nc.scalar.copy(out=grouped[:].bitcast(F32), in_=turned[:].rearrange("p a u r -> p a r u"))
             return grouped
 
@@ -193,40 +196,65 @@ def tile_advancedliquidneuralnetwork_pb_kernel(
         def turn_liq(i):
             return turn(liq_sb[:, i, :K_PASS], liq_sb[:, i, K_PASS:], "grouped_liq")
 
-        def prepare_x(pair):
-            grouped = turn(x_sb[:, 2 * pair, :], x_sb[:, 2 * pair + 1, :], "grouped_x")
-            tokens = slice(2 * pair * P, (2 * pair + 2) * P)
-            quantise(grouped, x_codes[:, tokens], x_scales[:, tokens])
+        grouped_x = {}
 
-        def xin_block(token_half, m):
+        def pair_tokens(pair):
+            return slice(2 * pair * P, (2 * pair + 2) * P)
+
+        def turn_x(pair):
+            grouped_x[pair] = turn(x_sb[:, 2 * pair, :], x_sb[:, 2 * pair + 1, :], "grouped_x")
+
+        def quantise_x(pair):
+            quantise(grouped_x[pair], x_codes[:, 0, pair_tokens(pair)], x_scales[:, 0, pair_tokens(pair)])
+
+        def turned_block(dst, w_codes, plane, codes, scales, bias_cols, token_half, m):
             tokens = columns(token_half)
             features = slice(m * P, (m + 1) * P)
+            groups = codes.shape[1]
             acc = bank("tp")
-            nc.tensor.matmul_mx(
-                out=acc[:],
-                lhsT=w_in_codes[:, 0, features].bitcast(FP8X4),
-                lhsT_scale=w_scales[:, PLANE_IN, features],
-                rhs=x_codes[:, tokens].bitcast(FP8X4),
-                rhs_scale=x_scales[:, tokens],
-                start=True,
-                stop=True,
-            )
+            for g in range(groups):
+                nc.tensor.matmul_mx(
+                    out=acc[:],
+                    lhsT=w_codes[:, g, features].bitcast(FP8X4),
+                    lhsT_scale=w_scales[:, plane + g, features],
+                    rhs=codes[:, g, tokens].bitcast(FP8X4),
+                    rhs_scale=scales[:, g, tokens],
+                    start=(g == 0),
+                    stop=(g == groups - 1),
+                )
             nc.scalar.activation(
-                out=xin_turned[:, m, tokens], in_=acc[:], func=ACT.Identity, bias=shift_cols[:, m : m + 1], scale=1.0
+                out=dst, in_=acc[:], func=ACT.Identity, bias=bias_cols[:, m : m + 1], scale=1.0
             )
 
-        def tokens_times_weight(tag, codes, scales, i, w_codes, plane):
+        def xin_block(token_half, m):
+            dst = xin_turned[:, m, columns(token_half)]
+            turned_block(dst, w_in_codes, PLANE_IN, x_codes, x_scales, shift_cols, token_half, m)
+
+        def att_block(token_half, m):
+            b_o_cols = block_cols(vec_cols, ROW_B_O)
+            turned_block(att_turned[:, m, :], w_o_codes, PLANE_O, v_codes, v_scales, b_o_cols, token_half, m)
+
+        def turn_back(turned, tag, i):
+            banks = [bank(tag), bank(tag)]
+            for m in range(H_BLOCKS):
+                q = m % (BANK // P)
+                nc.tensor.transpose(
+                    banks[m // (BANK // P)][:, q * P : (q + 1) * P], turned[:, m, i * P : (i + 1) * P], ident_f32[:]
+                )
+            return banks
+
+        def liq_times_w_v(i):
             banks = []
             for half in range(H_BANKS):
-                acc = bank(tag)
+                acc = bank("v")
                 for g in range(H_GROUPS):
                     group = slice(g * P, (g + 1) * P)
                     nc.tensor.matmul_mx(
                         out=acc[:],
-                        lhsT=codes[:, i, group].bitcast(FP8X4),
-                        lhsT_scale=scales[:, i, group],
-                        rhs=w_codes[:, g, columns(half)].bitcast(FP8X4),
-                        rhs_scale=w_scales[:, plane + g, columns(half)],
+                        lhsT=liq_codes[:, i, group].bitcast(FP8X4),
+                        lhsT_scale=liq_scales[:, i, group],
+                        rhs=w_v_codes[:, g, columns(half)].bitcast(FP8X4),
+                        rhs_scale=w_scales[:, PLANE_V + g, columns(half)],
                         start=(g == 0),
                         stop=(g == H_GROUPS - 1),
                     )
@@ -234,43 +262,38 @@ def tile_advancedliquidneuralnetwork_pb_kernel(
             return banks
 
         v_acc, att_acc, xin_acc = {}, {}, {}
-        grouped_liq, grouped_v = {}, {}
+        v_bf, grouped_liq, grouped_v = {}, {}, {}
         resid, work, h_share, sums, neg_mean, rstd = {}, {}, {}, {}, {}, {}
 
-        def start_residual(i):
-            resid[i] = ring.tile([P, H], F32, name="resid", tag="resid")
-            nc.vector.tensor_tensor(out=resid[i][:], in0=liq_sb[:, i, :], in1=b_o_rows[:], op=ALU.add)
-
         def share_of_h(i):
-            h_share[i] = ring.tile([P, H], F32, name="h_share", tag="h_share")
+            h_share[i] = ring.tile([P, H], F32, name="h_share", tag="h_share", bufs=H_SHARE_BUFS)
             nc.vector.tensor_tensor(out=h_share[i][:], in0=h_sb[:, i, :], in1=stay_rows[:], op=ALU.mult)
 
         def round_v(i):
-            v_bf = ring.tile([P, H], BF16, name="v_bf", tag="v_bf")
+            v_bf[i] = ring.tile([P, H], BF16, name="v_bf", tag="v_bf", bufs=3)
             for half in range(H_BANKS):
                 nc.vector.tensor_tensor(
-                    out=v_bf[:, columns(half)], in0=v_acc[i][half][:], in1=b_v_rows[:, columns(half)], op=ALU.add
+                    out=v_bf[i][:, columns(half)], in0=v_acc[i][half][:], in1=b_v_rows[:, columns(half)], op=ALU.add
                 )
-            grouped_v[i] = turn(v_bf[:, :K_PASS], v_bf[:, K_PASS:], "grouped_v")
 
-        def turn_xin_back(i):
-            xin_acc[i] = [bank("xin"), bank("xin")]
-            for m in range(H_BLOCKS):
-                q = m % (BANK // P)
-                nc.tensor.transpose(
-                    xin_acc[i][m // (BANK // P)][:, q * P : (q + 1) * P],
-                    xin_turned[:, m, i * P : (i + 1) * P],
-                    ident_f32[:],
-                )
+        def turn_v(pair):
+            for g in range(H_GROUPS):
+                features = slice(g * K_PASS, (g + 1) * K_PASS)
+                grouped_v[pair, g] = turn(v_bf[2 * pair][:, features], v_bf[2 * pair + 1][:, features], "grouped_v")
+
+        def quantise_v(pair):
+            for g in range(H_GROUPS):
+                quantise(grouped_v[pair, g], v_codes[:, g, pair_tokens(pair)], v_scales[:, g, pair_tokens(pair)])
 
         def add_residual(i):
+            resid[i] = ring.tile([P, H], F32, name="resid", tag="resid")
             sums[i] = stat.tile([P, H_BANKS], F32, name="sums", tag="sums")
             for half in range(H_BANKS):
                 nc.vector.scalar_tensor_tensor(
                     out=resid[i][:, columns(half)],
                     in0=att_acc[i][half][:],
                     scalar=1.0,
-                    in1=resid[i][:, columns(half)],
+                    in1=liq_sb[:, i, columns(half)],
                     op0=ALU.mult,
                     op1=ALU.add,
                     accum_out=sums[i][:, half : half + 1],
@@ -324,61 +347,69 @@ def tile_advancedliquidneuralnetwork_pb_kernel(
             nc.sync.dma_start(out=out_rows[:, i, :], in_=work[i][:])
 
         b_v_rows = spread_input_vector(ROW_B_V, "b_v_rows")
-        for i in range(2):
-            quantise(turn_liq(i), liq_codes[:, i, :], liq_scales[:, i, :])
-        v_acc[0] = tokens_times_weight("v", liq_codes, liq_scales, 0, w_v_codes, PLANE_V)
-        b_o_rows = spread_input_vector(ROW_B_O, "b_o_rows")
         rate_rows = keep.tile([P, H], F32)
         stay_rows = keep.tile([P, H], F32)
+        for half in range(H_BANKS):
+            rows = spread(rate_cols, ident_f32, half)
+            nc.vector.tensor_copy(out=rate_rows[:, columns(half)], in_=rows[:])
+            nc.vector.tensor_scalar(
+                out=stay_rows[:, columns(half)], in0=rows[:], scalar1=-1.0, scalar2=1.0, op0=ALU.mult, op1=ALU.add
+            )
+        for i in range(LIQ_AHEAD):
+            grouped_liq[i] = turn_liq(i)
+        for i in range(LIQ_AHEAD - 1):
+            quantise(grouped_liq[i], liq_codes[:, i, :], liq_scales[:, i, :])
+        v_acc[0] = liq_times_w_v(0)
+        g_rows = spread_input_vector(ROW_G, "g_rows")
 
         def live(tile_index):
             return 0 <= tile_index < TILES
 
-        for step in range(TILES + 4):
-            i = step
-            if live(i - 1):
-                start_residual(i - 1)
-            if live(i - 2):
-                add_residual(i - 2)
-            if live(i):
-                round_v(i)
-            if live(i + 2):
-                grouped_liq[i + 2] = turn_liq(i + 2)
-            if live(i + 1):
-                v_acc[i + 1] = tokens_times_weight("v", liq_codes, liq_scales, i + 1, w_v_codes, PLANE_V)
-            if live(i - 2):
-                variance(i - 2)
-            if live(i - 3):
-                share_of_h(i - 3)
-            if live(i - 1):
-                quantise(grouped_v[i - 1], v_codes[:, i - 1, :], v_scales[:, i - 1, :])
-                att_acc[i - 1] = tokens_times_weight("att", v_codes, v_scales, i - 1, w_o_codes, PLANE_O)
-            if live(i - 2):
-                centre_and_gain(i - 2)
-            if live(i - 4):
-                times_rate(i - 4)
-            if live(i - 3):
-                squash(i - 3)
-            if live(i - 2):
-                turn_xin_back(i - 2)
-            if live(i - 4):
-                add_share_of_h(i - 4)
-            if live(i + 2):
-                quantise(grouped_liq[i + 2], liq_codes[:, i + 2, :], liq_scales[:, i + 2, :])
-
-            if step == 0:
-                g_rows = spread_input_vector(ROW_G, "g_rows")
-            if step == 1:
-                for half in range(H_BANKS):
-                    rows = spread(rate_cols, ident_f32, half)
-                    nc.vector.tensor_copy(out=rate_rows[:, columns(half)], in_=rows[:])
-                    nc.vector.tensor_scalar(
-                        out=stay_rows[:, columns(half)], in0=rows[:], scalar1=-1.0, scalar2=1.0, op0=ALU.mult, op1=ALU.add
-                    )
-            for token_half, first_step in ((0, 0), (1, 3)):
-                if step == first_step:
-                    prepare_x(2 * token_half)
-                    prepare_x(2 * token_half + 1)
-                if step in (first_step, first_step + 1):
-                    for q in range(XIN_BLOCKS_A_STEP):
-                        xin_block(token_half, (step - first_step) * XIN_BLOCKS_A_STEP + q)
+        for s in range(TILES + 8):
+            if live(s - 6):
+                xin_acc[s - 6] = turn_back(xin_turned, "xin", s - 6)
+            if live(s - 5):
+                add_residual(s - 5)
+            if live(s):
+                round_v(s)
+                if s % 2 == 1:
+                    turn_v(s // 2)
+            if live(s + 1):
+                v_acc[s + 1] = liq_times_w_v(s + 1)
+            if live(s + LIQ_AHEAD):
+                grouped_liq[s + LIQ_AHEAD] = turn_liq(s + LIQ_AHEAD)
+            if live(s - 5):
+                variance(s - 5)
+            if live(s - 1) and s % 2 == 0:
+                quantise_v(s // 2 - 1)
+                if s % 4 == 0:
+                    for m in range(H_BLOCKS):
+                        att_block(s // 4 - 1, m)
+            if live(s - 4):
+                att_acc[s - 4] = turn_back(att_turned, "att", (s - 4) % 4)
+            if live(s - 5):
+                centre_and_gain(s - 5)
+            if live(s - 7):
+                times_rate(s - 7)
+            if live(s - 6):
+                squash(s - 6)
+            if live(s - 7):
+                add_share_of_h(s - 7)
+            if live(s + LIQ_AHEAD - 1):
+                t = s + LIQ_AHEAD - 1
+                quantise(grouped_liq[t], liq_codes[:, t, :], liq_scales[:, t, :])
+            if s < 4:
+                share_of_h(s)
+            if s == 4:
+                for i in range(4, TILES):
+                    share_of_h(i)
+            for token_half in range(2):
+                first_step = 4 * token_half + 2
+                for pair in (2 * token_half, 2 * token_half + 1):
+                    if s == first_step:
+                        turn_x(pair)
+                    if s == first_step + 1:
+                        quantise_x(pair)
+                if s in (first_step + 2, first_step + 3):
+                    for q in range(H_BLOCKS // 2):
+                        xin_block(token_half, (s - first_step - 2) * (H_BLOCKS // 2) + q)

@@ -59,7 +59,6 @@ def tile_advancedliquidneuralnetwork_pb_kernel(
         ring = ctx.enter_context(tc.tile_pool(name="ring", bufs=2))
         stat = ctx.enter_context(tc.tile_pool(name="stat", bufs=4))
         psum = ctx.enter_context(tc.psum_pool(name="psum", bufs=2))
-        ctx.enter_context(tc.manual_schedule())
 
         def bank(tag):
             return psum.tile([P, BANK], F32, name=tag, tag=tag)

@@ -174,7 +174,7 @@ def tile_advancedliquidneuralnetwork_pb_kernel(
             everywhere = keep.tile([P, H], BF16, name=name)
             for half in range(H_BANKS):
                 rows = spread(block_cols(vec_cols_bf, row), ident_bf, half)
-                nc.vector.tensor_copy(out=everywhere[:, columns(half)], in_=rows[:])
+                nc.scalar.copy(out=everywhere[:, columns(half)], in_=rows[:])
             return everywhere
 
         def turn(first, second, tag):
@@ -348,18 +348,11 @@ def tile_advancedliquidneuralnetwork_pb_kernel(
         b_v_rows = spread_input_vector(ROW_B_V, "b_v_rows")
         rate_rows = keep.tile([P, H], F32)
         stay_rows = keep.tile([P, H], F32)
-        for half in range(H_BANKS):
-            rows = spread(rate_cols, ident_f32, half)
-            nc.vector.tensor_copy(out=rate_rows[:, columns(half)], in_=rows[:])
-            nc.vector.tensor_scalar(
-                out=stay_rows[:, columns(half)], in0=rows[:], scalar1=-1.0, scalar2=1.0, op0=ALU.mult, op1=ALU.add
-            )
         for i in range(LIQ_AHEAD):
             grouped_liq[i] = turn_liq(i)
         for i in range(LIQ_AHEAD - 1):
             quantise(grouped_liq[i], liq_codes[:, i, :], liq_scales[:, i, :])
         v_acc[0] = liq_times_w_v(0)
-        g_rows = spread_input_vector(ROW_G, "g_rows")
 
         def live(tile_index):
             return 0 <= tile_index < TILES
@@ -397,10 +390,17 @@ def tile_advancedliquidneuralnetwork_pb_kernel(
             if live(s + LIQ_AHEAD - 1):
                 t = s + LIQ_AHEAD - 1
                 quantise(grouped_liq[t], liq_codes[:, t, :], liq_scales[:, t, :])
-            if s < 4:
-                share_of_h(s)
+            if s == 0:
+                for half in range(H_BANKS):
+                    rows = spread(rate_cols, ident_f32, half)
+                    nc.scalar.copy(out=rate_rows[:, columns(half)], in_=rows[:])
+                    nc.scalar.activation(out=stay_rows[:, columns(half)], in_=rows[:], func=ACT.Copy, bias=1.0, scale=-1.0)
+            if s == 1:
+                g_rows = spread_input_vector(ROW_G, "g_rows")
+            if 1 <= s < 4:
+                share_of_h(s - 1)
             if s == 4:
-                for i in range(4, TILES):
+                for i in range(3, TILES):
                     share_of_h(i)
             for token_half in range(2):
                 first_step = 4 * token_half + 2

@@ -88,8 +88,10 @@ def tile_advancedliquidneuralnetwork_pb_kernel(
         h_rows = h.rearrange("(p i) f -> p i f", i=TILES)
         out_rows = out.rearrange("(p i) f -> p i f", i=TILES)
 
-        nc.vector.memset(w_scales[:].bitcast(I32), 0)
         nc.vector.memset(vec_rows[:], 0.0)
+        nc.vector.memset(w_scales[:, PLANE_V : PLANE_V + H_GROUPS, :].bitcast(I32), 0)
+        nc.vector.memset(w_scales[:, PLANE_O : PLANE_O + H_GROUPS, :].bitcast(I32), 0)
+        nc.vector.memset(w_scales[:, PLANE_IN : PLANE_IN + 1, :].bitcast(I32), 0)
         nc.vector.memset(minus_half[:], -0.5)
         make_identity(nc, ident_bf[:])
         make_identity(nc, ident_f32[:])
@@ -123,15 +125,16 @@ def tile_advancedliquidneuralnetwork_pb_kernel(
                     in_=words[g].rearrange("p n t -> p (n t)").bitcast(I32),
                 )
 
-        load_tokens(liq_sb, liq_rows, 0, 2)
+        load_tokens(liq_sb, liq_rows, 0, 1)
+        load_tokens(liq_sb, liq_rows, 1, 1)
         load_weight(W_v_words, W_v_scales, w_v_codes, PLANE_V)
         load_tokens(liq_sb, liq_rows, 2, 2)
         load_tokens(h_sb, h_rows, 0, 2)
-        load_tokens(liq_sb, liq_rows, 4, 2)
-        load_tokens(h_sb, h_rows, 2, 2)
         load_weight(W_o_words, W_o_scales, w_o_codes, PLANE_O)
         load_tokens(x_sb, x_rows, 0, 4)
         load_weight(W_in_words, W_in_scales, w_in_codes, PLANE_IN)
+        load_tokens(liq_sb, liq_rows, 4, 2)
+        load_tokens(h_sb, h_rows, 2, 2)
         load_tokens(liq_sb, liq_rows, 6, 2)
         load_tokens(h_sb, h_rows, 4, 4)
         load_tokens(x_sb, x_rows, 4, 4)
@@ -345,10 +348,11 @@ def tile_advancedliquidneuralnetwork_pb_kernel(
             nc.vector.tensor_tensor(out=work[i][:], in0=work[i][:], in1=h_share[i][:], op=ALU.add)
             nc.sync.dma_start(out=out_rows[:, i, :], in_=work[i][:])
 
-        b_v_rows = spread_input_vector(ROW_B_V, "b_v_rows")
         rate_rows = keep.tile([P, H], F32)
         stay_rows = keep.tile([P, H], F32)
-        for i in range(LIQ_AHEAD):
+        grouped_liq[0] = turn_liq(0)
+        b_v_rows = spread_input_vector(ROW_B_V, "b_v_rows")
+        for i in range(1, LIQ_AHEAD):
             grouped_liq[i] = turn_liq(i)
         for i in range(LIQ_AHEAD - 1):
             quantise(grouped_liq[i], liq_codes[:, i, :], liq_scales[:, i, :])

@@ -77,7 +77,6 @@ def tile_advancedliquidneuralnetwork_pb_kernel(
         x_codes = keep.tile([P, 1, B], U32, align_bytes=64)
         x_scales = keep.tile([P, 1, B], U8, align_bytes=64)
         xin_turned = keep.tile([P, H_BLOCKS, B], F32)
-        att_turned = keep.tile([P, H_BLOCKS, BANK], F32)
         vec_rows = keep.tile([P, P], BF16)
         ident_bf = keep.tile([P, P], BF16)
         ident_f32 = keep.tile([P, P], F32)
@@ -129,33 +128,18 @@ def tile_advancedliquidneuralnetwork_pb_kernel(
         load_tokens(liq_sb, liq_rows, 1, 1)
         load_weight(W_v_words, W_v_scales, w_v_codes, PLANE_V)
         load_tokens(liq_sb, liq_rows, 2, 2)
-        load_tokens(h_sb, h_rows, 0, 2)
         load_weight(W_o_words, W_o_scales, w_o_codes, PLANE_O)
         load_tokens(x_sb, x_rows, 0, 4)
         load_weight(W_in_words, W_in_scales, w_in_codes, PLANE_IN)
+        load_tokens(h_sb, h_rows, 0, 2)
         load_tokens(liq_sb, liq_rows, 4, 2)
         load_tokens(h_sb, h_rows, 2, 2)
         load_tokens(liq_sb, liq_rows, 6, 2)
         load_tokens(h_sb, h_rows, 4, 4)
         load_tokens(x_sb, x_rows, 4, 4)
 
-        vec_ps = psum.tile([P, P], BF16, name="vec_ps", tag="tp")
-        nc.tensor.transpose(vec_ps[:], vec_rows[:], ident_bf[:])
-        vec_cols_bf = keep.tile([P, 6 * H_BLOCKS], BF16)
-        vec_cols = keep.tile([P, 6 * H_BLOCKS], F32)
-        nc.vector.tensor_copy(out=vec_cols_bf[:], in_=vec_ps[:, : 6 * H_BLOCKS])
-        nc.vector.tensor_copy(out=vec_cols[:], in_=vec_ps[:, : 6 * H_BLOCKS])
-
         def block_cols(cols, row):
             return cols[:, H_BLOCKS * row : H_BLOCKS * (row + 1)]
-
-        shift_cols = keep.tile([P, H_BLOCKS], F32)
-        rate_cols = keep.tile([P, H_BLOCKS], F32)
-        nc.vector.tensor_tensor(
-            out=shift_cols[:], in0=block_cols(vec_cols, ROW_BETA), in1=block_cols(vec_cols, ROW_B_IN), op=ALU.add
-        )
-        nc.vector.tensor_scalar_add(out=rate_cols[:], in0=block_cols(vec_cols, ROW_TAU), scalar1=TAU_EPS)
-        nc.vector.reciprocal(out=rate_cols[:], in_=rate_cols[:])
 
         def columns(half):
             return slice(half * BANK, (half + 1) * BANK)
@@ -198,6 +182,25 @@ def tile_advancedliquidneuralnetwork_pb_kernel(
         def turn_liq(i):
             return turn(liq_sb[:, i, :K_PASS], liq_sb[:, i, K_PASS:], "grouped_liq")
 
+        grouped_liq = {}
+        grouped_liq[0] = turn_liq(0)
+        grouped_liq[1] = turn_liq(1)
+
+        vec_ps = psum.tile([P, P], BF16, name="vec_ps", tag="tp")
+        nc.tensor.transpose(vec_ps[:], vec_rows[:], ident_bf[:])
+        vec_cols_bf = keep.tile([P, 6 * H_BLOCKS], BF16)
+        vec_cols = keep.tile([P, 6 * H_BLOCKS], F32)
+        nc.vector.tensor_copy(out=vec_cols_bf[:], in_=vec_ps[:, : 6 * H_BLOCKS])
+        nc.vector.tensor_copy(out=vec_cols[:], in_=vec_ps[:, : 6 * H_BLOCKS])
+
+        shift_cols = keep.tile([P, H_BLOCKS], F32)
+        rate_cols = keep.tile([P, H_BLOCKS], F32)
+        nc.vector.tensor_tensor(
+            out=shift_cols[:], in0=block_cols(vec_cols, ROW_BETA), in1=block_cols(vec_cols, ROW_B_IN), op=ALU.add
+        )
+        nc.vector.tensor_scalar_add(out=rate_cols[:], in0=block_cols(vec_cols, ROW_TAU), scalar1=TAU_EPS)
+        nc.vector.reciprocal(out=rate_cols[:], in_=rate_cols[:])
+
         grouped_x = {}
 
         def pair_tokens(pair):
@@ -232,9 +235,32 @@ def tile_advancedliquidneuralnetwork_pb_kernel(
             dst = xin_turned[:, m, columns(token_half)]
             turned_block(dst, w_in_codes, PLANE_IN, x_codes, x_scales, shift_cols, token_half, m)
 
-        def att_block(token_half, m):
+        def att_of_pair(pair):
             b_o_cols = block_cols(vec_cols, ROW_B_O)
-            turned_block(att_turned[:, m, :], w_o_codes, PLANE_O, v_codes, v_scales, b_o_cols, token_half, m)
+            att_turned[pair] = ring.tile([P, H_BLOCKS, 2 * P], F32, name="att_turned", tag="att_turned")
+            for mm in range(H_BLOCKS // 2):
+                acc = bank("tp")
+                for a in range(2):
+                    features = slice((2 * mm + a) * P, (2 * mm + a + 1) * P)
+                    for g in range(H_GROUPS):
+                        nc.tensor.matmul_mx(
+                            out=acc[:, 2 * a * P : (2 * a + 2) * P],
+                            lhsT=w_o_codes[:, g, features].bitcast(FP8X4),
+                            lhsT_scale=w_scales[:, PLANE_O + g, features],
+                            rhs=v_codes[:, g, pair_tokens(pair)].bitcast(FP8X4),
+                            rhs_scale=v_scales[:, g, pair_tokens(pair)],
+                            start=(g == 0),
+                            stop=(g == H_GROUPS - 1),
+                        )
+                for a in range(2):
+                    m = 2 * mm + a
+                    nc.scalar.activation(
+                        out=att_turned[pair][:, m, :],
+                        in_=acc[:, 2 * a * P : (2 * a + 2) * P],
+                        func=ACT.Identity,
+                        bias=b_o_cols[:, m : m + 1],
+                        scale=1.0,
+                    )
 
         def turn_back(turned, tag, i):
             banks = [bank(tag), bank(tag)]
@@ -263,8 +289,8 @@ def tile_advancedliquidneuralnetwork_pb_kernel(
                 banks.append(acc)
             return banks
 
-        v_acc, att_acc, xin_acc = {}, {}, {}
-        v_bf, grouped_liq, grouped_v = {}, {}, {}
+        v_acc, att_acc, xin_acc, att_turned = {}, {}, {}, {}
+        v_bf, grouped_v = {}, {}
         resid, work, h_share, sums, neg_mean, rstd = {}, {}, {}, {}, {}, {}
 
         def share_of_h(i):
@@ -350,9 +376,8 @@ def tile_advancedliquidneuralnetwork_pb_kernel(
 
         rate_rows = keep.tile([P, H], F32)
         stay_rows = keep.tile([P, H], F32)
-        grouped_liq[0] = turn_liq(0)
         b_v_rows = spread_input_vector(ROW_B_V, "b_v_rows")
-        for i in range(1, LIQ_AHEAD):
+        for i in range(2, LIQ_AHEAD):
             grouped_liq[i] = turn_liq(i)
         for i in range(LIQ_AHEAD - 1):
             quantise(grouped_liq[i], liq_codes[:, i, :], liq_scales[:, i, :])
@@ -361,11 +386,12 @@ def tile_advancedliquidneuralnetwork_pb_kernel(
         def live(tile_index):
             return 0 <= tile_index < TILES
 
-        for s in range(TILES + 8):
-            if live(s - 6):
-                xin_acc[s - 6] = turn_back(xin_turned, "xin", s - 6)
-            if live(s - 5):
-                add_residual(s - 5)
+        ATT_LAG = 2
+        for s in range(TILES + ATT_LAG + 4):
+            if live(s - ATT_LAG - 2):
+                xin_acc[s - ATT_LAG - 2] = turn_back(xin_turned, "xin", s - ATT_LAG - 2)
+            if live(s - ATT_LAG - 1):
+                add_residual(s - ATT_LAG - 1)
             if live(s):
                 round_v(s)
                 if s % 2 == 1:
@@ -374,23 +400,21 @@ def tile_advancedliquidneuralnetwork_pb_kernel(
                 v_acc[s + 1] = liq_times_w_v(s + 1)
             if live(s + LIQ_AHEAD):
                 grouped_liq[s + LIQ_AHEAD] = turn_liq(s + LIQ_AHEAD)
-            if live(s - 5):
-                variance(s - 5)
+            if live(s - ATT_LAG - 1):
+                variance(s - ATT_LAG - 1)
             if live(s - 1) and s % 2 == 0:
                 quantise_v(s // 2 - 1)
-                if s % 4 == 0:
-                    for m in range(H_BLOCKS):
-                        att_block(s // 4 - 1, m)
-            if live(s - 4):
-                att_acc[s - 4] = turn_back(att_turned, "att", (s - 4) % 4)
-            if live(s - 5):
-                centre_and_gain(s - 5)
-            if live(s - 7):
-                times_rate(s - 7)
-            if live(s - 6):
-                squash(s - 6)
-            if live(s - 7):
-                add_share_of_h(s - 7)
+                att_of_pair(s // 2 - 1)
+            if live(s - ATT_LAG):
+                att_acc[s - ATT_LAG] = turn_back(att_turned[(s - ATT_LAG) // 2], "att", (s - ATT_LAG) % 2)
+            if live(s - ATT_LAG - 1):
+                centre_and_gain(s - ATT_LAG - 1)
+            if live(s - ATT_LAG - 3):
+                times_rate(s - ATT_LAG - 3)
+            if live(s - ATT_LAG - 2):
+                squash(s - ATT_LAG - 2)
+            if live(s - ATT_LAG - 3):
+                add_share_of_h(s - ATT_LAG - 3)
             if live(s + LIQ_AHEAD - 1):
                 t = s + LIQ_AHEAD - 1
                 quantise(grouped_liq[t], liq_codes[:, t, :], liq_scales[:, t, :])
@@ -407,12 +431,12 @@ def tile_advancedliquidneuralnetwork_pb_kernel(
                 for i in range(3, TILES):
                     share_of_h(i)
             for token_half in range(2):
-                first_step = 4 * token_half + 2
+                first_step = 4 * token_half + 1
                 for pair in (2 * token_half, 2 * token_half + 1):
                     if s == first_step:
                         turn_x(pair)
                     if s == first_step + 1:
                         quantise_x(pair)
-                if s in (first_step + 2, first_step + 3):
+                if s in (first_step + 1, first_step + 2):
                     for q in range(H_BLOCKS // 2):
-                        xin_block(token_half, (s - first_step - 2) * (H_BLOCKS // 2) + q)
+                        xin_block(token_half, (s - first_step - 1) * (H_BLOCKS // 2) + q)

@@ -148,6 +148,9 @@ def tile_advancedliquidneuralnetwork_pb_kernel(
             rows = bank("tp")
             for q in range(BANK // P):
                 m = half * (BANK // P) + q
+                if ident is ident_f32:
+                    nc.tensor.transpose(rows[:, q * P : (q + 1) * P], cols[:, m : m + 1].to_broadcast([P, P]), ident[:])
+                    continue
                 nc.tensor.matmul(
                     out=rows[:, q * P : (q + 1) * P],
                     lhsT=cols[:, m : m + 1].to_broadcast([P, P]),
@@ -164,12 +167,15 @@ def tile_advancedliquidneuralnetwork_pb_kernel(
                 nc.scalar.copy(out=everywhere[:, columns(half)], in_=rows[:])
             return everywhere
 
-        def turn(first, second, tag):
+        def turn(first, second, tag, sorted_words=False):
             turned = psum.tile([P, 2, 2, P], F32, name="turned", tag="tp")
             for a, rows in enumerate((first, second)):
                 words = rows.bitcast(F32)
                 for u in range(2):
-                    nc.tensor.transpose(turned[:, a, u, :], words[:, u : K_PASS // 2 : 2], ident_f32[:])
+                    if sorted_words:
+                        nc.tensor.transpose(turned[:, a, u, :], words[:, u * P : (u + 1) * P], ident_f32[:])
+                    else:
+                        nc.tensor.transpose(turned[:, a, u, :], words[:, u : K_PASS // 2 : 2], ident_f32[:])
             grouped = ring.tile([P, 2, P, PACK], BF16, name=tag, tag=tag, bufs=3, align_bytes=64)
             nc.scalar.copy(out=grouped[:].bitcast(F32), in_=turned[:].rearrange("p a u r -> p a r u"))
             return grouped
@@ -301,13 +307,16 @@ def tile_advancedliquidneuralnetwork_pb_kernel(
             v_bf[i] = ring.tile([P, H], BF16, name="v_bf", tag="v_bf", bufs=3)
             for half in range(H_BANKS):
                 nc.vector.tensor_tensor(
-                    out=v_bf[i][:, columns(half)], in0=v_acc[i][half][:], in1=b_v_rows[:, columns(half)], op=ALU.add
+                    out=v_bf[i][:, columns(half)].rearrange("r (u p e) -> r u p e", u=2, e=2),
+                    in0=v_acc[i][half][:].rearrange("r (p u e) -> r u p e", u=2, e=2),
+                    in1=b_v_rows[:, columns(half)].rearrange("r (p u e) -> r u p e", u=2, e=2),
+                    op=ALU.add,
                 )
 
         def turn_v(pair):
             for g in range(H_GROUPS):
                 features = slice(g * K_PASS, (g + 1) * K_PASS)
-                grouped_v[pair, g] = turn(v_bf[2 * pair][:, features], v_bf[2 * pair + 1][:, features], "grouped_v")
+                grouped_v[pair, g] = turn(v_bf[2 * pair][:, features], v_bf[2 * pair + 1][:, features], "grouped_v", sorted_words=True)
 
         def quantise_v(pair):
             for g in range(H_GROUPS):
@@ -327,7 +336,7 @@ def tile_advancedliquidneuralnetwork_pb_kernel(
                     accum_out=sums[i][:, half : half + 1],
                 )
 
-        def variance(i):
+        def minus_mean(i):
             neg_mean[i] = stat.tile([P, 1], F32, name="neg_mean", tag="neg_mean")
             nc.vector.tensor_scalar(
                 out=neg_mean[i][:],
@@ -337,6 +346,8 @@ def tile_advancedliquidneuralnetwork_pb_kernel(
                 op0=ALU.add,
                 op1=ALU.mult,
             )
+
+        def variance(i):
             squares = ring.tile([P, H], BF16, name="squares", tag="squares")
             sum_sq = stat.tile([P, 1], F32, name="sum_sq", tag="sum_sq")
             nc.scalar.activation(
@@ -400,19 +411,20 @@ def tile_advancedliquidneuralnetwork_pb_kernel(
                 v_acc[s + 1] = liq_times_w_v(s + 1)
             if live(s + LIQ_AHEAD):
                 grouped_liq[s + LIQ_AHEAD] = turn_liq(s + LIQ_AHEAD)
+            if live(s - ATT_LAG - 3):
+                times_rate(s - ATT_LAG - 3)
             if live(s - ATT_LAG - 1):
+                minus_mean(s - ATT_LAG - 1)
                 variance(s - ATT_LAG - 1)
             if live(s - 1) and s % 2 == 0:
                 quantise_v(s // 2 - 1)
                 att_of_pair(s // 2 - 1)
             if live(s - ATT_LAG):
                 att_acc[s - ATT_LAG] = turn_back(att_turned[(s - ATT_LAG) // 2], "att", (s - ATT_LAG) % 2)
-            if live(s - ATT_LAG - 1):
-                centre_and_gain(s - ATT_LAG - 1)
-            if live(s - ATT_LAG - 3):
-                times_rate(s - ATT_LAG - 3)
             if live(s - ATT_LAG - 2):
                 squash(s - ATT_LAG - 2)
+            if live(s - ATT_LAG - 1):
+                centre_and_gain(s - ATT_LAG - 1)
             if live(s - ATT_LAG - 3):
                 add_share_of_h(s - ATT_LAG - 3)
             if live(s + LIQ_AHEAD - 1):

@@ -31,6 +31,7 @@ PLANES = 5
 WORK_BUFS = 4
 LIQ_AHEAD = 3
 H_SHARE_BUFS = TILES
+LAST_TILE = TILES - 1
 ROW_TAU, ROW_BETA, ROW_B_IN, ROW_B_V, ROW_B_O, ROW_G = 0, 1, 2, 3, 4, 5
 
 
@@ -376,14 +377,31 @@ def tile_advancedliquidneuralnetwork_pb_kernel(
                     op0=ALU.mult,
                     op1=ALU.add,
                 )
-            nc.scalar.activation(out=work[i][:], in_=work[i][:], func=ACT.Tanh)
+                if i == LAST_TILE:
+                    nc.scalar.activation(out=work[i][:, columns(half)], in_=work[i][:, columns(half)], func=ACT.Tanh)
+            if i != LAST_TILE:
+                nc.scalar.activation(out=work[i][:], in_=work[i][:], func=ACT.Tanh)
+
+        def blend_columns(i, cols):
+            nc.vector.tensor_tensor(out=work[i][:, cols], in0=work[i][:, cols], in1=rate_rows[:, cols], op=ALU.mult)
 
         def times_rate(i):
-            nc.vector.tensor_tensor(out=work[i][:], in0=work[i][:], in1=rate_rows[:], op=ALU.mult)
+            if i == LAST_TILE:
+                return
+            blend_columns(i, slice(0, H))
+
+        def finish_columns(i, cols):
+            nc.vector.tensor_tensor(out=work[i][:, cols], in0=work[i][:, cols], in1=h_share[i][:, cols], op=ALU.add)
+            nc.sync.dma_start(out=out_rows[:, i, cols], in_=work[i][:, cols])
 
         def add_share_of_h(i):
-            nc.vector.tensor_tensor(out=work[i][:], in0=work[i][:], in1=h_share[i][:], op=ALU.add)
-            nc.sync.dma_start(out=out_rows[:, i, :], in_=work[i][:])
+            if i == LAST_TILE:
+                blend_columns(i, columns(0))
+                blend_columns(i, columns(1))
+                finish_columns(i, columns(0))
+                finish_columns(i, columns(1))
+                return
+            finish_columns(i, slice(0, H))
 
         rate_rows = keep.tile([P, H], F32)
         stay_rows = keep.tile([P, H], F32)

@@ -377,10 +377,7 @@ def tile_advancedliquidneuralnetwork_pb_kernel(
                     op0=ALU.mult,
                     op1=ALU.add,
                 )
-                if i == LAST_TILE:
-                    nc.scalar.activation(out=work[i][:, columns(half)], in_=work[i][:, columns(half)], func=ACT.Tanh)
-            if i != LAST_TILE:
-                nc.scalar.activation(out=work[i][:], in_=work[i][:], func=ACT.Tanh)
+                nc.scalar.activation(out=work[i][:, columns(half)], in_=work[i][:, columns(half)], func=ACT.Tanh)
 
         def blend_columns(i, cols):
             nc.vector.tensor_tensor(out=work[i][:, cols], in0=work[i][:, cols], in1=rate_rows[:, cols], op=ALU.mult)

@@ -32,6 +32,7 @@ WORK_BUFS = 4
 LIQ_AHEAD = 3
 H_SHARE_BUFS = TILES
 LAST_TILE = TILES - 1
+WARM_UP_MATMULS = 8
 ROW_TAU, ROW_BETA, ROW_B_IN, ROW_B_V, ROW_B_O, ROW_G = 0, 1, 2, 3, 4, 5
 
 
@@ -407,6 +408,9 @@ def tile_advancedliquidneuralnetwork_pb_kernel(
             grouped_liq[i] = turn_liq(i)
         for i in range(LIQ_AHEAD - 1):
             quantise(grouped_liq[i], liq_codes[:, i, :], liq_scales[:, i, :])
+        for k in range(WARM_UP_MATMULS):
+            unread_bank = bank("xin")
+            nc.tensor.matmul(out=unread_bank[:], lhsT=ident_bf[:], rhs=liq_sb[:, 0, columns(k % 2)], start=True, stop=True)
         v_acc[0] = liq_times_w_v(0)
 
         def live(tile_index):

@@ -29,9 +29,8 @@ FLOPS = 2 * B * (IN * H + H * H + H * H)
 PLANE_IN, PLANE_V, PLANE_O = 0, 1, 3
 PLANES = 5
 WORK_BUFS = 4
-LIQ_AHEAD = 3
-H_SHARE_BUFS = TILES
-LAST_TILE = TILES - 1
+PSUM_BANKS = {"s": 3, "b": 3, "h": 2}
+PAIRS = TILES // 2
 WARM_UP_MATMULS = 8
 ROW_TAU, ROW_BETA, ROW_B_IN, ROW_B_V, ROW_B_O, ROW_G = 0, 1, 2, 3, 4, 5
 
@@ -60,10 +59,10 @@ def tile_advancedliquidneuralnetwork_pb_kernel(
         keep = ctx.enter_context(tc.tile_pool(name="keep", bufs=1))
         ring = ctx.enter_context(tc.tile_pool(name="ring", bufs=2))
         stat = ctx.enter_context(tc.tile_pool(name="stat", bufs=4))
-        psum = ctx.enter_context(tc.psum_pool(name="psum", bufs=2))
+        psum = ctx.enter_context(tc.psum_pool(name="psum", bufs=1))
 
         def bank(tag):
-            return psum.tile([P, BANK], F32, name=tag, tag=tag)
+            return psum.tile([P, BANK], F32, name=tag, tag=tag, bufs=PSUM_BANKS[tag])
 
         liq_sb = keep.tile([P, TILES, H], BF16)
         x_sb = keep.tile([P, TILES, IN], BF16)
@@ -83,6 +82,7 @@ def tile_advancedliquidneuralnetwork_pb_kernel(
         ident_bf = keep.tile([P, P], BF16)
         ident_f32 = keep.tile([P, P], F32)
         minus_half = keep.tile([P, 1], F32)
+        rate_rows = keep.tile([P, H], F32)
 
         liq_rows = liq.rearrange("(p i) f -> p i f", i=TILES)
         x_rows = x.rearrange("(p i) f -> p i f", i=TILES)
@@ -146,31 +146,33 @@ def tile_advancedliquidneuralnetwork_pb_kernel(
         def columns(half):
             return slice(half * BANK, (half + 1) * BANK)
 
-        def spread(cols, ident, half):
-            rows = bank("tp")
-            for q in range(BANK // P):
-                m = half * (BANK // P) + q
-                if ident is ident_f32:
-                    nc.tensor.transpose(rows[:, q * P : (q + 1) * P], cols[:, m : m + 1].to_broadcast([P, P]), ident[:])
-                    continue
-                nc.tensor.matmul(
-                    out=rows[:, q * P : (q + 1) * P],
-                    lhsT=cols[:, m : m + 1].to_broadcast([P, P]),
-                    rhs=ident[:],
-                    start=True,
-                    stop=True,
-                )
-            return rows
-
         def spread_input_vector(row, name):
             everywhere = keep.tile([P, H], BF16, name=name)
             for half in range(H_BANKS):
-                rows = spread(block_cols(vec_cols_bf, row), ident_bf, half)
+                rows = bank("s")
+                for q in range(BANK // P):
+                    r = H_BLOCKS * row + half * (BANK // P) + q
+                    nc.tensor.matmul(
+                        out=rows[:, q * P : (q + 1) * P],
+                        lhsT=ident_bf[:, r : r + 1].to_broadcast([P, P]),
+                        rhs=vec_rows[:],
+                        start=True,
+                        stop=True,
+                    )
                 nc.scalar.copy(out=everywhere[:, columns(half)], in_=rows[:])
             return everywhere
 
+        def spread_rate(half):
+            rows = bank("s")
+            for q in range(BANK // P):
+                m = half * (BANK // P) + q
+                nc.tensor.transpose(
+                    rows[:, q * P : (q + 1) * P], rate_cols[:, m : m + 1].to_broadcast([P, P]), ident_f32[:]
+                )
+            nc.scalar.copy(out=rate_rows[:, columns(half)], in_=rows[:])
+
         def turn(first, second, tag, sorted_words=False):
-            turned = psum.tile([P, 2, 2, P], F32, name="turned", tag="tp")
+            turned = psum.tile([P, 2, 2, P], F32, name="turned", tag="s", bufs=PSUM_BANKS["s"])
             for a, rows in enumerate((first, second)):
                 words = rows.bitcast(F32)
                 for u in range(2):
@@ -194,151 +196,148 @@ def tile_advancedliquidneuralnetwork_pb_kernel(
         grouped_liq[0] = turn_liq(0)
         grouped_liq[1] = turn_liq(1)
 
-        vec_ps = psum.tile([P, P], BF16, name="vec_ps", tag="tp")
+        def quantise_liq(i):
+            quantise(grouped_liq[i], liq_codes[:, i, :], liq_scales[:, i, :])
+
+        b_v_rows = spread_input_vector(ROW_B_V, "b_v_rows")
+        quantise_liq(0)
+        quantise_liq(1)
+
+        vec_ps = psum.tile([P, P], BF16, name="vec_ps", tag="s", bufs=PSUM_BANKS["s"])
         nc.tensor.transpose(vec_ps[:], vec_rows[:], ident_bf[:])
-        vec_cols_bf = keep.tile([P, 6 * H_BLOCKS], BF16)
         vec_cols = keep.tile([P, 6 * H_BLOCKS], F32)
-        nc.vector.tensor_copy(out=vec_cols_bf[:], in_=vec_ps[:, : 6 * H_BLOCKS])
         nc.vector.tensor_copy(out=vec_cols[:], in_=vec_ps[:, : 6 * H_BLOCKS])
+        g_cols = block_cols(vec_cols, ROW_G)
+        b_o_cols = block_cols(vec_cols, ROW_B_O)
 
         shift_cols = keep.tile([P, H_BLOCKS], F32)
         rate_cols = keep.tile([P, H_BLOCKS], F32)
+        h_factor_cols = keep.tile([P, H_BLOCKS], F32)
         nc.vector.tensor_tensor(
             out=shift_cols[:], in0=block_cols(vec_cols, ROW_BETA), in1=block_cols(vec_cols, ROW_B_IN), op=ALU.add
         )
         nc.vector.tensor_scalar_add(out=rate_cols[:], in0=block_cols(vec_cols, ROW_TAU), scalar1=TAU_EPS)
         nc.vector.reciprocal(out=rate_cols[:], in_=rate_cols[:])
-
-        grouped_x = {}
+        nc.vector.tensor_scalar(
+            out=h_factor_cols[:],
+            in0=block_cols(vec_cols, ROW_TAU),
+            scalar1=-1.0,
+            scalar2=TAU_EPS,
+            op0=ALU.add,
+            op1=ALU.add,
+        )
 
         def pair_tokens(pair):
             return slice(2 * pair * P, (2 * pair + 2) * P)
 
-        def turn_x(pair):
-            grouped_x[pair] = turn(x_sb[:, 2 * pair, :], x_sb[:, 2 * pair + 1, :], "grouped_x")
+        grouped_x, grouped_v = {}, {}
+        v_bf, resid, sums, neg_mean, rstd = {}, {}, {}, {}, {}
+        att_turned, turned_h, work = {}, {}, {}
 
-        def quantise_x(pair):
-            quantise(grouped_x[pair], x_codes[:, 0, pair_tokens(pair)], x_scales[:, 0, pair_tokens(pair)])
+        def stage_a(pair, a):
+            grouped_liq[2 * pair + a] = turn_liq(2 * pair + a)
 
-        def turned_block(dst, w_codes, plane, codes, scales, bias_cols, token_half, m):
-            tokens = columns(token_half)
-            features = slice(m * P, (m + 1) * P)
-            groups = codes.shape[1]
-            acc = bank("tp")
-            for g in range(groups):
+        def stage_aq(pair):
+            quantise_liq(2 * pair)
+            quantise_liq(2 * pair + 1)
+
+        def stage_b(pair, quarter):
+            i, half = 2 * pair + quarter // H_BANKS, quarter % H_BANKS
+            if half == 0:
+                v_bf[i] = ring.tile([P, H], BF16, name="v_bf", tag="v_bf", bufs=4)
+            acc = bank("b")
+            for g in range(H_GROUPS):
+                group = slice(g * P, (g + 1) * P)
                 nc.tensor.matmul_mx(
                     out=acc[:],
-                    lhsT=w_codes[:, g, features].bitcast(FP8X4),
-                    lhsT_scale=w_scales[:, plane + g, features],
-                    rhs=codes[:, g, tokens].bitcast(FP8X4),
-                    rhs_scale=scales[:, g, tokens],
+                    lhsT=liq_codes[:, i, group].bitcast(FP8X4),
+                    lhsT_scale=liq_scales[:, i, group],
+                    rhs=w_v_codes[:, g, columns(half)].bitcast(FP8X4),
+                    rhs_scale=w_scales[:, PLANE_V + g, columns(half)],
                     start=(g == 0),
-                    stop=(g == groups - 1),
+                    stop=(g == H_GROUPS - 1),
                 )
-            nc.scalar.activation(
-                out=dst, in_=acc[:], func=ACT.Identity, bias=bias_cols[:, m : m + 1], scale=1.0
+            nc.vector.tensor_tensor(
+                out=v_bf[i][:, columns(half)].rearrange("r (u p e) -> r u p e", u=2, e=2),
+                in0=acc[:].rearrange("r (p u e) -> r u p e", u=2, e=2),
+                in1=b_v_rows[:, columns(half)].rearrange("r (p u e) -> r u p e", u=2, e=2),
+                op=ALU.add,
             )
 
-        def xin_block(token_half, m):
-            dst = xin_turned[:, m, columns(token_half)]
-            turned_block(dst, w_in_codes, PLANE_IN, x_codes, x_scales, shift_cols, token_half, m)
+        def stage_c(pair, g):
+            features = slice(g * K_PASS, (g + 1) * K_PASS)
+            grouped_v[pair, g] = turn(v_bf[2 * pair][:, features], v_bf[2 * pair + 1][:, features], "grouped_v", sorted_words=True)
 
-        def att_of_pair(pair):
-            b_o_cols = block_cols(vec_cols, ROW_B_O)
-            att_turned[pair] = ring.tile([P, H_BLOCKS, 2 * P], F32, name="att_turned", tag="att_turned")
-            for mm in range(H_BLOCKS // 2):
-                acc = bank("tp")
-                for a in range(2):
-                    features = slice((2 * mm + a) * P, (2 * mm + a + 1) * P)
-                    for g in range(H_GROUPS):
-                        nc.tensor.matmul_mx(
-                            out=acc[:, 2 * a * P : (2 * a + 2) * P],
-                            lhsT=w_o_codes[:, g, features].bitcast(FP8X4),
-                            lhsT_scale=w_scales[:, PLANE_O + g, features],
-                            rhs=v_codes[:, g, pair_tokens(pair)].bitcast(FP8X4),
-                            rhs_scale=v_scales[:, g, pair_tokens(pair)],
-                            start=(g == 0),
-                            stop=(g == H_GROUPS - 1),
-                        )
-                for a in range(2):
-                    m = 2 * mm + a
-                    nc.scalar.activation(
-                        out=att_turned[pair][:, m, :],
-                        in_=acc[:, 2 * a * P : (2 * a + 2) * P],
-                        func=ACT.Identity,
-                        bias=b_o_cols[:, m : m + 1],
-                        scale=1.0,
-                    )
-
-        def turn_back(turned, tag, i):
-            banks = [bank(tag), bank(tag)]
-            for m in range(H_BLOCKS):
-                q = m % (BANK // P)
-                nc.tensor.transpose(
-                    banks[m // (BANK // P)][:, q * P : (q + 1) * P], turned[:, m, i * P : (i + 1) * P], ident_f32[:]
-                )
-            return banks
-
-        def liq_times_w_v(i):
-            banks = []
-            for half in range(H_BANKS):
-                acc = bank("v")
-                for g in range(H_GROUPS):
-                    group = slice(g * P, (g + 1) * P)
-                    nc.tensor.matmul_mx(
-                        out=acc[:],
-                        lhsT=liq_codes[:, i, group].bitcast(FP8X4),
-                        lhsT_scale=liq_scales[:, i, group],
-                        rhs=w_v_codes[:, g, columns(half)].bitcast(FP8X4),
-                        rhs_scale=w_scales[:, PLANE_V + g, columns(half)],
-                        start=(g == 0),
-                        stop=(g == H_GROUPS - 1),
-                    )
-                banks.append(acc)
-            return banks
-
-        v_acc, att_acc, xin_acc, att_turned = {}, {}, {}, {}
-        v_bf, grouped_v = {}, {}
-        resid, work, h_share, sums, neg_mean, rstd = {}, {}, {}, {}, {}, {}
-
-        def share_of_h(i):
-            h_share[i] = ring.tile([P, H], F32, name="h_share", tag="h_share", bufs=H_SHARE_BUFS)
-            nc.vector.tensor_tensor(out=h_share[i][:], in0=h_sb[:, i, :], in1=stay_rows[:], op=ALU.mult)
-
-        def round_v(i):
-            v_bf[i] = ring.tile([P, H], BF16, name="v_bf", tag="v_bf", bufs=3)
-            for half in range(H_BANKS):
-                nc.vector.tensor_tensor(
-                    out=v_bf[i][:, columns(half)].rearrange("r (u p e) -> r u p e", u=2, e=2),
-                    in0=v_acc[i][half][:].rearrange("r (p u e) -> r u p e", u=2, e=2),
-                    in1=b_v_rows[:, columns(half)].rearrange("r (p u e) -> r u p e", u=2, e=2),
-                    op=ALU.add,
-                )
-
-        def turn_v(pair):
-            for g in range(H_GROUPS):
-                features = slice(g * K_PASS, (g + 1) * K_PASS)
-                grouped_v[pair, g] = turn(v_bf[2 * pair][:, features], v_bf[2 * pair + 1][:, features], "grouped_v", sorted_words=True)
-
-        def quantise_v(pair):
+        def stage_cq(pair):
             for g in range(H_GROUPS):
                 quantise(grouped_v[pair, g], v_codes[:, g, pair_tokens(pair)], v_scales[:, g, pair_tokens(pair)])
 
-        def add_residual(i):
-            resid[i] = ring.tile([P, H], F32, name="resid", tag="resid")
-            sums[i] = stat.tile([P, H_BANKS], F32, name="sums", tag="sums")
-            for half in range(H_BANKS):
-                nc.vector.scalar_tensor_tensor(
-                    out=resid[i][:, columns(half)],
-                    in0=att_acc[i][half][:],
-                    scalar=1.0,
-                    in1=liq_sb[:, i, columns(half)],
-                    op0=ALU.mult,
-                    op1=ALU.add,
-                    accum_out=sums[i][:, half : half + 1],
+        def two_blocks(dst, first, w_codes, plane, codes, scales, bias_cols, pair):
+            groups = codes.shape[1]
+            acc = bank("s")
+            for a in range(2):
+                features = slice((first + a) * P, (first + a + 1) * P)
+                for g in range(groups):
+                    nc.tensor.matmul_mx(
+                        out=acc[:, 2 * a * P : (2 * a + 2) * P],
+                        lhsT=w_codes[:, g, features].bitcast(FP8X4),
+                        lhsT_scale=w_scales[:, plane + g, features],
+                        rhs=codes[:, g, pair_tokens(pair)].bitcast(FP8X4),
+                        rhs_scale=scales[:, g, pair_tokens(pair)],
+                        start=(g == 0),
+                        stop=(g == groups - 1),
+                    )
+            for a in range(2):
+                nc.scalar.activation(
+                    out=dst[:, first + a, :],
+                    in_=acc[:, 2 * a * P : (2 * a + 2) * P],
+                    func=ACT.Identity,
+                    bias=bias_cols[:, first + a : first + a + 1],
+                    scale=1.0,
                 )
 
-        def minus_mean(i):
+        def stage_d(pair, quarter):
+            if quarter == 0:
+                att_turned[pair] = ring.tile([P, H_BLOCKS, 2 * P], F32, name="att_turned", tag="att_turned", bufs=2)
+            two_blocks(att_turned[pair], 2 * quarter, w_o_codes, PLANE_O, v_codes, v_scales, b_o_cols, pair)
+
+        def cell(pair):
+            return xin_turned[:, :, pair_tokens(pair)]
+
+        def stage_x(pair, quarter):
+            two_blocks(cell(pair), 2 * quarter, w_in_codes, PLANE_IN, x_codes, x_scales, shift_cols, pair)
+
+        def stage_xt(pair):
+            grouped_x[pair] = turn(x_sb[:, 2 * pair, :], x_sb[:, 2 * pair + 1, :], "grouped_x")
+
+        def stage_xq(pair):
+            quantise(grouped_x[pair], x_codes[:, 0, pair_tokens(pair)], x_scales[:, 0, pair_tokens(pair)])
+
+        def stage_e(pair, quarter):
+            a, half = quarter // H_BANKS, quarter % H_BANKS
+            i = 2 * pair + a
+            if half == 0:
+                resid[i] = ring.tile([P, H], F32, name="resid", tag="resid", bufs=4)
+                sums[i] = stat.tile([P, H_BANKS], F32, name="sums", tag="sums")
+            acc = bank("b")
+            for q in range(BANK // P):
+                nc.tensor.transpose(
+                    acc[:, q * P : (q + 1) * P],
+                    att_turned[pair][:, half * (BANK // P) + q, a * P : (a + 1) * P],
+                    ident_f32[:],
+                )
+            nc.vector.scalar_tensor_tensor(
+                out=resid[i][:, columns(half)],
+                in0=acc[:],
+                scalar=1.0,
+                in1=liq_sb[:, i, columns(half)],
+                op0=ALU.mult,
+                op1=ALU.add,
+                accum_out=sums[i][:, half : half + 1],
+            )
+
+        def stage_n(pair, a):
+            i = 2 * pair + a
             neg_mean[i] = stat.tile([P, 1], F32, name="neg_mean", tag="neg_mean")
             nc.vector.tensor_scalar(
                 out=neg_mean[i][:],
@@ -348,8 +347,6 @@ def tile_advancedliquidneuralnetwork_pb_kernel(
                 op0=ALU.add,
                 op1=ALU.mult,
             )
-
-        def variance(i):
             squares = ring.tile([P, H], BF16, name="squares", tag="squares")
             sum_sq = stat.tile([P, 1], F32, name="sum_sq", tag="sum_sq")
             nc.scalar.activation(
@@ -361,113 +358,113 @@ def tile_advancedliquidneuralnetwork_pb_kernel(
             )
             rstd[i] = stat.tile([P, 1], F32, name="rstd", tag="rstd")
             nc.gpsimd.tensor_tensor(out=rstd[i][:], in0=var_eps[:], in1=minus_half[:], op=ALU.pow)
-
-        def centre_and_gain(i):
-            work[i] = ring.tile([P, H], F32, name="work", tag="work", bufs=WORK_BUFS)
-            nc.vector.scalar_tensor_tensor(
-                out=work[i][:], in0=resid[i][:], scalar=neg_mean[i][:], in1=g_rows[:], op0=ALU.add, op1=ALU.mult
+            nc.vector.tensor_scalar(
+                out=resid[i][:],
+                in0=resid[i][:],
+                scalar1=neg_mean[i][:],
+                scalar2=rstd[i][:],
+                op0=ALU.add,
+                op1=ALU.mult,
             )
 
-        def squash(i):
-            for half in range(H_BANKS):
+        def stage_f(pair, quarter):
+            acc = psum.tile([P, 2, 2 * P], F32, name="turned_q", tag="b", bufs=PSUM_BANKS["b"])
+            for b in range(2):
+                m = 2 * quarter + b
+                for a in range(2):
+                    nc.tensor.transpose(
+                        acc[:, b, a * P : (a + 1) * P], resid[2 * pair + a][:, m * P : (m + 1) * P], ident_f32[:]
+                    )
+            for b in range(2):
+                m = 2 * quarter + b
                 nc.vector.scalar_tensor_tensor(
-                    out=work[i][:, columns(half)],
-                    in0=work[i][:, columns(half)],
-                    scalar=rstd[i][:],
-                    in1=xin_acc[i][half][:],
+                    out=cell(pair)[:, m, :],
+                    in0=acc[:, b, :],
+                    scalar=g_cols[:, m : m + 1],
+                    in1=cell(pair)[:, m, :],
                     op0=ALU.mult,
                     op1=ALU.add,
                 )
-                nc.scalar.activation(out=work[i][:, columns(half)], in_=work[i][:, columns(half)], func=ACT.Tanh)
+            blocks = cell(pair)[:, 2 * quarter : 2 * quarter + 2, :]
+            nc.scalar.activation(out=blocks, in_=blocks, func=ACT.Tanh)
 
-        def blend_columns(i, cols):
-            nc.vector.tensor_tensor(out=work[i][:, cols], in0=work[i][:, cols], in1=rate_rows[:, cols], op=ALU.mult)
+        def stage_g(pair, half):
+            turned_h[pair, half] = psum.tile([P, 4, 2 * P], BF16, name="turned_h", tag="h", bufs=PSUM_BANKS["h"])
+            for b in range(4):
+                m = 4 * half + b
+                for a in range(2):
+                    nc.tensor.transpose(
+                        turned_h[pair, half][:, b, a * P : (a + 1) * P],
+                        h_sb[:, 2 * pair + a, m * P : (m + 1) * P],
+                        ident_bf[:],
+                    )
 
-        def times_rate(i):
-            if i == LAST_TILE:
-                return
-            blend_columns(i, slice(0, H))
+        def stage_y(pair, half):
+            for b in range(4):
+                m = 4 * half + b
+                nc.vector.scalar_tensor_tensor(
+                    out=cell(pair)[:, m, :],
+                    in0=turned_h[pair, half][:, b, :],
+                    scalar=h_factor_cols[:, m : m + 1],
+                    in1=cell(pair)[:, m, :],
+                    op0=ALU.mult,
+                    op1=ALU.add,
+                )
 
-        def finish_columns(i, cols):
-            nc.vector.tensor_tensor(out=work[i][:, cols], in0=work[i][:, cols], in1=h_share[i][:, cols], op=ALU.add)
+        def stage_h(pair, quarter):
+            half, a = quarter // 2, quarter % 2
+            i = 2 * pair + a
+            if half == 0:
+                work[i] = ring.tile([P, H], F32, name="work", tag="work", bufs=WORK_BUFS)
+            acc = bank("b")
+            for b in range(4):
+                nc.tensor.transpose(
+                    acc[:, b * P : (b + 1) * P], cell(pair)[:, 4 * half + b, a * P : (a + 1) * P], ident_f32[:]
+                )
+            cols = columns(half)
+            nc.vector.tensor_tensor(out=work[i][:, cols], in0=acc[:], in1=rate_rows[:, cols], op=ALU.mult)
             nc.sync.dma_start(out=out_rows[:, i, cols], in_=work[i][:, cols])
 
-        def add_share_of_h(i):
-            if i == LAST_TILE:
-                blend_columns(i, columns(0))
-                blend_columns(i, columns(1))
-                finish_columns(i, columns(0))
-                finish_columns(i, columns(1))
-                return
-            finish_columns(i, slice(0, H))
-
-        rate_rows = keep.tile([P, H], F32)
-        stay_rows = keep.tile([P, H], F32)
-        b_v_rows = spread_input_vector(ROW_B_V, "b_v_rows")
-        for i in range(2, LIQ_AHEAD):
-            grouped_liq[i] = turn_liq(i)
-        for i in range(LIQ_AHEAD - 1):
-            quantise(grouped_liq[i], liq_codes[:, i, :], liq_scales[:, i, :])
         for k in range(WARM_UP_MATMULS):
-            unread_bank = bank("xin")
+            unread_bank = bank("b")
             nc.tensor.matmul(out=unread_bank[:], lhsT=ident_bf[:], rhs=liq_sb[:, 0, columns(k % 2)], start=True, stop=True)
-        v_acc[0] = liq_times_w_v(0)
 
-        def live(tile_index):
-            return 0 <= tile_index < TILES
+        def live(pair):
+            return 0 <= pair < PAIRS
 
-        ATT_LAG = 2
-        for s in range(TILES + ATT_LAG + 4):
-            if live(s - ATT_LAG - 2):
-                xin_acc[s - ATT_LAG - 2] = turn_back(xin_turned, "xin", s - ATT_LAG - 2)
-            if live(s - ATT_LAG - 1):
-                add_residual(s - ATT_LAG - 1)
-            if live(s):
-                round_v(s)
-                if s % 2 == 1:
-                    turn_v(s // 2)
-            if live(s + 1):
-                v_acc[s + 1] = liq_times_w_v(s + 1)
-            if live(s + LIQ_AHEAD):
-                grouped_liq[s + LIQ_AHEAD] = turn_liq(s + LIQ_AHEAD)
-            if live(s - ATT_LAG - 3):
-                times_rate(s - ATT_LAG - 3)
-            if live(s - ATT_LAG - 1):
-                minus_mean(s - ATT_LAG - 1)
-                variance(s - ATT_LAG - 1)
-            if live(s - 1) and s % 2 == 0:
-                quantise_v(s // 2 - 1)
-                att_of_pair(s // 2 - 1)
-            if live(s - ATT_LAG):
-                att_acc[s - ATT_LAG] = turn_back(att_turned[(s - ATT_LAG) // 2], "att", (s - ATT_LAG) % 2)
-            if live(s - ATT_LAG - 2):
-                squash(s - ATT_LAG - 2)
-            if live(s - ATT_LAG - 1):
-                centre_and_gain(s - ATT_LAG - 1)
-            if live(s - ATT_LAG - 3):
-                add_share_of_h(s - ATT_LAG - 3)
-            if live(s + LIQ_AHEAD - 1):
-                t = s + LIQ_AHEAD - 1
-                quantise(grouped_liq[t], liq_codes[:, t, :], liq_scales[:, t, :])
-            if s == 0:
-                for half in range(H_BANKS):
-                    rows = spread(rate_cols, ident_f32, half)
-                    nc.scalar.copy(out=rate_rows[:, columns(half)], in_=rows[:])
-                    nc.scalar.activation(out=stay_rows[:, columns(half)], in_=rows[:], func=ACT.Copy, bias=1.0, scale=-1.0)
-            if s == 1:
-                g_rows = spread_input_vector(ROW_G, "g_rows")
-            if 1 <= s < 4:
-                share_of_h(s - 1)
-            if s == 4:
-                for i in range(3, TILES):
-                    share_of_h(i)
-            for token_half in range(2):
-                first_step = 4 * token_half + 1
-                for pair in (2 * token_half, 2 * token_half + 1):
-                    if s == first_step:
-                        turn_x(pair)
-                    if s == first_step + 1:
-                        quantise_x(pair)
-                if s in (first_step + 1, first_step + 2):
-                    for q in range(H_BLOCKS // 2):
-                        xin_block(token_half, (s - first_step - 1) * (H_BLOCKS // 2) + q)
+        def each(pair, stage, parts):
+            return [(stage, pair, part) for part in parts] if live(pair) else []
+
+        def run(calls):
+            for stage, *args in calls:
+                stage(*args)
+
+        def woven(*lists):
+            longest = max(len(calls) for calls in lists)
+            for n in range(longest):
+                for calls in lists:
+                    run(calls[n * len(calls) // longest : (n + 1) * len(calls) // longest])
+
+        with tc.manual_schedule(engines={mybir.EngineType.PE}):
+            quarters = range(4)
+            halves = range(2)
+            for j in range(-1, PAIRS + 3):
+                if live(j - 2):
+                    stage_y(j - 2, 0)
+                    stage_y(j - 2, 1)
+                woven(each(j, stage_d, quarters), each(j + 1, stage_b, quarters), each(j, stage_x, quarters))
+                if j == -1:
+                    spread_rate(0)
+                    spread_rate(1)
+                woven(each(j, stage_e, quarters), each(j + 1, stage_c, halves) + each(j + 2, stage_a, halves))
+                if live(j + 1):
+                    stage_cq(j + 1)
+                if live(j + 2):
+                    stage_aq(j + 2)
+                if live(j):
+                    stage_n(j, 0)
+                    stage_n(j, 1)
+                if live(j + 1):
+                    stage_xt(j + 1)
+                    stage_xq(j + 1)
+                woven(each(j - 1, stage_f, quarters), each(j - 1, stage_g, halves), each(j - 2, stage_h, quarters))

@@ -29,8 +29,16 @@ FLOPS = 2 * B * (IN * H + H * H + H * H)
 PLANE_IN, PLANE_V, PLANE_O = 0, 1, 3
 PLANES = 5
 WORK_BUFS = 4
-PSUM_BANKS = {"s": 3, "b": 3, "h": 2}
+PSUM_BANKS = {"s": 3, "b": 5}
 PAIRS = TILES // 2
+LIQ_COPIES_ON_VECTOR = ()
+X_COPIES_ON_VECTOR = ()
+V_COPIES_ON_VECTOR = ()
+TOKEN_PAIRS = (0, 1, 2, 3)
+LIQ_B_ON_GPSIMD = ()
+H_ON_GPSIMD = ()
+NORM_ON_VECTOR = (0, 1, 2, 3, 4, 5, 6, 7)
+LIQ_B_BUFS = max(1, 2 * len(TOKEN_PAIRS))
 WARM_UP_MATMULS = 8
 ROW_TAU, ROW_BETA, ROW_B_IN, ROW_B_V, ROW_B_O, ROW_G = 0, 1, 2, 3, 4, 5
 
@@ -171,7 +179,7 @@ def tile_advancedliquidneuralnetwork_pb_kernel(
                 )
             nc.scalar.copy(out=rate_rows[:, columns(half)], in_=rows[:])
 
-        def turn(first, second, tag, sorted_words=False):
+        def turn(first, second, tag, sorted_words=False, on_vector=False):
             turned = psum.tile([P, 2, 2, P], F32, name="turned", tag="s", bufs=PSUM_BANKS["s"])
             for a, rows in enumerate((first, second)):
                 words = rows.bitcast(F32)
@@ -181,7 +189,10 @@ def tile_advancedliquidneuralnetwork_pb_kernel(
                     else:
                         nc.tensor.transpose(turned[:, a, u, :], words[:, u : K_PASS // 2 : 2], ident_f32[:])
             grouped = ring.tile([P, 2, P, PACK], BF16, name=tag, tag=tag, bufs=3, align_bytes=64)
-            nc.scalar.copy(out=grouped[:].bitcast(F32), in_=turned[:].rearrange("p a u r -> p a r u"))
+            if on_vector:
+                nc.vector.tensor_copy(out=grouped[:].bitcast(F32), in_=turned[:].rearrange("p a u r -> p a r u"))
+            else:
+                nc.scalar.copy(out=grouped[:].bitcast(F32), in_=turned[:].rearrange("p a u r -> p a r u"))
             return grouped
 
         def quantise(grouped, codes, scales):
@@ -190,7 +201,7 @@ def tile_advancedliquidneuralnetwork_pb_kernel(
             )
 
         def turn_liq(i):
-            return turn(liq_sb[:, i, :K_PASS], liq_sb[:, i, K_PASS:], "grouped_liq")
+            return turn(liq_sb[:, i, :K_PASS], liq_sb[:, i, K_PASS:], "grouped_liq", on_vector=i in LIQ_COPIES_ON_VECTOR)
 
         grouped_liq = {}
         grouped_liq[0] = turn_liq(0)
@@ -203,6 +214,9 @@ def tile_advancedliquidneuralnetwork_pb_kernel(
         quantise_liq(0)
         quantise_liq(1)
 
+        if TOKEN_PAIRS:
+            b_o_rows = spread_input_vector(ROW_B_O, "b_o_rows")
+
         vec_ps = psum.tile([P, P], BF16, name="vec_ps", tag="s", bufs=PSUM_BANKS["s"])
         nc.tensor.transpose(vec_ps[:], vec_rows[:], ident_bf[:])
         vec_cols = keep.tile([P, 6 * H_BLOCKS], F32)
@@ -212,20 +226,13 @@ def tile_advancedliquidneuralnetwork_pb_kernel(
 
         shift_cols = keep.tile([P, H_BLOCKS], F32)
         rate_cols = keep.tile([P, H_BLOCKS], F32)
-        h_factor_cols = keep.tile([P, H_BLOCKS], F32)
         nc.vector.tensor_tensor(
             out=shift_cols[:], in0=block_cols(vec_cols, ROW_BETA), in1=block_cols(vec_cols, ROW_B_IN), op=ALU.add
         )
         nc.vector.tensor_scalar_add(out=rate_cols[:], in0=block_cols(vec_cols, ROW_TAU), scalar1=TAU_EPS)
         nc.vector.reciprocal(out=rate_cols[:], in_=rate_cols[:])
-        nc.vector.tensor_scalar(
-            out=h_factor_cols[:],
-            in0=block_cols(vec_cols, ROW_TAU),
-            scalar1=-1.0,
-            scalar2=TAU_EPS,
-            op0=ALU.add,
-            op1=ALU.add,
-        )
+        minus_ident = keep.tile([P, P], BF16)
+        nc.vector.tensor_scalar_mul(out=minus_ident[:], in0=ident_bf[:], scalar1=-1.0)
 
         def pair_tokens(pair):
             return slice(2 * pair * P, (2 * pair + 2) * P)
@@ -237,12 +244,11 @@ def tile_advancedliquidneuralnetwork_pb_kernel(
         def stage_a(pair, a):
             grouped_liq[2 * pair + a] = turn_liq(2 * pair + a)
 
-        def stage_aq(pair):
-            quantise_liq(2 * pair)
-            quantise_liq(2 * pair + 1)
+        def stage_aq(pair, a):
+            quantise_liq(2 * pair + a)
 
         def stage_b(pair, quarter):
-            i, half = 2 * pair + quarter // H_BANKS, quarter % H_BANKS
+            i, half = 2 * pair + quarter % 2, quarter // 2
             if half == 0:
                 v_bf[i] = ring.tile([P, H], BF16, name="v_bf", tag="v_bf", bufs=4)
             acc = bank("b")
@@ -266,11 +272,10 @@ def tile_advancedliquidneuralnetwork_pb_kernel(
 
         def stage_c(pair, g):
             features = slice(g * K_PASS, (g + 1) * K_PASS)
-            grouped_v[pair, g] = turn(v_bf[2 * pair][:, features], v_bf[2 * pair + 1][:, features], "grouped_v", sorted_words=True)
+            grouped_v[pair, g] = turn(v_bf[2 * pair][:, features], v_bf[2 * pair + 1][:, features], "grouped_v", sorted_words=True, on_vector=pair in V_COPIES_ON_VECTOR)
 
-        def stage_cq(pair):
-            for g in range(H_GROUPS):
-                quantise(grouped_v[pair, g], v_codes[:, g, pair_tokens(pair)], v_scales[:, g, pair_tokens(pair)])
+        def stage_cq(pair, g):
+            quantise(grouped_v[pair, g], v_codes[:, g, pair_tokens(pair)], v_scales[:, g, pair_tokens(pair)])
 
         def two_blocks(dst, first, w_codes, plane, codes, scales, bias_cols, pair):
             groups = codes.shape[1]
@@ -301,6 +306,41 @@ def tile_advancedliquidneuralnetwork_pb_kernel(
                 att_turned[pair] = ring.tile([P, H_BLOCKS, 2 * P], F32, name="att_turned", tag="att_turned", bufs=2)
             two_blocks(att_turned[pair], 2 * quarter, w_o_codes, PLANE_O, v_codes, v_scales, b_o_cols, pair)
 
+        liq_b = {}
+
+        def stage_l(pair, a):
+            i = 2 * pair + a
+            liq_b[i] = ring.tile([P, H], F32, name="liq_b", tag="liq_b", bufs=LIQ_B_BUFS)
+            engine = nc.gpsimd if i in LIQ_B_ON_GPSIMD else nc.vector
+            engine.tensor_tensor(out=liq_b[i][:], in0=liq_sb[:, i, :], in1=b_o_rows[:], op=ALU.add)
+
+        def stage_t(pair, quarter):
+            i, half = 2 * pair + quarter // H_BANKS, quarter % H_BANKS
+            if half == 0:
+                resid[i] = liq_b[i]
+                sums[i] = stat.tile([P, H_BANKS], F32, name="sums", tag="sums")
+            acc = bank("b")
+            tokens = slice(i * P, (i + 1) * P)
+            for g in range(H_GROUPS):
+                nc.tensor.matmul_mx(
+                    out=acc[:],
+                    lhsT=v_codes[:, g, tokens].bitcast(FP8X4),
+                    lhsT_scale=v_scales[:, g, tokens],
+                    rhs=w_o_codes[:, g, columns(half)].bitcast(FP8X4),
+                    rhs_scale=w_scales[:, PLANE_O + g, columns(half)],
+                    start=(g == 0),
+                    stop=(g == H_GROUPS - 1),
+                )
+            nc.vector.scalar_tensor_tensor(
+                out=resid[i][:, columns(half)],
+                in0=acc[:],
+                scalar=1.0,
+                in1=liq_b[i][:, columns(half)],
+                op0=ALU.mult,
+                op1=ALU.add,
+                accum_out=sums[i][:, half : half + 1],
+            )
+
         def cell(pair):
             return xin_turned[:, :, pair_tokens(pair)]
 
@@ -308,7 +348,7 @@ def tile_advancedliquidneuralnetwork_pb_kernel(
             two_blocks(cell(pair), 2 * quarter, w_in_codes, PLANE_IN, x_codes, x_scales, shift_cols, pair)
 
         def stage_xt(pair):
-            grouped_x[pair] = turn(x_sb[:, 2 * pair, :], x_sb[:, 2 * pair + 1, :], "grouped_x")
+            grouped_x[pair] = turn(x_sb[:, 2 * pair, :], x_sb[:, 2 * pair + 1, :], "grouped_x", on_vector=pair in X_COPIES_ON_VECTOR)
 
         def stage_xq(pair):
             quantise(grouped_x[pair], x_codes[:, 0, pair_tokens(pair)], x_scales[:, 0, pair_tokens(pair)])
@@ -358,14 +398,21 @@ def tile_advancedliquidneuralnetwork_pb_kernel(
             )
             rstd[i] = stat.tile([P, 1], F32, name="rstd", tag="rstd")
             nc.gpsimd.tensor_tensor(out=rstd[i][:], in0=var_eps[:], in1=minus_half[:], op=ALU.pow)
-            nc.vector.tensor_scalar(
-                out=resid[i][:],
-                in0=resid[i][:],
-                scalar1=neg_mean[i][:],
-                scalar2=rstd[i][:],
-                op0=ALU.add,
-                op1=ALU.mult,
-            )
+            if i in NORM_ON_VECTOR:
+                nc.vector.tensor_scalar(
+                    out=resid[i][:],
+                    in0=resid[i][:],
+                    scalar1=neg_mean[i][:],
+                    scalar2=rstd[i][:],
+                    op0=ALU.add,
+                    op1=ALU.mult,
+                )
+            else:
+                shift = stat.tile([P, 1], F32, name="shift", tag="shift")
+                nc.gpsimd.tensor_tensor(out=shift[:], in0=neg_mean[i][:], in1=rstd[i][:], op=ALU.mult)
+                nc.scalar.activation(
+                    out=resid[i][:], in_=resid[i][:], func=ACT.Identity, bias=shift[:], scale=rstd[i][:]
+                )
 
         def stage_f(pair, quarter):
             acc = psum.tile([P, 2, 2 * P], F32, name="turned_q", tag="b", bufs=PSUM_BANKS["b"])
@@ -388,83 +435,65 @@ def tile_advancedliquidneuralnetwork_pb_kernel(
             blocks = cell(pair)[:, 2 * quarter : 2 * quarter + 2, :]
             nc.scalar.activation(out=blocks, in_=blocks, func=ACT.Tanh)
 
-        def stage_g(pair, half):
-            turned_h[pair, half] = psum.tile([P, 4, 2 * P], BF16, name="turned_h", tag="h", bufs=PSUM_BANKS["h"])
-            for b in range(4):
-                m = 4 * half + b
-                for a in range(2):
-                    nc.tensor.transpose(
-                        turned_h[pair, half][:, b, a * P : (a + 1) * P],
-                        h_sb[:, 2 * pair + a, m * P : (m + 1) * P],
-                        ident_bf[:],
-                    )
-
-        def stage_y(pair, half):
-            for b in range(4):
-                m = 4 * half + b
-                nc.vector.scalar_tensor_tensor(
-                    out=cell(pair)[:, m, :],
-                    in0=turned_h[pair, half][:, b, :],
-                    scalar=h_factor_cols[:, m : m + 1],
-                    in1=cell(pair)[:, m, :],
-                    op0=ALU.mult,
-                    op1=ALU.add,
-                )
-
         def stage_h(pair, quarter):
             half, a = quarter // 2, quarter % 2
             i = 2 * pair + a
             if half == 0:
                 work[i] = ring.tile([P, H], F32, name="work", tag="work", bufs=WORK_BUFS)
-            acc = bank("b")
-            for b in range(4):
-                nc.tensor.transpose(
-                    acc[:, b * P : (b + 1) * P], cell(pair)[:, 4 * half + b, a * P : (a + 1) * P], ident_f32[:]
-                )
             cols = columns(half)
+            acc = bank("b")
+            nc.tensor.matmul(out=acc[:], lhsT=minus_ident[:], rhs=h_sb[:, i, cols], start=True, stop=False)
+            for b in range(4):
+                nc.tensor.matmul(
+                    out=acc[:, b * P : (b + 1) * P],
+                    lhsT=cell(pair)[:, 4 * half + b, a * P : (a + 1) * P],
+                    rhs=ident_f32[:],
+                    is_transpose=True,
+                    start=False,
+                    stop=(b == 3),
+                )
             nc.vector.tensor_tensor(out=work[i][:, cols], in0=acc[:], in1=rate_rows[:, cols], op=ALU.mult)
+            engine = nc.gpsimd if i in H_ON_GPSIMD else nc.vector
+            engine.tensor_tensor(out=work[i][:, cols], in0=work[i][:, cols], in1=h_sb[:, i, cols], op=ALU.add)
             nc.sync.dma_start(out=out_rows[:, i, cols], in_=work[i][:, cols])
 
         for k in range(WARM_UP_MATMULS):
             unread_bank = bank("b")
             nc.tensor.matmul(out=unread_bank[:], lhsT=ident_bf[:], rhs=liq_sb[:, 0, columns(k % 2)], start=True, stop=True)
 
-        def live(pair):
-            return 0 <= pair < PAIRS
-
-        def each(pair, stage, parts):
-            return [(stage, pair, part) for part in parts] if live(pair) else []
-
-        def run(calls):
-            for stage, *args in calls:
-                stage(*args)
-
-        def woven(*lists):
-            longest = max(len(calls) for calls in lists)
-            for n in range(longest):
-                for calls in lists:
-                    run(calls[n * len(calls) // longest : (n + 1) * len(calls) // longest])
+        def due(first, parts=4, every=1):
+            return [
+                (k, n) for k in range(PAIRS) for n in range(parts) if first + 4 * k + every * n == slot
+            ]
 
         with tc.manual_schedule(engines={mybir.EngineType.PE}):
-            quarters = range(4)
-            halves = range(2)
-            for j in range(-1, PAIRS + 3):
-                if live(j - 2):
-                    stage_y(j - 2, 0)
-                    stage_y(j - 2, 1)
-                woven(each(j, stage_d, quarters), each(j + 1, stage_b, quarters), each(j, stage_x, quarters))
-                if j == -1:
+            for slot in range(14 + 4 * PAIRS):
+                for k, n in due(0):
+                    stage_b(k, n)
+                for k, n in due(6):
+                    stage_x(k, n)
+                for k, n in due(6):
+                    stage_t(k, n)
+                for k, n in due(8, 1):
+                    stage_n(k, 0)
+                for k, n in due(10, 1):
+                    stage_n(k, 1)
+                if slot == 4:
                     spread_rate(0)
                     spread_rate(1)
-                woven(each(j, stage_e, quarters), each(j + 1, stage_c, halves) + each(j + 2, stage_a, halves))
-                if live(j + 1):
-                    stage_cq(j + 1)
-                if live(j + 2):
-                    stage_aq(j + 2)
-                if live(j):
-                    stage_n(j, 0)
-                    stage_n(j, 1)
-                if live(j + 1):
-                    stage_xt(j + 1)
-                    stage_xq(j + 1)
-                woven(each(j - 1, stage_f, quarters), each(j - 1, stage_g, halves), each(j - 2, stage_h, quarters))
+                for k, n in due(12):
+                    stage_f(k, n)
+                for k, n in due(2, 2, 2):
+                    stage_c(k, n)
+                    stage_cq(k, n)
+                for k, n in due(14):
+                    stage_h(k, n)
+                for k, n in due(-3, 2):
+                    if k > 0:
+                        stage_a(k, n)
+                        stage_aq(k, n)
+                for k, n in due(3, 1):
+                    stage_xt(k)
+                    stage_xq(k)
+                for k, n in due(1, 2):
+                    stage_l(k, n)

@@ -36,11 +36,12 @@ X_COPIES_ON_VECTOR = ()
 V_COPIES_ON_VECTOR = ()
 TOKEN_PAIRS = (0, 1, 2, 3)
 LIQ_B_ON_GPSIMD = ()
-H_ON_GPSIMD = ()
-NORM_ON_VECTOR = (0, 1, 2, 3, 4, 5, 6, 7)
+H_ON_GPSIMD = (4,5)
+CLOCK_PAIRS = (2, 3)
+NORM_ON_VECTOR = (-1,)
 LIQ_B_BUFS = max(1, 2 * len(TOKEN_PAIRS))
-WARM_UP_MATMULS = 8
-ROW_TAU, ROW_BETA, ROW_B_IN, ROW_B_V, ROW_B_O, ROW_G = 0, 1, 2, 3, 4, 5
+WARM_UP_MATMULS = 12
+ROW_TAU, ROW_BETA, ROW_B_IN, ROW_G, ROW_B_O = 0, 1, 2, 3, 4
 
 
 def tile_advancedliquidneuralnetwork_pb_kernel(
@@ -86,7 +87,9 @@ def tile_advancedliquidneuralnetwork_pb_kernel(
         x_codes = keep.tile([P, 1, B], U32, align_bytes=64)
         x_scales = keep.tile([P, 1, B], U8, align_bytes=64)
         xin_turned = keep.tile([P, H_BLOCKS, B], F32)
+        first_rows = keep.tile([P, P], BF16)
         vec_rows = keep.tile([P, P], BF16)
+        table_loaded = keep.tile([P, 1], F32)
         ident_bf = keep.tile([P, P], BF16)
         ident_f32 = keep.tile([P, P], F32)
         minus_half = keep.tile([P, 1], F32)
@@ -97,56 +100,63 @@ def tile_advancedliquidneuralnetwork_pb_kernel(
         h_rows = h.rearrange("(p i) f -> p i f", i=TILES)
         out_rows = out.rearrange("(p i) f -> p i f", i=TILES)
 
-        nc.vector.memset(vec_rows[:], 0.0)
+        nc.vector.memset(minus_half[:], -0.5)
         nc.vector.memset(w_scales[:, PLANE_V : PLANE_V + H_GROUPS, :].bitcast(I32), 0)
+        nc.vector.memset(first_rows[:], 0.0)
+        nc.vector.memset(vec_rows[:], 0.0)
         nc.vector.memset(w_scales[:, PLANE_O : PLANE_O + H_GROUPS, :].bitcast(I32), 0)
         nc.vector.memset(w_scales[:, PLANE_IN : PLANE_IN + 1, :].bitcast(I32), 0)
-        nc.vector.memset(minus_half[:], -0.5)
         make_identity(nc, ident_bf[:])
         make_identity(nc, ident_f32[:])
-
-        for row, vec in (
-            (ROW_TAU, tau),
-            (ROW_BETA, beta_att),
-            (ROW_B_IN, b_in),
-            (ROW_B_V, b_v),
-            (ROW_B_O, b_o),
-            (ROW_G, g_att),
-        ):
-            nc.scalar.dma_start(
-                out=vec_rows[H_BLOCKS * row : H_BLOCKS * (row + 1), :],
-                in_=vec.rearrange("(m c) -> m c", c=P),
-            )
+        nc.scalar.activation(out=table_loaded[:], in_=minus_half[:], func=ACT.Tanh)
 
         def load_tokens(dst, src, first, count):
             nc.sync.dma_start(out=dst[:, first : first + count, :], in_=src[:, first : first + count, :])
 
-        def load_weight(words, scales, codes, plane):
-            groups = words.shape[0]
+        def load_scales(scales, plane):
+            groups = scales.shape[0]
             for quad in range(4):
                 nc.sync.dma_start(
                     out=w_scales[32 * quad : 32 * quad + 4, plane : plane + groups, :].bitcast(I32),
                     in_=scales[:, 4 * quad : 4 * quad + 4, :].bitcast(I32).rearrange("g r n -> r g n"),
                 )
-            for g in range(groups):
+
+        def load_codes(words, codes, cols):
+            for g in range(words.shape[0]):
                 nc.sync.dma_start(
-                    out=codes[:, g, :].bitcast(I32),
-                    in_=words[g].rearrange("p n t -> p (n t)").bitcast(I32),
+                    out=codes[:, g, cols].bitcast(I32),
+                    in_=words[g, :, cols, :].rearrange("p n t -> p (n t)").bitcast(I32),
                 )
 
+        def load_vector(rows, row, vec):
+            nc.sync.dma_start(
+                out=rows[H_BLOCKS * row : H_BLOCKS * (row + 1), :], in_=vec.rearrange("(m c) -> m c", c=P)
+            )
+
+        every = slice(0, H)
         load_tokens(liq_sb, liq_rows, 0, 1)
+        load_codes(W_v_words, w_v_codes, slice(0, BANK))
+        load_scales(W_v_scales, PLANE_V)
+        load_vector(first_rows, 0, b_v)
         load_tokens(liq_sb, liq_rows, 1, 1)
-        load_weight(W_v_words, W_v_scales, w_v_codes, PLANE_V)
+        load_codes(W_v_words, w_v_codes, slice(BANK, H))
+        load_vector(vec_rows, ROW_B_O, b_o)
+        load_vector(vec_rows, ROW_TAU, tau)
+        load_vector(vec_rows, ROW_G, g_att)
+        load_vector(vec_rows, ROW_BETA, beta_att)
+        load_vector(vec_rows, ROW_B_IN, b_in)
         load_tokens(liq_sb, liq_rows, 2, 2)
-        load_weight(W_o_words, W_o_scales, w_o_codes, PLANE_O)
+        load_scales(W_o_scales, PLANE_O)
+        load_codes(W_o_words, w_o_codes, every)
         load_tokens(x_sb, x_rows, 0, 4)
-        load_weight(W_in_words, W_in_scales, w_in_codes, PLANE_IN)
-        load_tokens(h_sb, h_rows, 0, 2)
+        load_scales(W_in_scales, PLANE_IN)
+        load_codes(W_in_words, w_in_codes, every)
         load_tokens(liq_sb, liq_rows, 4, 2)
-        load_tokens(h_sb, h_rows, 2, 2)
+        load_tokens(h_sb, h_rows, 0, 2)
         load_tokens(liq_sb, liq_rows, 6, 2)
-        load_tokens(h_sb, h_rows, 4, 4)
+        load_tokens(h_sb, h_rows, 2, 2)
         load_tokens(x_sb, x_rows, 4, 4)
+        load_tokens(h_sb, h_rows, 4, 4)
 
         def block_cols(cols, row):
             return cols[:, H_BLOCKS * row : H_BLOCKS * (row + 1)]
@@ -154,7 +164,7 @@ def tile_advancedliquidneuralnetwork_pb_kernel(
         def columns(half):
             return slice(half * BANK, (half + 1) * BANK)
 
-        def spread_input_vector(row, name):
+        def spread_input_vector(rows_tile, row, name):
             everywhere = keep.tile([P, H], BF16, name=name)
             for half in range(H_BANKS):
                 rows = bank("s")
@@ -163,7 +173,7 @@ def tile_advancedliquidneuralnetwork_pb_kernel(
                     nc.tensor.matmul(
                         out=rows[:, q * P : (q + 1) * P],
                         lhsT=ident_bf[:, r : r + 1].to_broadcast([P, P]),
-                        rhs=vec_rows[:],
+                        rhs=rows_tile[:],
                         start=True,
                         stop=True,
                     )
@@ -204,25 +214,27 @@ def tile_advancedliquidneuralnetwork_pb_kernel(
             return turn(liq_sb[:, i, :K_PASS], liq_sb[:, i, K_PASS:], "grouped_liq", on_vector=i in LIQ_COPIES_ON_VECTOR)
 
         grouped_liq = {}
-        grouped_liq[0] = turn_liq(0)
-        grouped_liq[1] = turn_liq(1)
 
         def quantise_liq(i):
             quantise(grouped_liq[i], liq_codes[:, i, :], liq_scales[:, i, :])
 
-        b_v_rows = spread_input_vector(ROW_B_V, "b_v_rows")
+        for k in range(WARM_UP_MATMULS):
+            unread_bank = bank("b")
+            nc.tensor.matmul(out=unread_bank[:, :P], lhsT=ident_bf[:], rhs=ident_bf[:], start=True, stop=True)
+        grouped_liq[0] = turn_liq(0)
         quantise_liq(0)
+        b_v_rows = spread_input_vector(first_rows, 0, "b_v_rows")
+        grouped_liq[1] = turn_liq(1)
         quantise_liq(1)
 
         if TOKEN_PAIRS:
-            b_o_rows = spread_input_vector(ROW_B_O, "b_o_rows")
+            b_o_rows = spread_input_vector(vec_rows, ROW_B_O, "b_o_rows")
 
         vec_ps = psum.tile([P, P], BF16, name="vec_ps", tag="s", bufs=PSUM_BANKS["s"])
         nc.tensor.transpose(vec_ps[:], vec_rows[:], ident_bf[:])
-        vec_cols = keep.tile([P, 6 * H_BLOCKS], F32)
-        nc.vector.tensor_copy(out=vec_cols[:], in_=vec_ps[:, : 6 * H_BLOCKS])
+        vec_cols = keep.tile([P, 5 * H_BLOCKS], F32)
+        nc.vector.tensor_copy(out=vec_cols[:], in_=vec_ps[:, : 5 * H_BLOCKS])
         g_cols = block_cols(vec_cols, ROW_G)
-        b_o_cols = block_cols(vec_cols, ROW_B_O)
 
         shift_cols = keep.tile([P, H_BLOCKS], F32)
         rate_cols = keep.tile([P, H_BLOCKS], F32)
@@ -301,11 +313,6 @@ def tile_advancedliquidneuralnetwork_pb_kernel(
                     scale=1.0,
                 )
 
-        def stage_d(pair, quarter):
-            if quarter == 0:
-                att_turned[pair] = ring.tile([P, H_BLOCKS, 2 * P], F32, name="att_turned", tag="att_turned", bufs=2)
-            two_blocks(att_turned[pair], 2 * quarter, w_o_codes, PLANE_O, v_codes, v_scales, b_o_cols, pair)
-
         liq_b = {}
 
         def stage_l(pair, a):
@@ -352,29 +359,6 @@ def tile_advancedliquidneuralnetwork_pb_kernel(
 
         def stage_xq(pair):
             quantise(grouped_x[pair], x_codes[:, 0, pair_tokens(pair)], x_scales[:, 0, pair_tokens(pair)])
-
-        def stage_e(pair, quarter):
-            a, half = quarter // H_BANKS, quarter % H_BANKS
-            i = 2 * pair + a
-            if half == 0:
-                resid[i] = ring.tile([P, H], F32, name="resid", tag="resid", bufs=4)
-                sums[i] = stat.tile([P, H_BANKS], F32, name="sums", tag="sums")
-            acc = bank("b")
-            for q in range(BANK // P):
-                nc.tensor.transpose(
-                    acc[:, q * P : (q + 1) * P],
-                    att_turned[pair][:, half * (BANK // P) + q, a * P : (a + 1) * P],
-                    ident_f32[:],
-                )
-            nc.vector.scalar_tensor_tensor(
-                out=resid[i][:, columns(half)],
-                in0=acc[:],
-                scalar=1.0,
-                in1=liq_sb[:, i, columns(half)],
-                op0=ALU.mult,
-                op1=ALU.add,
-                accum_out=sums[i][:, half : half + 1],
-            )
 
         def stage_n(pair, a):
             i = 2 * pair + a
@@ -442,6 +426,8 @@ def tile_advancedliquidneuralnetwork_pb_kernel(
                 work[i] = ring.tile([P, H], F32, name="work", tag="work", bufs=WORK_BUFS)
             cols = columns(half)
             acc = bank("b")
+            if pair in CLOCK_PAIRS:
+                nc.tensor.matmul(out=acc[:], lhsT=minus_ident[:], rhs=h_sb[:, i, cols], start=True, stop=True)
             nc.tensor.matmul(out=acc[:], lhsT=minus_ident[:], rhs=h_sb[:, i, cols], start=True, stop=False)
             for b in range(4):
                 nc.tensor.matmul(
@@ -457,17 +443,13 @@ def tile_advancedliquidneuralnetwork_pb_kernel(
             engine.tensor_tensor(out=work[i][:, cols], in0=work[i][:, cols], in1=h_sb[:, i, cols], op=ALU.add)
             nc.sync.dma_start(out=out_rows[:, i, cols], in_=work[i][:, cols])
 
-        for k in range(WARM_UP_MATMULS):
-            unread_bank = bank("b")
-            nc.tensor.matmul(out=unread_bank[:], lhsT=ident_bf[:], rhs=liq_sb[:, 0, columns(k % 2)], start=True, stop=True)
-
         def due(first, parts=4, every=1):
             return [
                 (k, n) for k in range(PAIRS) for n in range(parts) if first + 4 * k + every * n == slot
             ]
 
         with tc.manual_schedule(engines={mybir.EngineType.PE}):
-            for slot in range(14 + 4 * PAIRS):
+            for slot in range(15 + 4 * PAIRS):
                 for k, n in due(0):
                     stage_b(k, n)
                 for k, n in due(6):
@@ -481,12 +463,12 @@ def tile_advancedliquidneuralnetwork_pb_kernel(
                 if slot == 4:
                     spread_rate(0)
                     spread_rate(1)
-                for k, n in due(12):
+                for k, n in due(13):
                     stage_f(k, n)
                 for k, n in due(2, 2, 2):
                     stage_c(k, n)
                     stage_cq(k, n)
-                for k, n in due(14):
+                for k, n in due(15):
                     stage_h(k, n)
                 for k, n in due(-3, 2):
                     if k > 0:

@@ -135,8 +135,8 @@ def tile_advancedliquidneuralnetwork_pb_kernel(
 
         every = slice(0, H)
         load_tokens(liq_sb, liq_rows, 0, 1)
-        load_codes(W_v_words, w_v_codes, slice(0, BANK))
         load_scales(W_v_scales, PLANE_V)
+        load_codes(W_v_words, w_v_codes, slice(0, BANK))
         load_vector(first_rows, 0, b_v)
         load_tokens(liq_sb, liq_rows, 1, 1)
         load_codes(W_v_words, w_v_codes, slice(BANK, H))
@@ -449,26 +449,26 @@ def tile_advancedliquidneuralnetwork_pb_kernel(
             ]
 
         with tc.manual_schedule(engines={mybir.EngineType.PE}):
-            for slot in range(15 + 4 * PAIRS):
+            for slot in range(19 + 4 * PAIRS):
                 for k, n in due(0):
                     stage_b(k, n)
                 for k, n in due(6):
                     stage_x(k, n)
-                for k, n in due(6):
+                for k, n in due(8):
                     stage_t(k, n)
-                for k, n in due(8, 1):
-                    stage_n(k, 0)
                 for k, n in due(10, 1):
+                    stage_n(k, 0)
+                for k, n in due(12, 1):
                     stage_n(k, 1)
                 if slot == 4:
                     spread_rate(0)
                     spread_rate(1)
-                for k, n in due(13):
+                for k, n in due(16):
                     stage_f(k, n)
-                for k, n in due(2, 2, 2):
+                for k, n in due(3, 2, 2):
                     stage_c(k, n)
                     stage_cq(k, n)
-                for k, n in due(15):
+                for k, n in due(19):
                     stage_h(k, n)
                 for k, n in due(-3, 2):
                     if k > 0:

@@ -33,7 +33,6 @@ PSUM_BANKS = {"s": 3, "b": 5}
 PAIRS = TILES // 2
 LIQ_COPIES_ON_VECTOR = ()
 X_COPIES_ON_VECTOR = ()
-V_COPIES_ON_VECTOR = ()
 TOKEN_PAIRS = (0, 1, 2, 3)
 LIQ_B_ON_GPSIMD = ()
 H_ON_GPSIMD = (4,5)
@@ -78,6 +77,8 @@ def tile_advancedliquidneuralnetwork_pb_kernel(
         h_sb = keep.tile([P, TILES, H], BF16)
         w_in_codes = keep.tile([P, 1, H], U32, align_bytes=64)
         w_v_codes = keep.tile([P, H_GROUPS, H], U32, align_bytes=64)
+        w_v_sorted = keep.tile([P, H_GROUPS, H], U32, align_bytes=64)
+        w_v_sorted_scales = keep.tile([P, H_GROUPS, H], U8, align_bytes=64)
         w_o_codes = keep.tile([P, H_GROUPS, H], U32, align_bytes=64)
         w_scales = keep.tile([P, PLANES, H], U8, align_bytes=64)
         liq_codes = keep.tile([P, TILES, H_GROUPS * P], U32, align_bytes=64)
@@ -87,7 +88,7 @@ def tile_advancedliquidneuralnetwork_pb_kernel(
         x_codes = keep.tile([P, 1, B], U32, align_bytes=64)
         x_scales = keep.tile([P, 1, B], U8, align_bytes=64)
         xin_turned = keep.tile([P, H_BLOCKS, B], F32)
-        first_rows = keep.tile([P, P], BF16)
+        b_v_cols = keep.tile([P, H_GROUPS, PACK], BF16)
         vec_rows = keep.tile([P, P], BF16)
         table_loaded = keep.tile([P, 1], F32)
         ident_bf = keep.tile([P, P], BF16)
@@ -102,7 +103,6 @@ def tile_advancedliquidneuralnetwork_pb_kernel(
 
         nc.vector.memset(minus_half[:], -0.5)
         nc.vector.memset(w_scales[:, PLANE_V : PLANE_V + H_GROUPS, :].bitcast(I32), 0)
-        nc.vector.memset(first_rows[:], 0.0)
         nc.vector.memset(vec_rows[:], 0.0)
         nc.vector.memset(w_scales[:, PLANE_O : PLANE_O + H_GROUPS, :].bitcast(I32), 0)
         nc.vector.memset(w_scales[:, PLANE_IN : PLANE_IN + 1, :].bitcast(I32), 0)
@@ -137,7 +137,7 @@ def tile_advancedliquidneuralnetwork_pb_kernel(
         load_tokens(liq_sb, liq_rows, 0, 1)
         load_scales(W_v_scales, PLANE_V)
         load_codes(W_v_words, w_v_codes, slice(0, BANK))
-        load_vector(first_rows, 0, b_v)
+        nc.sync.dma_start(out=b_v_cols[:], in_=b_v.rearrange("(g p t) -> p g t", g=H_GROUPS, t=PACK))
         load_tokens(liq_sb, liq_rows, 1, 1)
         load_codes(W_v_words, w_v_codes, slice(BANK, H))
         load_vector(vec_rows, ROW_B_O, b_o)
@@ -164,7 +164,7 @@ def tile_advancedliquidneuralnetwork_pb_kernel(
         def columns(half):
             return slice(half * BANK, (half + 1) * BANK)
 
-        def spread_input_vector(rows_tile, row, name):
+        def spread_input_vector(row, name):
             everywhere = keep.tile([P, H], BF16, name=name)
             for half in range(H_BANKS):
                 rows = bank("s")
@@ -173,7 +173,7 @@ def tile_advancedliquidneuralnetwork_pb_kernel(
                     nc.tensor.matmul(
                         out=rows[:, q * P : (q + 1) * P],
                         lhsT=ident_bf[:, r : r + 1].to_broadcast([P, P]),
-                        rhs=rows_tile[:],
+                        rhs=vec_rows[:],
                         start=True,
                         stop=True,
                     )
@@ -189,15 +189,12 @@ def tile_advancedliquidneuralnetwork_pb_kernel(
                 )
             nc.scalar.copy(out=rate_rows[:, columns(half)], in_=rows[:])
 
-        def turn(first, second, tag, sorted_words=False, on_vector=False):
+        def turn(first, second, tag, on_vector=False):
             turned = psum.tile([P, 2, 2, P], F32, name="turned", tag="s", bufs=PSUM_BANKS["s"])
             for a, rows in enumerate((first, second)):
                 words = rows.bitcast(F32)
                 for u in range(2):
-                    if sorted_words:
-                        nc.tensor.transpose(turned[:, a, u, :], words[:, u * P : (u + 1) * P], ident_f32[:])
-                    else:
-                        nc.tensor.transpose(turned[:, a, u, :], words[:, u : K_PASS // 2 : 2], ident_f32[:])
+                    nc.tensor.transpose(turned[:, a, u, :], words[:, u : K_PASS // 2 : 2], ident_f32[:])
             grouped = ring.tile([P, 2, P, PACK], BF16, name=tag, tag=tag, bufs=3, align_bytes=64)
             if on_vector:
                 nc.vector.tensor_copy(out=grouped[:].bitcast(F32), in_=turned[:].rearrange("p a u r -> p a r u"))
@@ -223,12 +220,11 @@ def tile_advancedliquidneuralnetwork_pb_kernel(
             nc.tensor.matmul(out=unread_bank[:, :P], lhsT=ident_bf[:], rhs=ident_bf[:], start=True, stop=True)
         grouped_liq[0] = turn_liq(0)
         quantise_liq(0)
-        b_v_rows = spread_input_vector(first_rows, 0, "b_v_rows")
         grouped_liq[1] = turn_liq(1)
         quantise_liq(1)
 
         if TOKEN_PAIRS:
-            b_o_rows = spread_input_vector(vec_rows, ROW_B_O, "b_o_rows")
+            b_o_rows = spread_input_vector(ROW_B_O, "b_o_rows")
 
         vec_ps = psum.tile([P, P], BF16, name="vec_ps", tag="s", bufs=PSUM_BANKS["s"])
         nc.tensor.transpose(vec_ps[:], vec_rows[:], ident_bf[:])
@@ -250,7 +246,7 @@ def tile_advancedliquidneuralnetwork_pb_kernel(
             return slice(2 * pair * P, (2 * pair + 2) * P)
 
         grouped_x, grouped_v = {}, {}
-        v_bf, resid, sums, neg_mean, rstd = {}, {}, {}, {}, {}
+        resid, sums, neg_mean, rstd = {}, {}, {}, {}
         att_turned, turned_h, work = {}, {}, {}
 
         def stage_a(pair, a):
@@ -259,35 +255,50 @@ def tile_advancedliquidneuralnetwork_pb_kernel(
         def stage_aq(pair, a):
             quantise_liq(2 * pair + a)
 
+        def sort_columns(group_of_v):
+            cols = columns(group_of_v)
+            for g in range(H_GROUPS):
+                nc.vector.tensor_copy(
+                    out=w_v_sorted[:, g, cols].bitcast(I32).rearrange("p (t m) -> p t m", t=PACK),
+                    in_=w_v_codes[:, g, cols].bitcast(I32).rearrange("p (m t) -> p t m", t=PACK),
+                )
+                nc.vector.tensor_copy(
+                    out=w_v_sorted_scales[:, g, cols].rearrange("p (t m) -> p t m", t=PACK),
+                    in_=w_scales[:, PLANE_V + g, cols].rearrange("p (m t) -> p t m", t=PACK),
+                )
+
         def stage_b(pair, quarter):
             i, half = 2 * pair + quarter % 2, quarter // 2
-            if half == 0:
-                v_bf[i] = ring.tile([P, H], BF16, name="v_bf", tag="v_bf", bufs=4)
-            acc = bank("b")
-            for g in range(H_GROUPS):
-                group = slice(g * P, (g + 1) * P)
-                nc.tensor.matmul_mx(
-                    out=acc[:],
-                    lhsT=liq_codes[:, i, group].bitcast(FP8X4),
-                    lhsT_scale=liq_scales[:, i, group],
-                    rhs=w_v_codes[:, g, columns(half)].bitcast(FP8X4),
-                    rhs_scale=w_scales[:, PLANE_V + g, columns(half)],
-                    start=(g == 0),
-                    stop=(g == H_GROUPS - 1),
-                )
+            acc = psum.tile([P, PACK, P], F32, name="turned_v", tag="b", bufs=PSUM_BANKS["b"])
+            for t in range(PACK):
+                features = slice(half * K_PASS + t * P, half * K_PASS + (t + 1) * P)
+                for g in range(H_GROUPS):
+                    group = slice(g * P, (g + 1) * P)
+                    nc.tensor.matmul_mx(
+                        out=acc[:, t, :],
+                        lhsT=w_v_sorted[:, g, features].bitcast(FP8X4),
+                        lhsT_scale=w_v_sorted_scales[:, g, features],
+                        rhs=liq_codes[:, i, group].bitcast(FP8X4),
+                        rhs_scale=liq_scales[:, i, group],
+                        start=(g == 0),
+                        stop=(g == H_GROUPS - 1),
+                    )
+            grouped_v[i, half] = ring.tile([P, P, PACK], BF16, name="grouped_v", tag="grouped_v", bufs=4, align_bytes=64)
             nc.vector.tensor_tensor(
-                out=v_bf[i][:, columns(half)].rearrange("r (u p e) -> r u p e", u=2, e=2),
-                in0=acc[:].rearrange("r (p u e) -> r u p e", u=2, e=2),
-                in1=b_v_rows[:, columns(half)].rearrange("r (p u e) -> r u p e", u=2, e=2),
+                out=grouped_v[i, half][:],
+                in0=acc[:].rearrange("p t n -> p n t"),
+                in1=b_v_cols[:, half, :].unsqueeze(1).to_broadcast([P, P, PACK]),
                 op=ALU.add,
             )
 
-        def stage_c(pair, g):
-            features = slice(g * K_PASS, (g + 1) * K_PASS)
-            grouped_v[pair, g] = turn(v_bf[2 * pair][:, features], v_bf[2 * pair + 1][:, features], "grouped_v", sorted_words=True, on_vector=pair in V_COPIES_ON_VECTOR)
-
-        def stage_cq(pair, g):
-            quantise(grouped_v[pair, g], v_codes[:, g, pair_tokens(pair)], v_scales[:, g, pair_tokens(pair)])
+        def stage_bq(pair, quarter):
+            i, half = 2 * pair + quarter % 2, quarter // 2
+            tokens = slice(i * P, (i + 1) * P)
+            nc.vector.quantize_mx(
+                out=v_codes[:, half, tokens].bitcast(FP8X4),
+                scales=v_scales[:, half, tokens],
+                in_=grouped_v[i, half][:].rearrange("p n t -> p (n t)"),
+            )
 
         def two_blocks(dst, first, w_codes, plane, codes, scales, bias_cols, pair):
             groups = codes.shape[1]
@@ -445,30 +456,33 @@ def tile_advancedliquidneuralnetwork_pb_kernel(
 
         def due(first, parts=4, every=1):
             return [
-                (k, n) for k in range(PAIRS) for n in range(parts) if first + 4 * k + every * n == slot
+                (k, n) for k in range(PAIRS) for n in range(parts) if max(first + 4 * k + every * n, 0) == slot
             ]
 
+        sort_columns(0)
         with tc.manual_schedule(engines={mybir.EngineType.PE}):
-            for slot in range(19 + 4 * PAIRS):
+            for slot in range(15 + 4 * PAIRS):
                 for k, n in due(0):
                     stage_b(k, n)
+                    stage_bq(k, n)
+                if slot == 0:
+                    sort_columns(1)
                 for k, n in due(6):
                     stage_x(k, n)
-                for k, n in due(8):
+                for k, n in due(0, 2):
+                    stage_l(k, n)
+                for k, n in due(4):
                     stage_t(k, n)
-                for k, n in due(10, 1):
+                for k, n in due(5, 1):
                     stage_n(k, 0)
-                for k, n in due(12, 1):
+                for k, n in due(7, 1):
                     stage_n(k, 1)
                 if slot == 4:
                     spread_rate(0)
                     spread_rate(1)
-                for k, n in due(16):
+                for k, n in due(12):
                     stage_f(k, n)
-                for k, n in due(3, 2, 2):
-                    stage_c(k, n)
-                    stage_cq(k, n)
-                for k, n in due(19):
+                for k, n in due(15):
                     stage_h(k, n)
                 for k, n in due(-3, 2):
                     if k > 0:
@@ -477,5 +491,3 @@ def tile_advancedliquidneuralnetwork_pb_kernel(
                 for k, n in due(3, 1):
                     stage_xt(k)
                     stage_xq(k)
-                for k, n in due(1, 2):
-                    stage_l(k, n)

@@ -460,34 +460,33 @@ def tile_advancedliquidneuralnetwork_pb_kernel(
             ]
 
         sort_columns(0)
-        with tc.manual_schedule(engines={mybir.EngineType.PE}):
-            for slot in range(15 + 4 * PAIRS):
-                for k, n in due(0):
-                    stage_b(k, n)
-                    stage_bq(k, n)
-                if slot == 0:
-                    sort_columns(1)
-                for k, n in due(6):
-                    stage_x(k, n)
-                for k, n in due(0, 2):
-                    stage_l(k, n)
-                for k, n in due(4):
-                    stage_t(k, n)
-                for k, n in due(5, 1):
-                    stage_n(k, 0)
-                for k, n in due(7, 1):
-                    stage_n(k, 1)
-                if slot == 4:
-                    spread_rate(0)
-                    spread_rate(1)
-                for k, n in due(12):
-                    stage_f(k, n)
-                for k, n in due(15):
-                    stage_h(k, n)
-                for k, n in due(-3, 2):
-                    if k > 0:
-                        stage_a(k, n)
-                        stage_aq(k, n)
-                for k, n in due(3, 1):
-                    stage_xt(k)
-                    stage_xq(k)
+        for slot in range(15 + 4 * PAIRS):
+            for k, n in due(0):
+                stage_b(k, n)
+                stage_bq(k, n)
+            if slot == 0:
+                sort_columns(1)
+            for k, n in due(6):
+                stage_x(k, n)
+            for k, n in due(0, 2):
+                stage_l(k, n)
+            for k, n in due(4):
+                stage_t(k, n)
+            for k, n in due(5, 1):
+                stage_n(k, 0)
+            for k, n in due(7, 1):
+                stage_n(k, 1)
+            if slot == 4:
+                spread_rate(0)
+                spread_rate(1)
+            for k, n in due(12):
+                stage_f(k, n)
+            for k, n in due(15):
+                stage_h(k, n)
+            for k, n in due(-3, 2):
+                if k > 0:
+                    stage_a(k, n)
+                    stage_aq(k, n)
+            for k, n in due(3, 1):
+                stage_xt(k)
+                stage_xq(k)

@@ -29,16 +29,15 @@ FLOPS = 2 * B * (IN * H + H * H + H * H)
 PLANE_IN, PLANE_V, PLANE_O = 0, 1, 3
 PLANES = 5
 WORK_BUFS = 4
+CELL_BUFS = 3
+MEAN_ON_GPSIMD = ()
 PSUM_BANKS = {"s": 3, "b": 5}
 PAIRS = TILES // 2
 LIQ_COPIES_ON_VECTOR = ()
 X_COPIES_ON_VECTOR = ()
-TOKEN_PAIRS = (0, 1, 2, 3)
-LIQ_B_ON_GPSIMD = ()
-H_ON_GPSIMD = (4,5)
+H_ON_GPSIMD = (0, 1, 4, 5)
 CLOCK_PAIRS = (2, 3)
 NORM_ON_VECTOR = (-1,)
-LIQ_B_BUFS = max(1, 2 * len(TOKEN_PAIRS))
 WARM_UP_MATMULS = 12
 ROW_TAU, ROW_BETA, ROW_B_IN, ROW_G, ROW_B_O = 0, 1, 2, 3, 4
 
@@ -76,9 +75,9 @@ def tile_advancedliquidneuralnetwork_pb_kernel(
         x_sb = keep.tile([P, TILES, IN], BF16)
         h_sb = keep.tile([P, TILES, H], BF16)
         w_in_codes = keep.tile([P, 1, H], U32, align_bytes=64)
-        w_v_codes = keep.tile([P, H_GROUPS, H], U32, align_bytes=64)
-        w_v_sorted = keep.tile([P, H_GROUPS, H], U32, align_bytes=64)
-        w_v_sorted_scales = keep.tile([P, H_GROUPS, H], U8, align_bytes=64)
+        w_v_codes = keep.tile([P, H_BANKS, H_GROUPS, BANK], U32, align_bytes=64)
+        w_v_sorted = keep.tile([P, H_BANKS, H_GROUPS, BANK], U32, align_bytes=64)
+        w_v_sorted_scales = keep.tile([P, H_BANKS, H_GROUPS, BANK], U8, align_bytes=64)
         w_o_codes = keep.tile([P, H_GROUPS, H], U32, align_bytes=64)
         w_scales = keep.tile([P, PLANES, H], U8, align_bytes=64)
         liq_codes = keep.tile([P, TILES, H_GROUPS * P], U32, align_bytes=64)
@@ -87,7 +86,6 @@ def tile_advancedliquidneuralnetwork_pb_kernel(
         v_scales = keep.tile([P, H_GROUPS, B], U8, align_bytes=64)
         x_codes = keep.tile([P, 1, B], U32, align_bytes=64)
         x_scales = keep.tile([P, 1, B], U8, align_bytes=64)
-        xin_turned = keep.tile([P, H_BLOCKS, B], F32)
         b_v_cols = keep.tile([P, H_GROUPS, PACK], BF16)
         vec_rows = keep.tile([P, P], BF16)
         table_loaded = keep.tile([P, 1], F32)
@@ -103,11 +101,11 @@ def tile_advancedliquidneuralnetwork_pb_kernel(
 
         nc.vector.memset(minus_half[:], -0.5)
         nc.vector.memset(w_scales[:, PLANE_V : PLANE_V + H_GROUPS, :].bitcast(I32), 0)
-        nc.vector.memset(vec_rows[:], 0.0)
-        nc.vector.memset(w_scales[:, PLANE_O : PLANE_O + H_GROUPS, :].bitcast(I32), 0)
-        nc.vector.memset(w_scales[:, PLANE_IN : PLANE_IN + 1, :].bitcast(I32), 0)
         make_identity(nc, ident_bf[:])
         make_identity(nc, ident_f32[:])
+        nc.gpsimd.memset(vec_rows[:], 0.0)
+        nc.gpsimd.memset(w_scales[:, PLANE_O : PLANE_O + H_GROUPS, :].bitcast(I32), 0)
+        nc.gpsimd.memset(w_scales[:, PLANE_IN : PLANE_IN + 1, :].bitcast(I32), 0)
         nc.scalar.activation(out=table_loaded[:], in_=minus_half[:], func=ACT.Tanh)
 
         def load_tokens(dst, src, first, count):
@@ -121,11 +119,17 @@ def tile_advancedliquidneuralnetwork_pb_kernel(
                     in_=scales[:, 4 * quad : 4 * quad + 4, :].bitcast(I32).rearrange("g r n -> r g n"),
                 )
 
-        def load_codes(words, codes, cols):
+        def load_half_of_w_v(half):
+            for g in range(H_GROUPS):
+                nc.sync.dma_start(
+                    out=w_v_codes[:, half, g, :].bitcast(I32),
+                    in_=W_v_words[g, :, half * BANK : (half + 1) * BANK, :].rearrange("p n t -> p (n t)").bitcast(I32),
+                )
+
+        def load_codes(words, codes):
             for g in range(words.shape[0]):
                 nc.sync.dma_start(
-                    out=codes[:, g, cols].bitcast(I32),
-                    in_=words[g, :, cols, :].rearrange("p n t -> p (n t)").bitcast(I32),
+                    out=codes[:, g, :].bitcast(I32), in_=words[g].rearrange("p n t -> p (n t)").bitcast(I32)
                 )
 
         def load_vector(rows, row, vec):
@@ -133,13 +137,12 @@ def tile_advancedliquidneuralnetwork_pb_kernel(
                 out=rows[H_BLOCKS * row : H_BLOCKS * (row + 1), :], in_=vec.rearrange("(m c) -> m c", c=P)
             )
 
-        every = slice(0, H)
         load_tokens(liq_sb, liq_rows, 0, 1)
         load_scales(W_v_scales, PLANE_V)
-        load_codes(W_v_words, w_v_codes, slice(0, BANK))
+        load_half_of_w_v(0)
         nc.sync.dma_start(out=b_v_cols[:], in_=b_v.rearrange("(g p t) -> p g t", g=H_GROUPS, t=PACK))
         load_tokens(liq_sb, liq_rows, 1, 1)
-        load_codes(W_v_words, w_v_codes, slice(BANK, H))
+        load_half_of_w_v(1)
         load_vector(vec_rows, ROW_B_O, b_o)
         load_vector(vec_rows, ROW_TAU, tau)
         load_vector(vec_rows, ROW_G, g_att)
@@ -147,10 +150,10 @@ def tile_advancedliquidneuralnetwork_pb_kernel(
         load_vector(vec_rows, ROW_B_IN, b_in)
         load_tokens(liq_sb, liq_rows, 2, 2)
         load_scales(W_o_scales, PLANE_O)
-        load_codes(W_o_words, w_o_codes, every)
+        load_codes(W_o_words, w_o_codes)
         load_tokens(x_sb, x_rows, 0, 4)
         load_scales(W_in_scales, PLANE_IN)
-        load_codes(W_in_words, w_in_codes, every)
+        load_codes(W_in_words, w_in_codes)
         load_tokens(liq_sb, liq_rows, 4, 2)
         load_tokens(h_sb, h_rows, 0, 2)
         load_tokens(liq_sb, liq_rows, 6, 2)
@@ -219,12 +222,9 @@ def tile_advancedliquidneuralnetwork_pb_kernel(
             unread_bank = bank("b")
             nc.tensor.matmul(out=unread_bank[:, :P], lhsT=ident_bf[:], rhs=ident_bf[:], start=True, stop=True)
         grouped_liq[0] = turn_liq(0)
-        quantise_liq(0)
         grouped_liq[1] = turn_liq(1)
-        quantise_liq(1)
 
-        if TOKEN_PAIRS:
-            b_o_rows = spread_input_vector(ROW_B_O, "b_o_rows")
+        b_o_rows = spread_input_vector(ROW_B_O, "b_o_rows")
 
         vec_ps = psum.tile([P, P], BF16, name="vec_ps", tag="s", bufs=PSUM_BANKS["s"])
         nc.tensor.transpose(vec_ps[:], vec_rows[:], ident_bf[:])
@@ -234,18 +234,21 @@ def tile_advancedliquidneuralnetwork_pb_kernel(
 
         shift_cols = keep.tile([P, H_BLOCKS], F32)
         rate_cols = keep.tile([P, H_BLOCKS], F32)
-        nc.vector.tensor_tensor(
+        nc.gpsimd.tensor_tensor(
             out=shift_cols[:], in0=block_cols(vec_cols, ROW_BETA), in1=block_cols(vec_cols, ROW_B_IN), op=ALU.add
         )
         nc.vector.tensor_scalar_add(out=rate_cols[:], in0=block_cols(vec_cols, ROW_TAU), scalar1=TAU_EPS)
         nc.vector.reciprocal(out=rate_cols[:], in_=rate_cols[:])
         minus_ident = keep.tile([P, P], BF16)
-        nc.vector.tensor_scalar_mul(out=minus_ident[:], in0=ident_bf[:], scalar1=-1.0)
+        nc.gpsimd.tensor_scalar(
+            out=minus_ident[:], in0=ident_bf[:], scalar1=-1.0, scalar2=0.0, op0=ALU.mult, op1=ALU.add
+        )
 
         def pair_tokens(pair):
             return slice(2 * pair * P, (2 * pair + 2) * P)
 
         grouped_x, grouped_v = {}, {}
+        cell = {}
         resid, sums, neg_mean, rstd = {}, {}, {}, {}
         att_turned, turned_h, work = {}, {}, {}
 
@@ -257,85 +260,58 @@ def tile_advancedliquidneuralnetwork_pb_kernel(
 
         def sort_columns(group_of_v):
             cols = columns(group_of_v)
-            for g in range(H_GROUPS):
-                nc.vector.tensor_copy(
-                    out=w_v_sorted[:, g, cols].bitcast(I32).rearrange("p (t m) -> p t m", t=PACK),
-                    in_=w_v_codes[:, g, cols].bitcast(I32).rearrange("p (m t) -> p t m", t=PACK),
-                )
-                nc.vector.tensor_copy(
-                    out=w_v_sorted_scales[:, g, cols].rearrange("p (t m) -> p t m", t=PACK),
-                    in_=w_scales[:, PLANE_V + g, cols].rearrange("p (m t) -> p t m", t=PACK),
-                )
+            nc.vector.tensor_copy(
+                out=w_v_sorted[:, group_of_v, :, :].bitcast(I32).rearrange("p g (t m) -> p g t m", t=PACK),
+                in_=w_v_codes[:, group_of_v, :, :].bitcast(I32).rearrange("p g (m t) -> p g t m", t=PACK),
+            )
+            nc.gpsimd.tensor_copy(
+                out=w_v_sorted_scales[:, group_of_v, :, :].rearrange("p g (t m) -> p g t m", t=PACK),
+                in_=w_scales[:, PLANE_V : PLANE_V + H_GROUPS, cols].rearrange("p g (m t) -> p g t m", t=PACK),
+            )
 
         def stage_b(pair, quarter):
             i, half = 2 * pair + quarter % 2, quarter // 2
             acc = psum.tile([P, PACK, P], F32, name="turned_v", tag="b", bufs=PSUM_BANKS["b"])
             for t in range(PACK):
-                features = slice(half * K_PASS + t * P, half * K_PASS + (t + 1) * P)
+                features = slice(t * P, (t + 1) * P)
                 for g in range(H_GROUPS):
                     group = slice(g * P, (g + 1) * P)
                     nc.tensor.matmul_mx(
                         out=acc[:, t, :],
-                        lhsT=w_v_sorted[:, g, features].bitcast(FP8X4),
-                        lhsT_scale=w_v_sorted_scales[:, g, features],
+                        lhsT=w_v_sorted[:, half, g, features].bitcast(FP8X4),
+                        lhsT_scale=w_v_sorted_scales[:, half, g, features],
                         rhs=liq_codes[:, i, group].bitcast(FP8X4),
                         rhs_scale=liq_scales[:, i, group],
                         start=(g == 0),
                         stop=(g == H_GROUPS - 1),
                     )
-            grouped_v[i, half] = ring.tile([P, P, PACK], BF16, name="grouped_v", tag="grouped_v", bufs=4, align_bytes=64)
+            if i % 2 == 0:
+                grouped_v[pair, half] = ring.tile([P, 2, P, PACK], BF16, name="grouped_v", tag="grouped_v", bufs=3, align_bytes=64)
             nc.vector.tensor_tensor(
-                out=grouped_v[i, half][:],
+                out=grouped_v[pair, half][:, i % 2, :, :],
                 in0=acc[:].rearrange("p t n -> p n t"),
                 in1=b_v_cols[:, half, :].unsqueeze(1).to_broadcast([P, P, PACK]),
                 op=ALU.add,
             )
 
-        def stage_bq(pair, quarter):
-            i, half = 2 * pair + quarter % 2, quarter // 2
-            tokens = slice(i * P, (i + 1) * P)
-            nc.vector.quantize_mx(
-                out=v_codes[:, half, tokens].bitcast(FP8X4),
-                scales=v_scales[:, half, tokens],
-                in_=grouped_v[i, half][:].rearrange("p n t -> p (n t)"),
-            )
-
-        def two_blocks(dst, first, w_codes, plane, codes, scales, bias_cols, pair):
-            groups = codes.shape[1]
-            acc = bank("s")
-            for a in range(2):
-                features = slice((first + a) * P, (first + a + 1) * P)
-                for g in range(groups):
-                    nc.tensor.matmul_mx(
-                        out=acc[:, 2 * a * P : (2 * a + 2) * P],
-                        lhsT=w_codes[:, g, features].bitcast(FP8X4),
-                        lhsT_scale=w_scales[:, plane + g, features],
-                        rhs=codes[:, g, pair_tokens(pair)].bitcast(FP8X4),
-                        rhs_scale=scales[:, g, pair_tokens(pair)],
-                        start=(g == 0),
-                        stop=(g == groups - 1),
-                    )
-            for a in range(2):
-                nc.scalar.activation(
-                    out=dst[:, first + a, :],
-                    in_=acc[:, 2 * a * P : (2 * a + 2) * P],
-                    func=ACT.Identity,
-                    bias=bias_cols[:, first + a : first + a + 1],
-                    scale=1.0,
-                )
+        def stage_bq(pair, half):
+            quantise(grouped_v[pair, half], v_codes[:, half, pair_tokens(pair)], v_scales[:, half, pair_tokens(pair)])
 
         liq_b = {}
 
-        def stage_l(pair, a):
-            i = 2 * pair + a
-            liq_b[i] = ring.tile([P, H], F32, name="liq_b", tag="liq_b", bufs=LIQ_B_BUFS)
-            engine = nc.gpsimd if i in LIQ_B_ON_GPSIMD else nc.vector
-            engine.tensor_tensor(out=liq_b[i][:], in0=liq_sb[:, i, :], in1=b_o_rows[:], op=ALU.add)
+        def stage_l(pair):
+            liq_b[pair] = ring.tile([P, 2, H], F32, name="liq_b", tag="liq_b", bufs=PAIRS)
+            nc.vector.tensor_tensor(
+                out=liq_b[pair][:],
+                in0=liq_sb[:, 2 * pair : 2 * pair + 2, :],
+                in1=b_o_rows[:].unsqueeze(1).to_broadcast([P, 2, H]),
+                op=ALU.add,
+            )
 
         def stage_t(pair, quarter):
             i, half = 2 * pair + quarter // H_BANKS, quarter % H_BANKS
             if half == 0:
-                resid[i] = liq_b[i]
+                resid[i] = liq_b[pair][:, i % 2, :]
                 sums[i] = stat.tile([P, H_BANKS], F32, name="sums", tag="sums")
             acc = bank("b")
             tokens = slice(i * P, (i + 1) * P)
@@ -353,17 +329,11 @@ def tile_advancedliquidneuralnetwork_pb_kernel(
                 out=resid[i][:, columns(half)],
                 in0=acc[:],
                 scalar=1.0,
-                in1=liq_b[i][:, columns(half)],
+                in1=resid[i][:, columns(half)],
                 op0=ALU.mult,
                 op1=ALU.add,
                 accum_out=sums[i][:, half : half + 1],
             )
-
-        def cell(pair):
-            return xin_turned[:, :, pair_tokens(pair)]
-
-        def stage_x(pair, quarter):
-            two_blocks(cell(pair), 2 * quarter, w_in_codes, PLANE_IN, x_codes, x_scales, shift_cols, pair)
 
         def stage_xt(pair):
             grouped_x[pair] = turn(x_sb[:, 2 * pair, :], x_sb[:, 2 * pair + 1, :], "grouped_x", on_vector=pair in X_COPIES_ON_VECTOR)
@@ -374,7 +344,7 @@ def tile_advancedliquidneuralnetwork_pb_kernel(
         def stage_n(pair, a):
             i = 2 * pair + a
             neg_mean[i] = stat.tile([P, 1], F32, name="neg_mean", tag="neg_mean")
-            nc.vector.tensor_scalar(
+            (nc.gpsimd if i in MEAN_ON_GPSIMD else nc.vector).tensor_scalar(
                 out=neg_mean[i][:],
                 in0=sums[i][:, 0:1],
                 scalar1=sums[i][:, 1:2],
@@ -385,7 +355,7 @@ def tile_advancedliquidneuralnetwork_pb_kernel(
             squares = ring.tile([P, H], BF16, name="squares", tag="squares")
             sum_sq = stat.tile([P, 1], F32, name="sum_sq", tag="sum_sq")
             nc.scalar.activation(
-                out=squares[:], in_=resid[i][:], func=ACT.Square, bias=neg_mean[i][:], scale=1.0, accum_out=sum_sq[:]
+                out=squares[:], in_=resid[i], func=ACT.Square, bias=neg_mean[i][:], scale=1.0, accum_out=sum_sq[:]
             )
             var_eps = stat.tile([P, 1], F32, name="var_eps", tag="var_eps")
             nc.gpsimd.tensor_scalar(
@@ -395,8 +365,8 @@ def tile_advancedliquidneuralnetwork_pb_kernel(
             nc.gpsimd.tensor_tensor(out=rstd[i][:], in0=var_eps[:], in1=minus_half[:], op=ALU.pow)
             if i in NORM_ON_VECTOR:
                 nc.vector.tensor_scalar(
-                    out=resid[i][:],
-                    in0=resid[i][:],
+                    out=resid[i],
+                    in0=resid[i],
                     scalar1=neg_mean[i][:],
                     scalar2=rstd[i][:],
                     op0=ALU.add,
@@ -406,11 +376,14 @@ def tile_advancedliquidneuralnetwork_pb_kernel(
                 shift = stat.tile([P, 1], F32, name="shift", tag="shift")
                 nc.gpsimd.tensor_tensor(out=shift[:], in0=neg_mean[i][:], in1=rstd[i][:], op=ALU.mult)
                 nc.scalar.activation(
-                    out=resid[i][:], in_=resid[i][:], func=ACT.Identity, bias=shift[:], scale=rstd[i][:]
+                    out=resid[i], in_=resid[i], func=ACT.Identity, bias=shift[:], scale=rstd[i][:]
                 )
 
         def stage_f(pair, quarter):
-            acc = psum.tile([P, 2, 2 * P], F32, name="turned_q", tag="b", bufs=PSUM_BANKS["b"])
+            if quarter == 0:
+                cell[pair] = ring.tile([P, H_BLOCKS, 2 * P], F32, name="cell", tag="cell", bufs=CELL_BUFS)
+            acc = psum.tile([P, 2, 2 * P], F32, name="turned_q", tag="s", bufs=PSUM_BANKS["s"])
+            xin = psum.tile([P, 2, 2 * P], F32, name="xin", tag="b", bufs=PSUM_BANKS["b"])
             for b in range(2):
                 m = 2 * quarter + b
                 for a in range(2):
@@ -419,15 +392,27 @@ def tile_advancedliquidneuralnetwork_pb_kernel(
                     )
             for b in range(2):
                 m = 2 * quarter + b
-                nc.vector.scalar_tensor_tensor(
-                    out=cell(pair)[:, m, :],
-                    in0=acc[:, b, :],
-                    scalar=g_cols[:, m : m + 1],
-                    in1=cell(pair)[:, m, :],
-                    op0=ALU.mult,
-                    op1=ALU.add,
+                features = slice(m * P, (m + 1) * P)
+                nc.tensor.matmul_mx(
+                    out=xin[:, b, :],
+                    lhsT=w_in_codes[:, 0, features].bitcast(FP8X4),
+                    lhsT_scale=w_scales[:, PLANE_IN, features],
+                    rhs=x_codes[:, 0, pair_tokens(pair)].bitcast(FP8X4),
+                    rhs_scale=x_scales[:, 0, pair_tokens(pair)],
+                    start=True,
+                    stop=True,
                 )
-            blocks = cell(pair)[:, 2 * quarter : 2 * quarter + 2, :]
+            for b in range(2):
+                m = 2 * quarter + b
+                nc.scalar.activation(
+                    out=cell[pair][:, m, :],
+                    in_=acc[:, b, :],
+                    func=ACT.Identity,
+                    bias=shift_cols[:, m : m + 1],
+                    scale=g_cols[:, m : m + 1],
+                )
+            blocks = cell[pair][:, 2 * quarter : 2 * quarter + 2, :]
+            nc.vector.tensor_tensor(out=blocks, in0=xin[:], in1=blocks, op=ALU.add)
             nc.scalar.activation(out=blocks, in_=blocks, func=ACT.Tanh)
 
         def stage_h(pair, quarter):
@@ -443,7 +428,7 @@ def tile_advancedliquidneuralnetwork_pb_kernel(
             for b in range(4):
                 nc.tensor.matmul(
                     out=acc[:, b * P : (b + 1) * P],
-                    lhsT=cell(pair)[:, 4 * half + b, a * P : (a + 1) * P],
+                    lhsT=cell[pair][:, 4 * half + b, a * P : (a + 1) * P],
                     rhs=ident_f32[:],
                     is_transpose=True,
                     start=False,
@@ -459,17 +444,18 @@ def tile_advancedliquidneuralnetwork_pb_kernel(
                 (k, n) for k in range(PAIRS) for n in range(parts) if max(first + 4 * k + every * n, 0) == slot
             ]
 
-        sort_columns(0)
+        with tc.manual_schedule(engines={mybir.EngineType.DVE}):
+            sort_columns(0)
+            quantise_liq(0)
+            quantise_liq(1)
+            sort_columns(1)
         for slot in range(15 + 4 * PAIRS):
             for k, n in due(0):
                 stage_b(k, n)
-                stage_bq(k, n)
-            if slot == 0:
-                sort_columns(1)
-            for k, n in due(6):
-                stage_x(k, n)
-            for k, n in due(0, 2):
-                stage_l(k, n)
+                if n % 2 == 1:
+                    stage_bq(k, n // 2)
+            for k, n in due(1, 1):
+                stage_l(k)
             for k, n in due(4):
                 stage_t(k, n)
             for k, n in due(5, 1):
@@ -487,6 +473,6 @@ def tile_advancedliquidneuralnetwork_pb_kernel(
                 if k > 0:
                     stage_a(k, n)
                     stage_aq(k, n)
-            for k, n in due(3, 1):
+            for k, n in due(5, 1):
                 stage_xt(k)
                 stage_xq(k)

@@ -31,12 +31,10 @@ PLANES = 5
 WORK_BUFS = 4
 CELL_BUFS = 3
 MEAN_ON_GPSIMD = ()
-PSUM_BANKS = {"s": 3, "b": 5}
+PSUM_BANKS = {"s": 3, "b": 3, "h": 2}
 PAIRS = TILES // 2
 LIQ_COPIES_ON_VECTOR = ()
 X_COPIES_ON_VECTOR = ()
-H_ON_GPSIMD = (0, 1, 4, 5)
-CLOCK_PAIRS = (2, 3)
 NORM_ON_VECTOR = (-1,)
 WARM_UP_MATMULS = 12
 ROW_TAU, ROW_BETA, ROW_B_IN, ROW_G, ROW_B_O = 0, 1, 2, 3, 4
@@ -151,12 +149,12 @@ def tile_advancedliquidneuralnetwork_pb_kernel(
         load_tokens(liq_sb, liq_rows, 2, 2)
         load_scales(W_o_scales, PLANE_O)
         load_codes(W_o_words, w_o_codes)
-        load_tokens(x_sb, x_rows, 0, 4)
+        load_tokens(liq_sb, liq_rows, 4, 2)
+        load_tokens(liq_sb, liq_rows, 6, 2)
         load_scales(W_in_scales, PLANE_IN)
         load_codes(W_in_words, w_in_codes)
-        load_tokens(liq_sb, liq_rows, 4, 2)
+        load_tokens(x_sb, x_rows, 0, 4)
         load_tokens(h_sb, h_rows, 0, 2)
-        load_tokens(liq_sb, liq_rows, 6, 2)
         load_tokens(h_sb, h_rows, 2, 2)
         load_tokens(x_sb, x_rows, 4, 4)
         load_tokens(h_sb, h_rows, 4, 4)
@@ -239,9 +237,14 @@ def tile_advancedliquidneuralnetwork_pb_kernel(
         )
         nc.vector.tensor_scalar_add(out=rate_cols[:], in0=block_cols(vec_cols, ROW_TAU), scalar1=TAU_EPS)
         nc.vector.reciprocal(out=rate_cols[:], in_=rate_cols[:])
-        minus_ident = keep.tile([P, P], BF16)
-        nc.gpsimd.tensor_scalar(
-            out=minus_ident[:], in0=ident_bf[:], scalar1=-1.0, scalar2=0.0, op0=ALU.mult, op1=ALU.add
+        h_factor_cols = keep.tile([P, H_BLOCKS], F32)
+        nc.vector.tensor_scalar(
+            out=h_factor_cols[:],
+            in0=block_cols(vec_cols, ROW_TAU),
+            scalar1=-1.0,
+            scalar2=TAU_EPS,
+            op0=ALU.add,
+            op1=ALU.add,
         )
 
         def pair_tokens(pair):
@@ -358,9 +361,7 @@ def tile_advancedliquidneuralnetwork_pb_kernel(
                 out=squares[:], in_=resid[i], func=ACT.Square, bias=neg_mean[i][:], scale=1.0, accum_out=sum_sq[:]
             )
             var_eps = stat.tile([P, 1], F32, name="var_eps", tag="var_eps")
-            nc.gpsimd.tensor_scalar(
-                out=var_eps[:], in0=sum_sq[:], scalar1=1.0 / H, scalar2=LN_EPS, op0=ALU.mult, op1=ALU.add
-            )
+            nc.scalar.activation(out=var_eps[:], in_=sum_sq[:], func=ACT.Copy, bias=LN_EPS, scale=1.0 / H)
             rstd[i] = stat.tile([P, 1], F32, name="rstd", tag="rstd")
             nc.gpsimd.tensor_tensor(out=rstd[i][:], in0=var_eps[:], in1=minus_half[:], op=ALU.pow)
             if i in NORM_ON_VECTOR:
@@ -374,7 +375,7 @@ def tile_advancedliquidneuralnetwork_pb_kernel(
                 )
             else:
                 shift = stat.tile([P, 1], F32, name="shift", tag="shift")
-                nc.gpsimd.tensor_tensor(out=shift[:], in0=neg_mean[i][:], in1=rstd[i][:], op=ALU.mult)
+                nc.scalar.activation(out=shift[:], in_=neg_mean[i][:], func=ACT.Copy, scale=rstd[i][:])
                 nc.scalar.activation(
                     out=resid[i], in_=resid[i], func=ACT.Identity, bias=shift[:], scale=rstd[i][:]
                 )
@@ -415,6 +416,29 @@ def tile_advancedliquidneuralnetwork_pb_kernel(
             nc.vector.tensor_tensor(out=blocks, in0=xin[:], in1=blocks, op=ALU.add)
             nc.scalar.activation(out=blocks, in_=blocks, func=ACT.Tanh)
 
+        def stage_g(pair, half):
+            turned_h[pair, half] = psum.tile([P, 4, 2 * P], BF16, name="turned_h", tag="h", bufs=PSUM_BANKS["h"])
+            for b in range(4):
+                m = 4 * half + b
+                for a in range(2):
+                    nc.tensor.transpose(
+                        turned_h[pair, half][:, b, a * P : (a + 1) * P],
+                        h_sb[:, 2 * pair + a, m * P : (m + 1) * P],
+                        ident_bf[:],
+                    )
+
+        def stage_y(pair, half):
+            for b in range(4):
+                m = 4 * half + b
+                nc.vector.scalar_tensor_tensor(
+                    out=cell[pair][:, m, :],
+                    in0=turned_h[pair, half][:, b, :],
+                    scalar=h_factor_cols[:, m : m + 1],
+                    in1=cell[pair][:, m, :],
+                    op0=ALU.mult,
+                    op1=ALU.add,
+                )
+
         def stage_h(pair, quarter):
             half, a = quarter // 2, quarter % 2
             i = 2 * pair + a
@@ -422,21 +446,11 @@ def tile_advancedliquidneuralnetwork_pb_kernel(
                 work[i] = ring.tile([P, H], F32, name="work", tag="work", bufs=WORK_BUFS)
             cols = columns(half)
             acc = bank("b")
-            if pair in CLOCK_PAIRS:
-                nc.tensor.matmul(out=acc[:], lhsT=minus_ident[:], rhs=h_sb[:, i, cols], start=True, stop=True)
-            nc.tensor.matmul(out=acc[:], lhsT=minus_ident[:], rhs=h_sb[:, i, cols], start=True, stop=False)
             for b in range(4):
-                nc.tensor.matmul(
-                    out=acc[:, b * P : (b + 1) * P],
-                    lhsT=cell[pair][:, 4 * half + b, a * P : (a + 1) * P],
-                    rhs=ident_f32[:],
-                    is_transpose=True,
-                    start=False,
-                    stop=(b == 3),
+                nc.tensor.transpose(
+                    acc[:, b * P : (b + 1) * P], cell[pair][:, 4 * half + b, a * P : (a + 1) * P], ident_f32[:]
                 )
             nc.vector.tensor_tensor(out=work[i][:, cols], in0=acc[:], in1=rate_rows[:, cols], op=ALU.mult)
-            engine = nc.gpsimd if i in H_ON_GPSIMD else nc.vector
-            engine.tensor_tensor(out=work[i][:, cols], in0=work[i][:, cols], in1=h_sb[:, i, cols], op=ALU.add)
             nc.sync.dma_start(out=out_rows[:, i, cols], in_=work[i][:, cols])
 
         def due(first, parts=4, every=1):
@@ -449,12 +463,12 @@ def tile_advancedliquidneuralnetwork_pb_kernel(
             quantise_liq(0)
             quantise_liq(1)
             sort_columns(1)
-        for slot in range(15 + 4 * PAIRS):
+        for slot in range(16 + 4 * PAIRS):
             for k, n in due(0):
                 stage_b(k, n)
                 if n % 2 == 1:
                     stage_bq(k, n // 2)
-            for k, n in due(1, 1):
+            for k, n in due(2, 1):
                 stage_l(k)
             for k, n in due(4):
                 stage_t(k, n)
@@ -467,7 +481,10 @@ def tile_advancedliquidneuralnetwork_pb_kernel(
                 spread_rate(1)
             for k, n in due(12):
                 stage_f(k, n)
-            for k, n in due(15):
+            for k, n in due(13, 2, 2):
+                stage_g(k, n)
+                stage_y(k, n)
+            for k, n in due(16):
                 stage_h(k, n)
             for k, n in due(-3, 2):
                 if k > 0:

@@ -33,8 +33,6 @@ CELL_BUFS = 3
 MEAN_ON_GPSIMD = ()
 PSUM_BANKS = {"s": 3, "b": 3, "h": 2}
 PAIRS = TILES // 2
-LIQ_COPIES_ON_VECTOR = ()
-X_COPIES_ON_VECTOR = ()
 NORM_ON_VECTOR = (-1,)
 WARM_UP_MATMULS = 12
 ROW_TAU, ROW_BETA, ROW_B_IN, ROW_G, ROW_B_O = 0, 1, 2, 3, 4
@@ -97,13 +95,13 @@ def tile_advancedliquidneuralnetwork_pb_kernel(
         h_rows = h.rearrange("(p i) f -> p i f", i=TILES)
         out_rows = out.rearrange("(p i) f -> p i f", i=TILES)
 
-        nc.vector.memset(minus_half[:], -0.5)
         nc.vector.memset(w_scales[:, PLANE_V : PLANE_V + H_GROUPS, :].bitcast(I32), 0)
+        nc.vector.memset(minus_half[:], -0.5)
+        nc.vector.memset(vec_rows[:], 0.0)
+        nc.vector.memset(w_scales[:, PLANE_O : PLANE_O + H_GROUPS, :].bitcast(I32), 0)
+        nc.vector.memset(w_scales[:, PLANE_IN : PLANE_IN + 1, :].bitcast(I32), 0)
         make_identity(nc, ident_bf[:])
         make_identity(nc, ident_f32[:])
-        nc.gpsimd.memset(vec_rows[:], 0.0)
-        nc.gpsimd.memset(w_scales[:, PLANE_O : PLANE_O + H_GROUPS, :].bitcast(I32), 0)
-        nc.gpsimd.memset(w_scales[:, PLANE_IN : PLANE_IN + 1, :].bitcast(I32), 0)
         nc.scalar.activation(out=table_loaded[:], in_=minus_half[:], func=ACT.Tanh)
 
         def load_tokens(dst, src, first, count):
@@ -190,17 +188,14 @@ def tile_advancedliquidneuralnetwork_pb_kernel(
                 )
             nc.scalar.copy(out=rate_rows[:, columns(half)], in_=rows[:])
 
-        def turn(first, second, tag, on_vector=False):
+        def turn(first, second, tag):
             turned = psum.tile([P, 2, 2, P], F32, name="turned", tag="s", bufs=PSUM_BANKS["s"])
             for a, rows in enumerate((first, second)):
                 words = rows.bitcast(F32)
                 for u in range(2):
                     nc.tensor.transpose(turned[:, a, u, :], words[:, u : K_PASS // 2 : 2], ident_f32[:])
             grouped = ring.tile([P, 2, P, PACK], BF16, name=tag, tag=tag, bufs=3, align_bytes=64)
-            if on_vector:
-                nc.vector.tensor_copy(out=grouped[:].bitcast(F32), in_=turned[:].rearrange("p a u r -> p a r u"))
-            else:
-                nc.scalar.copy(out=grouped[:].bitcast(F32), in_=turned[:].rearrange("p a u r -> p a r u"))
+            nc.scalar.copy(out=grouped[:].bitcast(F32), in_=turned[:].rearrange("p a u r -> p a r u"))
             return grouped
 
         def quantise(grouped, codes, scales):
@@ -209,7 +204,7 @@ def tile_advancedliquidneuralnetwork_pb_kernel(
             )
 
         def turn_liq(i):
-            return turn(liq_sb[:, i, :K_PASS], liq_sb[:, i, K_PASS:], "grouped_liq", on_vector=i in LIQ_COPIES_ON_VECTOR)
+            return turn(liq_sb[:, i, :K_PASS], liq_sb[:, i, K_PASS:], "grouped_liq")
 
         grouped_liq = {}
 
@@ -232,7 +227,7 @@ def tile_advancedliquidneuralnetwork_pb_kernel(
 
         shift_cols = keep.tile([P, H_BLOCKS], F32)
         rate_cols = keep.tile([P, H_BLOCKS], F32)
-        nc.gpsimd.tensor_tensor(
+        nc.vector.tensor_tensor(
             out=shift_cols[:], in0=block_cols(vec_cols, ROW_BETA), in1=block_cols(vec_cols, ROW_B_IN), op=ALU.add
         )
         nc.vector.tensor_scalar_add(out=rate_cols[:], in0=block_cols(vec_cols, ROW_TAU), scalar1=TAU_EPS)
@@ -261,15 +256,16 @@ def tile_advancedliquidneuralnetwork_pb_kernel(
         def stage_aq(pair, a):
             quantise_liq(2 * pair + a)
 
-        def sort_columns(group_of_v):
-            cols = columns(group_of_v)
+        def sort_scales(half):
             nc.vector.tensor_copy(
-                out=w_v_sorted[:, group_of_v, :, :].bitcast(I32).rearrange("p g (t m) -> p g t m", t=PACK),
-                in_=w_v_codes[:, group_of_v, :, :].bitcast(I32).rearrange("p g (m t) -> p g t m", t=PACK),
+                out=w_v_sorted_scales[:, half, :, :].rearrange("p g (t m) -> p g t m", t=PACK),
+                in_=w_scales[:, PLANE_V : PLANE_V + H_GROUPS, columns(half)].rearrange("p g (m t) -> p g t m", t=PACK),
             )
-            nc.gpsimd.tensor_copy(
-                out=w_v_sorted_scales[:, group_of_v, :, :].rearrange("p g (t m) -> p g t m", t=PACK),
-                in_=w_scales[:, PLANE_V : PLANE_V + H_GROUPS, cols].rearrange("p g (m t) -> p g t m", t=PACK),
+
+        def sort_codes(half):
+            nc.vector.tensor_copy(
+                out=w_v_sorted[:, half, :, :].bitcast(I32).rearrange("p g (t m) -> p g t m", t=PACK),
+                in_=w_v_codes[:, half, :, :].bitcast(I32).rearrange("p g (m t) -> p g t m", t=PACK),
             )
 
         def stage_b(pair, quarter):
@@ -339,7 +335,7 @@ def tile_advancedliquidneuralnetwork_pb_kernel(
             )
 
         def stage_xt(pair):
-            grouped_x[pair] = turn(x_sb[:, 2 * pair, :], x_sb[:, 2 * pair + 1, :], "grouped_x", on_vector=pair in X_COPIES_ON_VECTOR)
+            grouped_x[pair] = turn(x_sb[:, 2 * pair, :], x_sb[:, 2 * pair + 1, :], "grouped_x")
 
         def stage_xq(pair):
             quantise(grouped_x[pair], x_codes[:, 0, pair_tokens(pair)], x_scales[:, 0, pair_tokens(pair)])
@@ -459,10 +455,12 @@ def tile_advancedliquidneuralnetwork_pb_kernel(
             ]
 
         with tc.manual_schedule(engines={mybir.EngineType.DVE}):
-            sort_columns(0)
+            sort_scales(0)
+            sort_codes(0)
             quantise_liq(0)
+            sort_scales(1)
             quantise_liq(1)
-            sort_columns(1)
+            sort_codes(1)
         for slot in range(16 + 4 * PAIRS):
             for k, n in due(0):
                 stage_b(k, n)

@@ -18,6 +18,7 @@ K_PASS = P * PACK
 BANK = 512
 B, IN, H = 1024, 512, 1024
 TILES = B // P
+PAIRS = TILES // 2
 H_GROUPS = H // K_PASS
 H_BANKS = H // BANK
 H_BLOCKS = H // P
@@ -28,14 +29,19 @@ FLOPS = 2 * B * (IN * H + H * H + H * H)
 
 PLANE_IN, PLANE_V, PLANE_O = 0, 1, 3
 PLANES = 5
-WORK_BUFS = 4
-CELL_BUFS = 3
-MEAN_ON_GPSIMD = ()
-PSUM_BANKS = {"s": 3, "b": 3, "h": 2}
-PAIRS = TILES // 2
-NORM_ON_VECTOR = (-1,)
-WARM_UP_MATMULS = 12
+
 ROW_TAU, ROW_BETA, ROW_B_IN, ROW_G, ROW_B_O = 0, 1, 2, 3, 4
+VECTORS = 5
+
+PSUM_BANKS = {"scalar": 3, "vector": 3, "h": 2}
+CELL_BUFS = 3
+OUT_BUFS = 4
+WARM_UP_MATMULS = 12
+
+ATT_FIRST = 4
+NORMALISE_FIRST = (5, 7)
+SQUASH_FIRST = 10
+END_FIRST = SQUASH_FIRST + 4
 
 
 def tile_advancedliquidneuralnetwork_pb_kernel(
@@ -64,8 +70,8 @@ def tile_advancedliquidneuralnetwork_pb_kernel(
         stat = ctx.enter_context(tc.tile_pool(name="stat", bufs=4))
         psum = ctx.enter_context(tc.psum_pool(name="psum", bufs=1))
 
-        def bank(tag):
-            return psum.tile([P, BANK], F32, name=tag, tag=tag, bufs=PSUM_BANKS[tag])
+        def bank(tag, shape=(BANK,), dtype=F32):
+            return psum.tile([P, *shape], dtype, name=tag, tag=tag, bufs=PSUM_BANKS[tag])
 
         liq_sb = keep.tile([P, TILES, H], BF16)
         x_sb = keep.tile([P, TILES, IN], BF16)
@@ -80,8 +86,8 @@ def tile_advancedliquidneuralnetwork_pb_kernel(
         liq_scales = keep.tile([P, TILES, H_GROUPS * P], U8, align_bytes=64)
         v_codes = keep.tile([P, H_GROUPS, B], U32, align_bytes=64)
         v_scales = keep.tile([P, H_GROUPS, B], U8, align_bytes=64)
-        x_codes = keep.tile([P, 1, B], U32, align_bytes=64)
-        x_scales = keep.tile([P, 1, B], U8, align_bytes=64)
+        x_codes = keep.tile([P, B], U32, align_bytes=64)
+        x_scales = keep.tile([P, B], U8, align_bytes=64)
         b_v_cols = keep.tile([P, H_GROUPS, PACK], BF16)
         vec_rows = keep.tile([P, P], BF16)
         table_loaded = keep.tile([P, 1], F32)
@@ -89,11 +95,15 @@ def tile_advancedliquidneuralnetwork_pb_kernel(
         ident_f32 = keep.tile([P, P], F32)
         minus_half = keep.tile([P, 1], F32)
         rate_rows = keep.tile([P, H], F32)
+        b_o_rows = keep.tile([P, H], BF16)
 
         liq_rows = liq.rearrange("(p i) f -> p i f", i=TILES)
         x_rows = x.rearrange("(p i) f -> p i f", i=TILES)
         h_rows = h.rearrange("(p i) f -> p i f", i=TILES)
         out_rows = out.rearrange("(p i) f -> p i f", i=TILES)
+
+        def columns(half):
+            return slice(half * BANK, (half + 1) * BANK)
 
         nc.vector.memset(w_scales[:, PLANE_V : PLANE_V + H_GROUPS, :].bitcast(I32), 0)
         nc.vector.memset(minus_half[:], -0.5)
@@ -115,22 +125,16 @@ def tile_advancedliquidneuralnetwork_pb_kernel(
                     in_=scales[:, 4 * quad : 4 * quad + 4, :].bitcast(I32).rearrange("g r n -> r g n"),
                 )
 
+        def load_codes(dst, words):
+            nc.sync.dma_start(out=dst.bitcast(I32), in_=words.rearrange("p n t -> p (n t)").bitcast(I32))
+
         def load_half_of_w_v(half):
             for g in range(H_GROUPS):
-                nc.sync.dma_start(
-                    out=w_v_codes[:, half, g, :].bitcast(I32),
-                    in_=W_v_words[g, :, half * BANK : (half + 1) * BANK, :].rearrange("p n t -> p (n t)").bitcast(I32),
-                )
+                load_codes(w_v_codes[:, half, g, :], W_v_words[g, :, columns(half), :])
 
-        def load_codes(words, codes):
-            for g in range(words.shape[0]):
-                nc.sync.dma_start(
-                    out=codes[:, g, :].bitcast(I32), in_=words[g].rearrange("p n t -> p (n t)").bitcast(I32)
-                )
-
-        def load_vector(rows, row, vec):
+        def load_vector(row, vec):
             nc.sync.dma_start(
-                out=rows[H_BLOCKS * row : H_BLOCKS * (row + 1), :], in_=vec.rearrange("(m c) -> m c", c=P)
+                out=vec_rows[H_BLOCKS * row : H_BLOCKS * (row + 1), :], in_=vec.rearrange("(m c) -> m c", c=P)
             )
 
         load_tokens(liq_sb, liq_rows, 0, 1)
@@ -139,57 +143,27 @@ def tile_advancedliquidneuralnetwork_pb_kernel(
         nc.sync.dma_start(out=b_v_cols[:], in_=b_v.rearrange("(g p t) -> p g t", g=H_GROUPS, t=PACK))
         load_tokens(liq_sb, liq_rows, 1, 1)
         load_half_of_w_v(1)
-        load_vector(vec_rows, ROW_B_O, b_o)
-        load_vector(vec_rows, ROW_TAU, tau)
-        load_vector(vec_rows, ROW_G, g_att)
-        load_vector(vec_rows, ROW_BETA, beta_att)
-        load_vector(vec_rows, ROW_B_IN, b_in)
+        load_vector(ROW_B_O, b_o)
+        load_vector(ROW_TAU, tau)
+        load_vector(ROW_G, g_att)
+        load_vector(ROW_BETA, beta_att)
+        load_vector(ROW_B_IN, b_in)
         load_tokens(liq_sb, liq_rows, 2, 2)
         load_scales(W_o_scales, PLANE_O)
-        load_codes(W_o_words, w_o_codes)
+        for g in range(H_GROUPS):
+            load_codes(w_o_codes[:, g, :], W_o_words[g])
         load_tokens(liq_sb, liq_rows, 4, 2)
         load_tokens(liq_sb, liq_rows, 6, 2)
         load_scales(W_in_scales, PLANE_IN)
-        load_codes(W_in_words, w_in_codes)
+        load_codes(w_in_codes[:, 0, :], W_in_words[0])
         load_tokens(x_sb, x_rows, 0, 4)
         load_tokens(h_sb, h_rows, 0, 2)
         load_tokens(h_sb, h_rows, 2, 2)
         load_tokens(x_sb, x_rows, 4, 4)
         load_tokens(h_sb, h_rows, 4, 4)
 
-        def block_cols(cols, row):
-            return cols[:, H_BLOCKS * row : H_BLOCKS * (row + 1)]
-
-        def columns(half):
-            return slice(half * BANK, (half + 1) * BANK)
-
-        def spread_input_vector(row, name):
-            everywhere = keep.tile([P, H], BF16, name=name)
-            for half in range(H_BANKS):
-                rows = bank("s")
-                for q in range(BANK // P):
-                    r = H_BLOCKS * row + half * (BANK // P) + q
-                    nc.tensor.matmul(
-                        out=rows[:, q * P : (q + 1) * P],
-                        lhsT=ident_bf[:, r : r + 1].to_broadcast([P, P]),
-                        rhs=vec_rows[:],
-                        start=True,
-                        stop=True,
-                    )
-                nc.scalar.copy(out=everywhere[:, columns(half)], in_=rows[:])
-            return everywhere
-
-        def spread_rate(half):
-            rows = bank("s")
-            for q in range(BANK // P):
-                m = half * (BANK // P) + q
-                nc.tensor.transpose(
-                    rows[:, q * P : (q + 1) * P], rate_cols[:, m : m + 1].to_broadcast([P, P]), ident_f32[:]
-                )
-            nc.scalar.copy(out=rate_rows[:, columns(half)], in_=rows[:])
-
         def turn(first, second, tag):
-            turned = psum.tile([P, 2, 2, P], F32, name="turned", tag="s", bufs=PSUM_BANKS["s"])
+            turned = bank("scalar", (2, 2, P))
             for a, rows in enumerate((first, second)):
                 words = rows.bitcast(F32)
                 for u in range(2):
@@ -203,58 +177,77 @@ def tile_advancedliquidneuralnetwork_pb_kernel(
                 out=codes.bitcast(FP8X4), scales=scales, in_=grouped[:].rearrange("p a r t -> p (a r t)")
             )
 
-        def turn_liq(i):
-            return turn(liq_sb[:, i, :K_PASS], liq_sb[:, i, K_PASS:], "grouped_liq")
+        grouped_liq, grouped_x = {}, {}
 
-        grouped_liq = {}
+        def turn_liq(i):
+            grouped_liq[i] = turn(liq_sb[:, i, :K_PASS], liq_sb[:, i, K_PASS:], "grouped_liq")
 
         def quantise_liq(i):
             quantise(grouped_liq[i], liq_codes[:, i, :], liq_scales[:, i, :])
 
-        for k in range(WARM_UP_MATMULS):
-            unread_bank = bank("b")
+        def pair_tokens(pair):
+            return slice(2 * pair * P, (2 * pair + 2) * P)
+
+        def turn_x(pair):
+            grouped_x[pair] = turn(x_sb[:, 2 * pair, :], x_sb[:, 2 * pair + 1, :], "grouped_x")
+
+        def quantise_x(pair):
+            quantise(grouped_x[pair], x_codes[:, pair_tokens(pair)], x_scales[:, pair_tokens(pair)])
+
+        for _ in range(WARM_UP_MATMULS):
+            unread_bank = bank("vector")
             nc.tensor.matmul(out=unread_bank[:, :P], lhsT=ident_bf[:], rhs=ident_bf[:], start=True, stop=True)
-        grouped_liq[0] = turn_liq(0)
-        grouped_liq[1] = turn_liq(1)
+        turn_liq(0)
+        turn_liq(1)
 
-        b_o_rows = spread_input_vector(ROW_B_O, "b_o_rows")
+        for half in range(H_BANKS):
+            rows = bank("scalar")
+            for q in range(BANK // P):
+                r = H_BLOCKS * ROW_B_O + half * (BANK // P) + q
+                nc.tensor.matmul(
+                    out=rows[:, q * P : (q + 1) * P],
+                    lhsT=ident_bf[:, r : r + 1].to_broadcast([P, P]),
+                    rhs=vec_rows[:],
+                    start=True,
+                    stop=True,
+                )
+            nc.scalar.copy(out=b_o_rows[:, columns(half)], in_=rows[:])
 
-        vec_ps = psum.tile([P, P], BF16, name="vec_ps", tag="s", bufs=PSUM_BANKS["s"])
+        vec_ps = bank("scalar", (P,), BF16)
         nc.tensor.transpose(vec_ps[:], vec_rows[:], ident_bf[:])
-        vec_cols = keep.tile([P, 5 * H_BLOCKS], F32)
-        nc.vector.tensor_copy(out=vec_cols[:], in_=vec_ps[:, : 5 * H_BLOCKS])
-        g_cols = block_cols(vec_cols, ROW_G)
+        vec_cols = keep.tile([P, VECTORS * H_BLOCKS], F32)
+        nc.vector.tensor_copy(out=vec_cols[:], in_=vec_ps[:, : VECTORS * H_BLOCKS])
 
+        def vector_cols(row):
+            return vec_cols[:, H_BLOCKS * row : H_BLOCKS * (row + 1)]
+
+        g_cols = vector_cols(ROW_G)
         shift_cols = keep.tile([P, H_BLOCKS], F32)
         rate_cols = keep.tile([P, H_BLOCKS], F32)
-        nc.vector.tensor_tensor(
-            out=shift_cols[:], in0=block_cols(vec_cols, ROW_BETA), in1=block_cols(vec_cols, ROW_B_IN), op=ALU.add
-        )
-        nc.vector.tensor_scalar_add(out=rate_cols[:], in0=block_cols(vec_cols, ROW_TAU), scalar1=TAU_EPS)
-        nc.vector.reciprocal(out=rate_cols[:], in_=rate_cols[:])
         h_factor_cols = keep.tile([P, H_BLOCKS], F32)
+        nc.vector.tensor_tensor(
+            out=shift_cols[:], in0=vector_cols(ROW_BETA), in1=vector_cols(ROW_B_IN), op=ALU.add
+        )
+        nc.vector.tensor_scalar_add(out=rate_cols[:], in0=vector_cols(ROW_TAU), scalar1=TAU_EPS)
+        nc.vector.reciprocal(out=rate_cols[:], in_=rate_cols[:])
         nc.vector.tensor_scalar(
             out=h_factor_cols[:],
-            in0=block_cols(vec_cols, ROW_TAU),
+            in0=vector_cols(ROW_TAU),
             scalar1=-1.0,
             scalar2=TAU_EPS,
             op0=ALU.add,
             op1=ALU.add,
         )
 
-        def pair_tokens(pair):
-            return slice(2 * pair * P, (2 * pair + 2) * P)
-
-        grouped_x, grouped_v = {}, {}
-        cell = {}
-        resid, sums, neg_mean, rstd = {}, {}, {}, {}
-        att_turned, turned_h, work = {}, {}, {}
-
-        def stage_a(pair, a):
-            grouped_liq[2 * pair + a] = turn_liq(2 * pair + a)
-
-        def stage_aq(pair, a):
-            quantise_liq(2 * pair + a)
+        def spread_rate():
+            for half in range(H_BANKS):
+                rows = bank("scalar")
+                for q in range(BANK // P):
+                    m = half * (BANK // P) + q
+                    nc.tensor.transpose(
+                        rows[:, q * P : (q + 1) * P], rate_cols[:, m : m + 1].to_broadcast([P, P]), ident_f32[:]
+                    )
+                nc.scalar.copy(out=rate_rows[:, columns(half)], in_=rows[:])
 
         def sort_scales(half):
             nc.vector.tensor_copy(
@@ -268,9 +261,12 @@ def tile_advancedliquidneuralnetwork_pb_kernel(
                 in_=w_v_codes[:, half, :, :].bitcast(I32).rearrange("p g (m t) -> p g t m", t=PACK),
             )
 
-        def stage_b(pair, quarter):
-            i, half = 2 * pair + quarter % 2, quarter // 2
-            acc = psum.tile([P, PACK, P], F32, name="turned_v", tag="b", bufs=PSUM_BANKS["b"])
+        grouped_v, cell, liq_b = {}, {}, {}
+        resid, sums, out_tile = {}, {}, {}
+
+        def project(pair, part):
+            i, half = 2 * pair + part % 2, part // 2
+            acc = bank("vector", (PACK, P))
             for t in range(PACK):
                 features = slice(t * P, (t + 1) * P)
                 for g in range(H_GROUPS):
@@ -285,20 +281,20 @@ def tile_advancedliquidneuralnetwork_pb_kernel(
                         stop=(g == H_GROUPS - 1),
                     )
             if i % 2 == 0:
-                grouped_v[pair, half] = ring.tile([P, 2, P, PACK], BF16, name="grouped_v", tag="grouped_v", bufs=3, align_bytes=64)
+                grouped_v[pair, half] = ring.tile(
+                    [P, 2, P, PACK], BF16, name="grouped_v", tag="grouped_v", bufs=3, align_bytes=64
+                )
             nc.vector.tensor_tensor(
                 out=grouped_v[pair, half][:, i % 2, :, :],
                 in0=acc[:].rearrange("p t n -> p n t"),
                 in1=b_v_cols[:, half, :].unsqueeze(1).to_broadcast([P, P, PACK]),
                 op=ALU.add,
             )
+            if i % 2 == 1:
+                tokens = pair_tokens(pair)
+                quantise(grouped_v[pair, half], v_codes[:, half, tokens], v_scales[:, half, tokens])
 
-        def stage_bq(pair, half):
-            quantise(grouped_v[pair, half], v_codes[:, half, pair_tokens(pair)], v_scales[:, half, pair_tokens(pair)])
-
-        liq_b = {}
-
-        def stage_l(pair):
+        def add_b_o(pair):
             liq_b[pair] = ring.tile([P, 2, H], F32, name="liq_b", tag="liq_b", bufs=PAIRS)
             nc.vector.tensor_tensor(
                 out=liq_b[pair][:],
@@ -307,12 +303,12 @@ def tile_advancedliquidneuralnetwork_pb_kernel(
                 op=ALU.add,
             )
 
-        def stage_t(pair, quarter):
-            i, half = 2 * pair + quarter // H_BANKS, quarter % H_BANKS
+        def attend(pair, part):
+            i, half = 2 * pair + part // H_BANKS, part % H_BANKS
             if half == 0:
                 resid[i] = liq_b[pair][:, i % 2, :]
                 sums[i] = stat.tile([P, H_BANKS], F32, name="sums", tag="sums")
-            acc = bank("b")
+            acc = bank("vector")
             tokens = slice(i * P, (i + 1) * P)
             for g in range(H_GROUPS):
                 nc.tensor.matmul_mx(
@@ -334,17 +330,10 @@ def tile_advancedliquidneuralnetwork_pb_kernel(
                 accum_out=sums[i][:, half : half + 1],
             )
 
-        def stage_xt(pair):
-            grouped_x[pair] = turn(x_sb[:, 2 * pair, :], x_sb[:, 2 * pair + 1, :], "grouped_x")
-
-        def stage_xq(pair):
-            quantise(grouped_x[pair], x_codes[:, 0, pair_tokens(pair)], x_scales[:, 0, pair_tokens(pair)])
-
-        def stage_n(pair, a):
-            i = 2 * pair + a
-            neg_mean[i] = stat.tile([P, 1], F32, name="neg_mean", tag="neg_mean")
-            (nc.gpsimd if i in MEAN_ON_GPSIMD else nc.vector).tensor_scalar(
-                out=neg_mean[i][:],
+        def normalise(i):
+            neg_mean = stat.tile([P, 1], F32, name="neg_mean", tag="neg_mean")
+            nc.vector.tensor_scalar(
+                out=neg_mean[:],
                 in0=sums[i][:, 0:1],
                 scalar1=sums[i][:, 1:2],
                 scalar2=-1.0 / H,
@@ -354,105 +343,82 @@ def tile_advancedliquidneuralnetwork_pb_kernel(
             squares = ring.tile([P, H], BF16, name="squares", tag="squares")
             sum_sq = stat.tile([P, 1], F32, name="sum_sq", tag="sum_sq")
             nc.scalar.activation(
-                out=squares[:], in_=resid[i], func=ACT.Square, bias=neg_mean[i][:], scale=1.0, accum_out=sum_sq[:]
+                out=squares[:], in_=resid[i], func=ACT.Square, bias=neg_mean[:], scale=1.0, accum_out=sum_sq[:]
             )
             var_eps = stat.tile([P, 1], F32, name="var_eps", tag="var_eps")
             nc.scalar.activation(out=var_eps[:], in_=sum_sq[:], func=ACT.Copy, bias=LN_EPS, scale=1.0 / H)
-            rstd[i] = stat.tile([P, 1], F32, name="rstd", tag="rstd")
-            nc.gpsimd.tensor_tensor(out=rstd[i][:], in0=var_eps[:], in1=minus_half[:], op=ALU.pow)
-            if i in NORM_ON_VECTOR:
-                nc.vector.tensor_scalar(
-                    out=resid[i],
-                    in0=resid[i],
-                    scalar1=neg_mean[i][:],
-                    scalar2=rstd[i][:],
-                    op0=ALU.add,
-                    op1=ALU.mult,
-                )
-            else:
-                shift = stat.tile([P, 1], F32, name="shift", tag="shift")
-                nc.scalar.activation(out=shift[:], in_=neg_mean[i][:], func=ACT.Copy, scale=rstd[i][:])
-                nc.scalar.activation(
-                    out=resid[i], in_=resid[i], func=ACT.Identity, bias=shift[:], scale=rstd[i][:]
-                )
+            rstd = stat.tile([P, 1], F32, name="rstd", tag="rstd")
+            nc.gpsimd.tensor_tensor(out=rstd[:], in0=var_eps[:], in1=minus_half[:], op=ALU.pow)
+            offset = stat.tile([P, 1], F32, name="offset", tag="offset")
+            nc.scalar.activation(out=offset[:], in_=neg_mean[:], func=ACT.Copy, scale=rstd[:])
+            nc.scalar.activation(out=resid[i], in_=resid[i], func=ACT.Identity, bias=offset[:], scale=rstd[:])
 
-        def stage_f(pair, quarter):
-            if quarter == 0:
+        def squash(pair, part):
+            if part == 0:
                 cell[pair] = ring.tile([P, H_BLOCKS, 2 * P], F32, name="cell", tag="cell", bufs=CELL_BUFS)
-            acc = psum.tile([P, 2, 2 * P], F32, name="turned_q", tag="s", bufs=PSUM_BANKS["s"])
-            xin = psum.tile([P, 2, 2 * P], F32, name="xin", tag="b", bufs=PSUM_BANKS["b"])
-            for b in range(2):
-                m = 2 * quarter + b
+            normed = bank("scalar", (2, 2 * P))
+            xin = bank("vector", (2, 2 * P))
+            pair_of_blocks = (2 * part, 2 * part + 1)
+            for b, m in enumerate(pair_of_blocks):
                 for a in range(2):
                     nc.tensor.transpose(
-                        acc[:, b, a * P : (a + 1) * P], resid[2 * pair + a][:, m * P : (m + 1) * P], ident_f32[:]
+                        normed[:, b, a * P : (a + 1) * P], resid[2 * pair + a][:, m * P : (m + 1) * P], ident_f32[:]
                     )
-            for b in range(2):
-                m = 2 * quarter + b
+            for b, m in enumerate(pair_of_blocks):
                 features = slice(m * P, (m + 1) * P)
                 nc.tensor.matmul_mx(
                     out=xin[:, b, :],
                     lhsT=w_in_codes[:, 0, features].bitcast(FP8X4),
                     lhsT_scale=w_scales[:, PLANE_IN, features],
-                    rhs=x_codes[:, 0, pair_tokens(pair)].bitcast(FP8X4),
-                    rhs_scale=x_scales[:, 0, pair_tokens(pair)],
+                    rhs=x_codes[:, pair_tokens(pair)].bitcast(FP8X4),
+                    rhs_scale=x_scales[:, pair_tokens(pair)],
                     start=True,
                     stop=True,
                 )
-            for b in range(2):
-                m = 2 * quarter + b
+            for b, m in enumerate(pair_of_blocks):
                 nc.scalar.activation(
                     out=cell[pair][:, m, :],
-                    in_=acc[:, b, :],
+                    in_=normed[:, b, :],
                     func=ACT.Identity,
                     bias=shift_cols[:, m : m + 1],
                     scale=g_cols[:, m : m + 1],
                 )
-            blocks = cell[pair][:, 2 * quarter : 2 * quarter + 2, :]
+            blocks = cell[pair][:, 2 * part : 2 * part + 2, :]
             nc.vector.tensor_tensor(out=blocks, in0=xin[:], in1=blocks, op=ALU.add)
             nc.scalar.activation(out=blocks, in_=blocks, func=ACT.Tanh)
 
-        def stage_g(pair, half):
-            turned_h[pair, half] = psum.tile([P, 4, 2 * P], BF16, name="turned_h", tag="h", bufs=PSUM_BANKS["h"])
+        def blend(pair, half):
+            turned_h = bank("h", (4, 2 * P), BF16)
             for b in range(4):
                 m = 4 * half + b
                 for a in range(2):
                     nc.tensor.transpose(
-                        turned_h[pair, half][:, b, a * P : (a + 1) * P],
-                        h_sb[:, 2 * pair + a, m * P : (m + 1) * P],
-                        ident_bf[:],
+                        turned_h[:, b, a * P : (a + 1) * P], h_sb[:, 2 * pair + a, m * P : (m + 1) * P], ident_bf[:]
                     )
-
-        def stage_y(pair, half):
             for b in range(4):
                 m = 4 * half + b
                 nc.vector.scalar_tensor_tensor(
                     out=cell[pair][:, m, :],
-                    in0=turned_h[pair, half][:, b, :],
+                    in0=turned_h[:, b, :],
                     scalar=h_factor_cols[:, m : m + 1],
                     in1=cell[pair][:, m, :],
                     op0=ALU.mult,
                     op1=ALU.add,
                 )
 
-        def stage_h(pair, quarter):
-            half, a = quarter // 2, quarter % 2
+        def finish(pair, part):
+            half, a = part // 2, part % 2
             i = 2 * pair + a
             if half == 0:
-                work[i] = ring.tile([P, H], F32, name="work", tag="work", bufs=WORK_BUFS)
-            cols = columns(half)
-            acc = bank("b")
+                out_tile[i] = ring.tile([P, H], F32, name="out_tile", tag="out_tile", bufs=OUT_BUFS)
+            acc = bank("vector")
             for b in range(4):
                 nc.tensor.transpose(
                     acc[:, b * P : (b + 1) * P], cell[pair][:, 4 * half + b, a * P : (a + 1) * P], ident_f32[:]
                 )
-            nc.vector.tensor_tensor(out=work[i][:, cols], in0=acc[:], in1=rate_rows[:, cols], op=ALU.mult)
-            nc.sync.dma_start(out=out_rows[:, i, cols], in_=work[i][:, cols])
-
-        def due(first, parts=4, every=1):
-            return [
-                (k, n) for k in range(PAIRS) for n in range(parts) if max(first + 4 * k + every * n, 0) == slot
-            ]
+            cols = columns(half)
+            nc.vector.tensor_tensor(out=out_tile[i][:, cols], in0=acc[:], in1=rate_rows[:, cols], op=ALU.mult)
+            nc.sync.dma_start(out=out_rows[:, i, cols], in_=out_tile[i][:, cols])
 
         with tc.manual_schedule(engines={mybir.EngineType.DVE}):
             sort_scales(0)
@@ -461,33 +427,34 @@ def tile_advancedliquidneuralnetwork_pb_kernel(
             sort_scales(1)
             quantise_liq(1)
             sort_codes(1)
-        for slot in range(16 + 4 * PAIRS):
+
+        def due(first, parts=4, every=1):
+            return [
+                (k, n) for k in range(PAIRS) for n in range(parts) if max(first + 4 * k + every * n, 0) == slot
+            ]
+
+        for slot in range(END_FIRST + 4 * PAIRS):
             for k, n in due(0):
-                stage_b(k, n)
-                if n % 2 == 1:
-                    stage_bq(k, n // 2)
-            for k, n in due(2, 1):
-                stage_l(k)
-            for k, n in due(4):
-                stage_t(k, n)
-            for k, n in due(5, 1):
-                stage_n(k, 0)
-            for k, n in due(7, 1):
-                stage_n(k, 1)
+                project(k, n)
+            for k, _ in due(2, 1):
+                add_b_o(k)
+            for k, n in due(ATT_FIRST):
+                attend(k, n)
+            for a, first in enumerate(NORMALISE_FIRST):
+                for k, _ in due(first, 1):
+                    normalise(2 * k + a)
             if slot == 4:
-                spread_rate(0)
-                spread_rate(1)
-            for k, n in due(12):
-                stage_f(k, n)
-            for k, n in due(13, 2, 2):
-                stage_g(k, n)
-                stage_y(k, n)
-            for k, n in due(16):
-                stage_h(k, n)
-            for k, n in due(-3, 2):
+                spread_rate()
+            for k, n in due(SQUASH_FIRST):
+                squash(k, n)
+            for k, n in due(SQUASH_FIRST + 1, 2, 2):
+                blend(k, n)
+            for k, n in due(END_FIRST):
+                finish(k, n)
+            for k, n in due(-4, 2):
                 if k > 0:
-                    stage_a(k, n)
-                    stage_aq(k, n)
-            for k, n in due(5, 1):
-                stage_xt(k)
-                stage_xq(k)
+                    turn_liq(2 * k + n)
+                    quantise_liq(2 * k + n)
+            for k, _ in due(5, 1):
+                turn_x(k)
+                quantise_x(k)

from contextlib import ExitStack

import concourse.mybir as mybir
from concourse.masks import make_identity

F32 = mybir.dt.float32
BF16 = mybir.dt.bfloat16
I32 = mybir.dt.int32
U32 = mybir.dt.uint32
U8 = mybir.dt.uint8
FP8X4 = mybir.dt.float8_e4m3fn_x4
ALU = mybir.AluOpType
ACT = mybir.ActivationFunctionType

P = 128
PACK = 4
K_PASS = P * PACK
BANK = 512
B, IN, H = 1024, 512, 1024
TILES = B // P
PAIRS = TILES // 2
H_GROUPS = H // K_PASS
H_BANKS = H // BANK
H_BLOCKS = H // P
LN_EPS = 1e-5
TAU_EPS = 1e-6

FLOPS = 2 * B * (IN * H + H * H + H * H)

PLANE_IN, PLANE_V, PLANE_O = 0, 1, 3
PLANES = 5

ROW_TAU, ROW_BETA, ROW_B_IN, ROW_G, ROW_B_O = 0, 1, 2, 3, 4
VECTORS = 5

PSUM_BANKS = {"scalar": 3, "vector": 3, "h": 2}
CELL_BUFS = 3
OUT_BUFS = 4
WARM_UP_MATMULS = 12

ATT_FIRST = 4
NORMALISE_FIRST = (5, 7)
SQUASH_FIRST = 10
END_FIRST = SQUASH_FIRST + 4


def tile_advancedliquidneuralnetwork_pb_kernel(
    tc,
    liq,
    h,
    x,
    W_in_words,
    W_in_scales,
    b_in,
    W_v_words,
    W_v_scales,
    b_v,
    W_o_words,
    W_o_scales,
    b_o,
    g_att,
    beta_att,
    tau,
    out,
):
    nc = tc.nc
    with ExitStack() as ctx:
        keep = ctx.enter_context(tc.tile_pool(name="keep", bufs=1))
        ring = ctx.enter_context(tc.tile_pool(name="ring", bufs=2))
        stat = ctx.enter_context(tc.tile_pool(name="stat", bufs=4))
        psum = ctx.enter_context(tc.psum_pool(name="psum", bufs=1))

        def bank(tag, shape=(BANK,), dtype=F32):
            return psum.tile([P, *shape], dtype, name=tag, tag=tag, bufs=PSUM_BANKS[tag])

        liq_sb = keep.tile([P, TILES, H], BF16)
        x_sb = keep.tile([P, TILES, IN], BF16)
        h_sb = keep.tile([P, TILES, H], BF16)
        w_in_codes = keep.tile([P, 1, H], U32, align_bytes=64)
        w_v_codes = keep.tile([P, H_BANKS, H_GROUPS, BANK], U32, align_bytes=64)
        w_v_sorted = keep.tile([P, H_BANKS, H_GROUPS, BANK], U32, align_bytes=64)
        w_v_sorted_scales = keep.tile([P, H_BANKS, H_GROUPS, BANK], U8, align_bytes=64)
        w_o_codes = keep.tile([P, H_GROUPS, H], U32, align_bytes=64)
        w_scales = keep.tile([P, PLANES, H], U8, align_bytes=64)
        liq_codes = keep.tile([P, TILES, H_GROUPS * P], U32, align_bytes=64)
        liq_scales = keep.tile([P, TILES, H_GROUPS * P], U8, align_bytes=64)
        v_codes = keep.tile([P, H_GROUPS, B], U32, align_bytes=64)
        v_scales = keep.tile([P, H_GROUPS, B], U8, align_bytes=64)
        x_codes = keep.tile([P, B], U32, align_bytes=64)
        x_scales = keep.tile([P, B], U8, align_bytes=64)
        b_v_cols = keep.tile([P, H_GROUPS, PACK], BF16)
        vec_rows = keep.tile([P, P], BF16)
        table_loaded = keep.tile([P, 1], F32)
        ident_bf = keep.tile([P, P], BF16)
        ident_f32 = keep.tile([P, P], F32)
        minus_half = keep.tile([P, 1], F32)
        rate_rows = keep.tile([P, H], F32)
        b_o_rows = keep.tile([P, H], BF16)

        liq_rows = liq.rearrange("(p i) f -> p i f", i=TILES)
        x_rows = x.rearrange("(p i) f -> p i f", i=TILES)
        h_rows = h.rearrange("(p i) f -> p i f", i=TILES)
        out_rows = out.rearrange("(p i) f -> p i f", i=TILES)

        def columns(half):
            return slice(half * BANK, (half + 1) * BANK)

        nc.vector.memset(w_scales[:, PLANE_V : PLANE_V + H_GROUPS, :].bitcast(I32), 0)
        nc.vector.memset(minus_half[:], -0.5)
        nc.vector.memset(vec_rows[:], 0.0)
        nc.vector.memset(w_scales[:, PLANE_O : PLANE_O + H_GROUPS, :].bitcast(I32), 0)
        nc.vector.memset(w_scales[:, PLANE_IN : PLANE_IN + 1, :].bitcast(I32), 0)
        make_identity(nc, ident_bf[:])
        make_identity(nc, ident_f32[:])
        nc.scalar.activation(out=table_loaded[:], in_=minus_half[:], func=ACT.Tanh)

        def load_tokens(dst, src, first, count):
            nc.sync.dma_start(out=dst[:, first : first + count, :], in_=src[:, first : first + count, :])

        def load_scales(scales, plane):
            groups = scales.shape[0]
            for quad in range(4):
                nc.sync.dma_start(
                    out=w_scales[32 * quad : 32 * quad + 4, plane : plane + groups, :].bitcast(I32),
                    in_=scales[:, 4 * quad : 4 * quad + 4, :].bitcast(I32).rearrange("g r n -> r g n"),
                )

        def load_codes(dst, words):
            nc.sync.dma_start(out=dst.bitcast(I32), in_=words.rearrange("p n t -> p (n t)").bitcast(I32))

        def load_half_of_w_v(half):
            for g in range(H_GROUPS):
                load_codes(w_v_codes[:, half, g, :], W_v_words[g, :, columns(half), :])

        def load_vector(row, vec):
            nc.sync.dma_start(
                out=vec_rows[H_BLOCKS * row : H_BLOCKS * (row + 1), :], in_=vec.rearrange("(m c) -> m c", c=P)
            )

        load_tokens(liq_sb, liq_rows, 0, 1)
        load_scales(W_v_scales, PLANE_V)
        load_half_of_w_v(0)
        nc.sync.dma_start(out=b_v_cols[:], in_=b_v.rearrange("(g p t) -> p g t", g=H_GROUPS, t=PACK))
        load_tokens(liq_sb, liq_rows, 1, 1)
        load_half_of_w_v(1)
        load_vector(ROW_B_O, b_o)
        load_vector(ROW_TAU, tau)
        load_vector(ROW_G, g_att)
        load_vector(ROW_BETA, beta_att)
        load_vector(ROW_B_IN, b_in)
        load_tokens(liq_sb, liq_rows, 2, 2)
        load_scales(W_o_scales, PLANE_O)
        for g in range(H_GROUPS):
            load_codes(w_o_codes[:, g, :], W_o_words[g])
        load_tokens(liq_sb, liq_rows, 4, 2)
        load_tokens(liq_sb, liq_rows, 6, 2)
        load_scales(W_in_scales, PLANE_IN)
        load_codes(w_in_codes[:, 0, :], W_in_words[0])
        load_tokens(x_sb, x_rows, 0, 4)
        load_tokens(h_sb, h_rows, 0, 2)
        load_tokens(h_sb, h_rows, 2, 2)
        load_tokens(x_sb, x_rows, 4, 4)
        load_tokens(h_sb, h_rows, 4, 4)

        def turn(first, second, tag):
            turned = bank("scalar", (2, 2, P))
            for a, rows in enumerate((first, second)):
                words = rows.bitcast(F32)
                for u in range(2):
                    nc.tensor.transpose(turned[:, a, u, :], words[:, u : K_PASS // 2 : 2], ident_f32[:])
            grouped = ring.tile([P, 2, P, PACK], BF16, name=tag, tag=tag, bufs=3, align_bytes=64)
            nc.scalar.copy(out=grouped[:].bitcast(F32), in_=turned[:].rearrange("p a u r -> p a r u"))
            return grouped

        def quantise(grouped, codes, scales):
            nc.vector.quantize_mx(
                out=codes.bitcast(FP8X4), scales=scales, in_=grouped[:].rearrange("p a r t -> p (a r t)")
            )

        grouped_liq, grouped_x = {}, {}

        def turn_liq(i):
            grouped_liq[i] = turn(liq_sb[:, i, :K_PASS], liq_sb[:, i, K_PASS:], "grouped_liq")

        def quantise_liq(i):
            quantise(grouped_liq[i], liq_codes[:, i, :], liq_scales[:, i, :])

        def pair_tokens(pair):
            return slice(2 * pair * P, (2 * pair + 2) * P)

        def turn_x(pair):
            grouped_x[pair] = turn(x_sb[:, 2 * pair, :], x_sb[:, 2 * pair + 1, :], "grouped_x")

        def quantise_x(pair):
            quantise(grouped_x[pair], x_codes[:, pair_tokens(pair)], x_scales[:, pair_tokens(pair)])

        for _ in range(WARM_UP_MATMULS):
            unread_bank = bank("vector")
            nc.tensor.matmul(out=unread_bank[:, :P], lhsT=ident_bf[:], rhs=ident_bf[:], start=True, stop=True)
        turn_liq(0)
        turn_liq(1)

        for half in range(H_BANKS):
            rows = bank("scalar")
            for q in range(BANK // P):
                r = H_BLOCKS * ROW_B_O + half * (BANK // P) + q
                nc.tensor.matmul(
                    out=rows[:, q * P : (q + 1) * P],
                    lhsT=ident_bf[:, r : r + 1].to_broadcast([P, P]),
                    rhs=vec_rows[:],
                    start=True,
                    stop=True,
                )
            nc.scalar.copy(out=b_o_rows[:, columns(half)], in_=rows[:])

        vec_ps = bank("scalar", (P,), BF16)
        nc.tensor.transpose(vec_ps[:], vec_rows[:], ident_bf[:])
        vec_cols = keep.tile([P, VECTORS * H_BLOCKS], F32)
        nc.vector.tensor_copy(out=vec_cols[:], in_=vec_ps[:, : VECTORS * H_BLOCKS])

        def vector_cols(row):
            return vec_cols[:, H_BLOCKS * row : H_BLOCKS * (row + 1)]

        g_cols = vector_cols(ROW_G)
        shift_cols = keep.tile([P, H_BLOCKS], F32)
        rate_cols = keep.tile([P, H_BLOCKS], F32)
        h_factor_cols = keep.tile([P, H_BLOCKS], F32)
        nc.vector.tensor_tensor(
            out=shift_cols[:], in0=vector_cols(ROW_BETA), in1=vector_cols(ROW_B_IN), op=ALU.add
        )
        nc.vector.tensor_scalar_add(out=rate_cols[:], in0=vector_cols(ROW_TAU), scalar1=TAU_EPS)
        nc.vector.reciprocal(out=rate_cols[:], in_=rate_cols[:])
        nc.vector.tensor_scalar(
            out=h_factor_cols[:],
            in0=vector_cols(ROW_TAU),
            scalar1=-1.0,
            scalar2=TAU_EPS,
            op0=ALU.add,
            op1=ALU.add,
        )

        def spread_rate():
            for half in range(H_BANKS):
                rows = bank("scalar")
                for q in range(BANK // P):
                    m = half * (BANK // P) + q
                    nc.tensor.transpose(
                        rows[:, q * P : (q + 1) * P], rate_cols[:, m : m + 1].to_broadcast([P, P]), ident_f32[:]
                    )
                nc.scalar.copy(out=rate_rows[:, columns(half)], in_=rows[:])

        def sort_scales(half):
            nc.vector.tensor_copy(
                out=w_v_sorted_scales[:, half, :, :].rearrange("p g (t m) -> p g t m", t=PACK),
                in_=w_scales[:, PLANE_V : PLANE_V + H_GROUPS, columns(half)].rearrange("p g (m t) -> p g t m", t=PACK),
            )

        def sort_codes(half):
            nc.vector.tensor_copy(
                out=w_v_sorted[:, half, :, :].bitcast(I32).rearrange("p g (t m) -> p g t m", t=PACK),
                in_=w_v_codes[:, half, :, :].bitcast(I32).rearrange("p g (m t) -> p g t m", t=PACK),
            )

        grouped_v, cell, liq_b = {}, {}, {}
        resid, sums, out_tile = {}, {}, {}

        def project(pair, part):
            i, half = 2 * pair + part % 2, part // 2
            acc = bank("vector", (PACK, P))
            for t in range(PACK):
                features = slice(t * P, (t + 1) * P)
                for g in range(H_GROUPS):
                    group = slice(g * P, (g + 1) * P)
                    nc.tensor.matmul_mx(
                        out=acc[:, t, :],
                        lhsT=w_v_sorted[:, half, g, features].bitcast(FP8X4),
                        lhsT_scale=w_v_sorted_scales[:, half, g, features],
                        rhs=liq_codes[:, i, group].bitcast(FP8X4),
                        rhs_scale=liq_scales[:, i, group],
                        start=(g == 0),
                        stop=(g == H_GROUPS - 1),
                    )
            if i % 2 == 0:
                grouped_v[pair, half] = ring.tile(
                    [P, 2, P, PACK], BF16, name="grouped_v", tag="grouped_v", bufs=3, align_bytes=64
                )
            nc.vector.tensor_tensor(
                out=grouped_v[pair, half][:, i % 2, :, :],
                in0=acc[:].rearrange("p t n -> p n t"),
                in1=b_v_cols[:, half, :].unsqueeze(1).to_broadcast([P, P, PACK]),
                op=ALU.add,
            )
            if i % 2 == 1:
                tokens = pair_tokens(pair)
                quantise(grouped_v[pair, half], v_codes[:, half, tokens], v_scales[:, half, tokens])

        def add_b_o(pair):
            liq_b[pair] = ring.tile([P, 2, H], F32, name="liq_b", tag="liq_b", bufs=PAIRS)
            nc.vector.tensor_tensor(
                out=liq_b[pair][:],
                in0=liq_sb[:, 2 * pair : 2 * pair + 2, :],
                in1=b_o_rows[:].unsqueeze(1).to_broadcast([P, 2, H]),
                op=ALU.add,
            )

        def attend(pair, part):
            i, half = 2 * pair + part // H_BANKS, part % H_BANKS
            if half == 0:
                resid[i] = liq_b[pair][:, i % 2, :]
                sums[i] = stat.tile([P, H_BANKS], F32, name="sums", tag="sums")
            acc = bank("vector")
            tokens = slice(i * P, (i + 1) * P)
            for g in range(H_GROUPS):
                nc.tensor.matmul_mx(
                    out=acc[:],
                    lhsT=v_codes[:, g, tokens].bitcast(FP8X4),
                    lhsT_scale=v_scales[:, g, tokens],
                    rhs=w_o_codes[:, g, columns(half)].bitcast(FP8X4),
                    rhs_scale=w_scales[:, PLANE_O + g, columns(half)],
                    start=(g == 0),
                    stop=(g == H_GROUPS - 1),
                )
            nc.vector.scalar_tensor_tensor(
                out=resid[i][:, columns(half)],
                in0=acc[:],
                scalar=1.0,
                in1=resid[i][:, columns(half)],
                op0=ALU.mult,
                op1=ALU.add,
                accum_out=sums[i][:, half : half + 1],
            )

        def normalise(i):
            neg_mean = stat.tile([P, 1], F32, name="neg_mean", tag="neg_mean")
            nc.vector.tensor_scalar(
                out=neg_mean[:],
                in0=sums[i][:, 0:1],
                scalar1=sums[i][:, 1:2],
                scalar2=-1.0 / H,
                op0=ALU.add,
                op1=ALU.mult,
            )
            squares = ring.tile([P, H], BF16, name="squares", tag="squares")
            sum_sq = stat.tile([P, 1], F32, name="sum_sq", tag="sum_sq")
            nc.scalar.activation(
                out=squares[:], in_=resid[i], func=ACT.Square, bias=neg_mean[:], scale=1.0, accum_out=sum_sq[:]
            )
            var_eps = stat.tile([P, 1], F32, name="var_eps", tag="var_eps")
            nc.scalar.activation(out=var_eps[:], in_=sum_sq[:], func=ACT.Copy, bias=LN_EPS, scale=1.0 / H)
            rstd = stat.tile([P, 1], F32, name="rstd", tag="rstd")
            nc.gpsimd.tensor_tensor(out=rstd[:], in0=var_eps[:], in1=minus_half[:], op=ALU.pow)
            offset = stat.tile([P, 1], F32, name="offset", tag="offset")
            nc.scalar.activation(out=offset[:], in_=neg_mean[:], func=ACT.Copy, scale=rstd[:])
            nc.scalar.activation(out=resid[i], in_=resid[i], func=ACT.Identity, bias=offset[:], scale=rstd[:])

        def squash(pair, part):
            if part == 0:
                cell[pair] = ring.tile([P, H_BLOCKS, 2 * P], F32, name="cell", tag="cell", bufs=CELL_BUFS)
            normed = bank("scalar", (2, 2 * P))
            xin = bank("vector", (2, 2 * P))
            pair_of_blocks = (2 * part, 2 * part + 1)
            for b, m in enumerate(pair_of_blocks):
                for a in range(2):
                    nc.tensor.transpose(
                        normed[:, b, a * P : (a + 1) * P], resid[2 * pair + a][:, m * P : (m + 1) * P], ident_f32[:]
                    )
            for b, m in enumerate(pair_of_blocks):
                features = slice(m * P, (m + 1) * P)
                nc.tensor.matmul_mx(
                    out=xin[:, b, :],
                    lhsT=w_in_codes[:, 0, features].bitcast(FP8X4),
                    lhsT_scale=w_scales[:, PLANE_IN, features],
                    rhs=x_codes[:, pair_tokens(pair)].bitcast(FP8X4),
                    rhs_scale=x_scales[:, pair_tokens(pair)],
                    start=True,
                    stop=True,
                )
            for b, m in enumerate(pair_of_blocks):
                nc.scalar.activation(
                    out=cell[pair][:, m, :],
                    in_=normed[:, b, :],
                    func=ACT.Identity,
                    bias=shift_cols[:, m : m + 1],
                    scale=g_cols[:, m : m + 1],
                )
            blocks = cell[pair][:, 2 * part : 2 * part + 2, :]
            nc.vector.tensor_tensor(out=blocks, in0=xin[:], in1=blocks, op=ALU.add)
            nc.scalar.activation(out=blocks, in_=blocks, func=ACT.Tanh)

        def blend(pair, half):
            turned_h = bank("h", (4, 2 * P), BF16)
            for b in range(4):
                m = 4 * half + b
                for a in range(2):
                    nc.tensor.transpose(
                        turned_h[:, b, a * P : (a + 1) * P], h_sb[:, 2 * pair + a, m * P : (m + 1) * P], ident_bf[:]
                    )
            for b in range(4):
                m = 4 * half + b
                nc.vector.scalar_tensor_tensor(
                    out=cell[pair][:, m, :],
                    in0=turned_h[:, b, :],
                    scalar=h_factor_cols[:, m : m + 1],
                    in1=cell[pair][:, m, :],
                    op0=ALU.mult,
                    op1=ALU.add,
                )

        def finish(pair, part):
            half, a = part // 2, part % 2
            i = 2 * pair + a
            if half == 0:
                out_tile[i] = ring.tile([P, H], F32, name="out_tile", tag="out_tile", bufs=OUT_BUFS)
            acc = bank("vector")
            for b in range(4):
                nc.tensor.transpose(
                    acc[:, b * P : (b + 1) * P], cell[pair][:, 4 * half + b, a * P : (a + 1) * P], ident_f32[:]
                )
            cols = columns(half)
            nc.vector.tensor_tensor(out=out_tile[i][:, cols], in0=acc[:], in1=rate_rows[:, cols], op=ALU.mult)
            nc.sync.dma_start(out=out_rows[:, i, cols], in_=out_tile[i][:, cols])

        with tc.manual_schedule(engines={mybir.EngineType.DVE}):
            sort_scales(0)
            sort_codes(0)
            quantise_liq(0)
            sort_scales(1)
            quantise_liq(1)
            sort_codes(1)

        def due(first, parts=4, every=1):
            return [
                (k, n) for k in range(PAIRS) for n in range(parts) if max(first + 4 * k + every * n, 0) == slot
            ]

        for slot in range(END_FIRST + 4 * PAIRS):
            for k, n in due(0):
                project(k, n)
            for k, _ in due(2, 1):
                add_b_o(k)
            for k, n in due(ATT_FIRST):
                attend(k, n)
            for a, first in enumerate(NORMALISE_FIRST):
                for k, _ in due(first, 1):
                    normalise(2 * k + a)
            if slot == 4:
                spread_rate()
            for k, n in due(SQUASH_FIRST):
                squash(k, n)
            for k, n in due(SQUASH_FIRST + 1, 2, 2):
                blend(k, n)
            for k, n in due(END_FIRST):
                finish(k, n)
            for k, n in due(-4, 2):
                if k > 0:
                    turn_liq(2 * k + n)
                    quantise_liq(2 * k + n)
            for k, _ in due(5, 1):
                turn_x(k)
                quantise_x(k)
